import numpy as np
import ml_dtypes


def mxq(x, axis, fmt="e4m3"):
    dtype, down = {"e4m3": (ml_dtypes.float8_e4m3fn, 7), "e5m2": (ml_dtypes.float8_e5m2, 14)}[fmt]
    v = np.moveaxis(np.asarray(x, np.float32).astype(ml_dtypes.bfloat16).astype(np.float64), axis, -1)
    blocks = v.reshape(v.shape[:-1] + (-1, 32))
    amax = np.abs(blocks).max(-1, keepdims=True)
    byte = np.maximum(np.where(amax > 0, np.frexp(amax)[1] - 1 + 127, 0) - down, 1)
    scale = np.exp2(byte - 127.0)
    codes = (blocks / scale).astype(np.float32).astype(dtype).astype(np.float64)
    return np.moveaxis((codes * scale).reshape(v.shape), -1, axis)


WIDE = False


def mx_kscale(k):
    if not WIDE:
        return np.ones(k)
    levels = np.array([10, -10, 5, -5, 0])
    a = np.random.permutation(np.resize(levels, k // 512 * 4)).reshape(k // 512, 4)
    idx = np.arange(k)
    return np.exp2(a[idx // 512, idx % 128 // 32])


BF16 = ml_dtypes.bfloat16


def bf(x):
    return np.asarray(x, np.float32).astype(BF16)


def f64(x):
    return np.asarray(x).astype(np.float64)


E2M1 = np.array([0.0, 0.5, 1.0, 1.5, 2.0, 3.0, 4.0, 6.0, -0.0, -0.5, -1.0, -1.5, -2.0, -3.0, -4.0, -6.0])


def pack_weight(w, fmt):
    k, n = w.shape
    w = f64(bf(w)).reshape(k // 32, 32, n)
    amax = np.abs(w).max(1)
    if fmt == "e4m3":
        byte = np.frexp(amax)[1] - 1 + 127 - 7
    else:
        mant, ex = np.frexp(amax / 6.0)
        byte = np.where(mant > 0.5, ex, ex - 1) + 127
    byte = np.clip(np.where(amax > 0, byte, 1), 1, 254)
    scaled = (w * np.exp2(127.0 - byte)[:, None, :]).reshape(k, n).astype(np.float32)
    by_word = np.ascontiguousarray(scaled.reshape(k // 512, 128, 4, n).transpose(0, 1, 3, 2))
    if fmt == "e4m3":
        words = by_word.astype(ml_dtypes.float8_e4m3fn).view(np.uint8)
    else:
        c = by_word.astype(ml_dtypes.float4_e2m1fn).view(np.uint8) & 0xF
        words = c[..., 0::2] | (c[..., 1::2] << 4)
    return np.ascontiguousarray(words), np.ascontiguousarray(byte.astype(np.uint8).reshape(k // 512, 16, n))


def unpack_weight(words, scales, fmt):
    g, p, n, _ = words.shape
    if fmt == "e4m3":
        vals = np.ascontiguousarray(words).view(ml_dtypes.float8_e4m3fn).astype(np.float64)
    else:
        nib = np.empty((g, p, n, 4), np.uint8)
        nib[..., 0::2] = words & 0xF
        nib[..., 1::2] = words >> 4
        vals = E2M1[nib]
    vals = vals * np.repeat(np.exp2(scales.astype(np.float64) - 127.0), 8, axis=1)[..., None]
    return vals.transpose(0, 1, 3, 2).reshape(g * 512, n)


B, N, C = 64, 12, 512
BN_EPS = 1e-5
FMT = "e4m3"


def bn(v):
    mean = v.mean(axis=(0, 2), keepdims=True)
    var = v.var(axis=(0, 2), keepdims=True)
    return (v - mean) / np.sqrt(var + BN_EPS)


def sigmoid(v):
    return 1.0 / (1.0 + np.exp(-v))


def softmax(v, axis):
    p = np.exp(v - v.max(axis=axis, keepdims=True))
    return p / p.sum(axis=axis, keepdims=True)


def draw_w(a, f):
    w = np.random.standard_normal((C, C)) * a / np.sqrt(C) / f[None, :]
    return pack_weight(np.ascontiguousarray(w.T), FMT)


def setup_inputs():
    s, t = mx_kscale(C), mx_kscale(C)
    s, t = s / s.max(), t / t.max()
    x = bf(np.random.standard_normal((B, N, C)) * s)
    edge = bf(np.random.standard_normal((B, N * N, C)) * t)
    WA_words, WA_scales = draw_w(np.sqrt(2.0), s)
    WB_words, WB_scales = draw_w(np.sqrt(2.0), s)
    WE_words, WE_scales = draw_w(np.sqrt(2.0), t)
    WU_words, WU_scales = draw_w(0.4, s)
    WV_words, WV_scales = draw_w(0.5 * N, s)
    return {"x": x,
            "edge": edge,
            "WA_words": WA_words, "WA_scales": WA_scales,
            "WB_words": WB_words, "WB_scales": WB_scales,
            "WE_words": WE_words, "WE_scales": WE_scales,
            "WU_words": WU_words, "WU_scales": WU_scales,
            "WV_words": WV_words, "WV_scales": WV_scales}


def reference(x, edge, WA_words, WA_scales, WB_words, WB_scales, WE_words, WE_scales, WU_words, WU_scales, WV_words, WV_scales):
    x, edge = f64(x), f64(edge)
    xq = mxq(x, 2, "e4m3")
    Vix = xq @ unpack_weight(WA_words, WA_scales, FMT)
    Vjx = xq @ unpack_weight(WB_words, WB_scales, FMT)
    e_proj = mxq(edge, 2, "e4m3") @ unpack_weight(WE_words, WE_scales, FMT)
    agg = np.repeat(Vix, N, axis=1) + np.tile(Vjx, (1, N, 1)) + e_proj
    edge_out = edge + np.maximum(bn(agg), 0.0)
    e = sigmoid(edge_out).reshape(B, N, N, C)
    e = softmax(e, 2).reshape(B, N * N, C)
    Ujx = np.tile(xq @ unpack_weight(WV_words, WV_scales, FMT), (1, N, 1))
    Uix = xq @ unpack_weight(WU_words, WU_scales, FMT)
    msg = (e * Ujx).reshape(B, N, N, C).sum(axis=2)
    x_new = Uix + msg / N
    x_out = np.maximum(x + bn(x_new), 0.0)
    return x_out, edge_out

@@ -1,0 +1,267 @@
+from contextlib import ExitStack
+
+import concourse.mybir as mybir
+from concourse.masks import make_identity
+
+F32 = mybir.dt.float32
+BF16 = mybir.dt.bfloat16
+U8 = mybir.dt.uint8
+U32 = mybir.dt.uint32
+I32 = mybir.dt.int32
+FP8X4 = mybir.dt.float8_e4m3fn_x4
+ALU = mybir.AluOpType
+ACT = mybir.ActivationFunctionType
+AXIS = mybir.AxisListType
+
+GRAPHS, NODES, C = 64, 12, 512
+P = 128
+PACK = 4
+SLOTS = NODES // 2
+ROUND = 4
+ROUNDS_PER_SLOT = NODES // ROUND
+PAIRS = NODES // 2
+BN_EPS = 1e-5
+WEIGHT_NAMES = ("A", "B", "E", "U", "V")
+
+FLOPS = 2 * C * C * (GRAPHS * NODES * NODES + 4 * GRAPHS * NODES)
+
+
+def tile_graphmodel_pa_kernel(
+    tc, x, edge,
+    WA_words, WA_scales, WB_words, WB_scales, WE_words, WE_scales, WU_words, WU_scales, WV_words, WV_scales,
+    x_out, edge_out,
+):
+    nc = tc.nc
+    given = {
+        "A": (WA_words, WA_scales), "B": (WB_words, WB_scales), "E": (WE_words, WE_scales),
+        "U": (WU_words, WU_scales), "V": (WV_words, WV_scales),
+    }
+    x_rows = x.rearrange("b (h s) c -> (b h) s c", h=2)
+    x_out_rows = x_out.rearrange("b (h s) c -> (b h) s c", h=2)
+    edge_rows = edge.rearrange("b (h r) c -> (b h) r c", h=2)
+    edge_out_rows = edge_out.rearrange("b (h r) c -> (b h) r c", h=2)
+
+    with ExitStack() as ctx:
+        keep = ctx.enter_context(tc.tile_pool(name="keep", bufs=1))
+        edges = ctx.enter_context(tc.tile_pool(name="edges", bufs=3))
+        stage = ctx.enter_context(tc.tile_pool(name="stage", bufs=2))
+        normed = ctx.enter_context(tc.tile_pool(name="normed", bufs=3))
+        gates = ctx.enter_context(tc.tile_pool(name="gates", bufs=2))
+        gated = ctx.enter_context(tc.tile_pool(name="gated", bufs=1))
+        nodes = ctx.enter_context(tc.tile_pool(name="nodes", bufs=2))
+        small = ctx.enter_context(tc.tile_pool(name="small", bufs=4))
+        psum_flip = ctx.enter_context(tc.psum_pool(name="psum_flip", bufs=1))
+        psum_acc = ctx.enter_context(tc.psum_pool(name="psum_acc", bufs=6))
+        psum_sums = ctx.enter_context(tc.psum_pool(name="psum_sums", bufs=1))
+
+        x_own = keep.tile([P, SLOTS, C], BF16)
+        nc.scalar.dma_start(out=x_own[:], in_=x_rows)
+        x_all = edges.tile([P, NODES, C], BF16, tag="edge_in")
+        for h in range(2):
+            nc.scalar.dma_start(out=x_all[h:P:2, :, :], in_=x)
+
+        w_words = keep.tile([P, len(WEIGHT_NAMES), C], U32, align_bytes=64)
+        w_planes = keep.tile([P, len(WEIGHT_NAMES), C], U8, align_bytes=64)
+        nc.vector.memset(w_planes[:].bitcast(I32), 0)
+        for w in ("E", "A", "B", "V", "U"):
+            words, scales = given[w]
+            k = WEIGHT_NAMES.index(w)
+            for quadrant in range(4):
+                nc.sync.dma_start(
+                    out=w_planes[32 * quadrant : 32 * quadrant + 4, k, :].bitcast(I32),
+                    in_=scales[0, 4 * quadrant : 4 * quadrant + 4, :].bitcast(I32),
+                )
+            nc.sync.dma_start(
+                out=w_words[:, k, :].bitcast(I32),
+                in_=words[0].rearrange("p n t -> p (n t)").bitcast(I32),
+            )
+
+        ident = keep.tile([P, P], F32)
+        make_identity(nc, ident[:])
+        own_parity = keep.tile([P, 2], F32)
+        nc.vector.tensor_reduce(
+            out=own_parity[:], in_=ident[:].rearrange("p (a t) -> p t a", t=2), axis=AXIS.X, op=ALU.add
+        )
+        parity = keep.tile([P, P // 2, 2], F32)
+        nc.vector.tensor_scalar(
+            out=parity[:], in0=own_parity[:].unsqueeze(1).to_broadcast([P, P // 2, 2]),
+            scalar1=-1.0 / P, scalar2=None, op0=ALU.mult,
+        )
+        minus_eps = keep.tile([P, ROUND, 2], F32)
+        nc.vector.memset(minus_eps[:, :, 0], -BN_EPS)
+        nc.vector.memset(minus_eps[:, :, 1], 0.0)
+        minus_half = keep.tile([P, ROUND], F32)
+        nc.vector.memset(minus_half[:], -0.5)
+
+        def quantise_rows(rows, count, codes, planes):
+            grouped = stage.tile([P, count, P, PACK], BF16, align_bytes=64, tag="grouped")
+            for first in range(0, count, 2):
+                flipped = psum_flip.tile([P, 2, 2, P], F32)
+                for i in range(2):
+                    words = rows[:, first + i, :].bitcast(F32)
+                    for u in range(2):
+                        nc.tensor.transpose(flipped[:, i, u, :], words[:, u : C // 2 : 2], ident[:])
+                nc.scalar.copy(
+                    out=grouped[:, first : first + 2, :, :].bitcast(F32),
+                    in_=flipped[:].rearrange("q i u r -> q i r u"),
+                )
+            nc.vector.quantize_mx(
+                out=codes.bitcast(FP8X4), scales=planes, in_=grouped[:].rearrange("q i r t -> q (i r t)")
+            )
+
+        def multiply(out, codes, planes, index, w, start, stop, cols=slice(0, C)):
+            k = WEIGHT_NAMES.index(w)
+            nc.tensor.matmul_mx(
+                out=out,
+                lhsT=codes[:, index * P : (index + 1) * P].bitcast(FP8X4),
+                lhsT_scale=planes[:, index * P : (index + 1) * P],
+                rhs=w_words[:, k, cols].bitcast(FP8X4),
+                rhs_scale=w_planes[:, k, cols],
+                start=start,
+                stop=stop,
+            )
+
+        def norm_factors(stats, count):
+            mean_sq = small.tile([P, count, 2], F32, tag="mean_sq")
+            nc.vector.tensor_tensor(out=mean_sq[:], in0=stats[:, :, :, 1], in1=stats[:, :, :, 1], op=ALU.mult)
+            nc.vector.scalar_tensor_tensor(
+                out=stats[:, :, :, 0], in0=stats[:, :, :, 2], scalar=2.0 / C, in1=mean_sq[:],
+                op0=ALU.mult, op1=ALU.add,
+            )
+            sums = psum_sums.tile([P, count, 2], F32, tag="sums")
+            for half in range(2):
+                nc.tensor.matmul(
+                    out=sums[:], lhsT=parity[:].rearrange("p a t -> p (a t)"), rhs=stats[:, :, half, 0:2],
+                    start=(half == 0), stop=(half == 1),
+                )
+            minus = small.tile([P, count, 2], F32, tag="minus")
+            nc.vector.tensor_tensor(out=minus[:], in0=sums[:], in1=minus_eps[:, :count, :], op=ALU.add)
+            square = small.tile([P, count], F32, tag="square")
+            nc.vector.tensor_tensor(out=square[:], in0=minus[:, :, 1], in1=minus[:, :, 1], op=ALU.mult)
+            var_eps = small.tile([P, count], F32, tag="var_eps")
+            nc.vector.scalar_tensor_tensor(
+                out=var_eps[:], in0=minus[:, :, 0], scalar=-1.0, in1=square[:], op0=ALU.mult, op1=ALU.subtract
+            )
+            rstd = small.tile([P, count], F32, tag="rstd")
+            nc.gpsimd.tensor_tensor(out=rstd[:], in0=var_eps[:], in1=minus_half[:, :count], op=ALU.pow)
+            shift = small.tile([P, count], F32, tag="shift")
+            nc.vector.tensor_tensor(out=shift[:], in0=minus[:, :, 1], in1=rstd[:], op=ALU.mult)
+            return rstd, shift
+
+        all_codes = keep.tile([P, NODES * P], U32, align_bytes=64)
+        all_planes = keep.tile([P, NODES * P], U8, align_bytes=64)
+        own_codes = keep.tile([P, SLOTS * P], U32, align_bytes=64)
+        own_planes = keep.tile([P, SLOTS * P], U8, align_bytes=64)
+        for first, count in ((0, 4), (4, 2)):
+            cols = slice(first * P, (first + count) * P)
+            quantise_rows(x_own[:, first : first + count, :], count, own_codes[:, cols], own_planes[:, cols])
+        for first in range(0, NODES, ROUND):
+            cols = slice(first * P, (first + ROUND) * P)
+            quantise_rows(x_all[:, first : first + ROUND, :], ROUND, all_codes[:, cols], all_planes[:, cols])
+
+        edge_in = {}
+        gate = {}
+        weighted = {}
+        message_source = keep.tile([P, PAIRS, C, 2], F32)
+
+        def load_edges(s):
+            edge_in[s] = edges.tile([P, NODES, C], BF16, name="edge_in%d" % s, tag="edge_in")
+            nc.sync.dma_start(out=edge_in[s][:], in_=edge_rows[:, s * NODES : (s + 1) * NODES, :])
+
+        def message_sources():
+            half = C // 2
+            for a in range(PAIRS):
+                for first in range(0, C, half):
+                    both = psum_acc.tile([P, 2, half], F32, tag="acc")
+                    for t in range(2):
+                        multiply(both[:, t, :], all_codes, all_planes, 2 * a + t, "V", True, True,
+                                 cols=slice(first, first + half))
+                    nc.scalar.mul(
+                        out=message_source[:, a, first : first + half, :],
+                        in_=both[:].rearrange("p t c -> p c t"),
+                        mul=1.0 / NODES,
+                    )
+
+        def edge_round(s, j0):
+            codes = stage.tile([P, ROUND * P], U32, align_bytes=64, tag="codes")
+            planes = stage.tile([P, ROUND * P], U8, align_bytes=64, tag="planes")
+            quantise_rows(edge_in[s][:, j0 : j0 + ROUND, :], ROUND, codes[:], planes[:])
+            stats = small.tile([P, ROUND, 2, 3], F32, tag="stats")
+            acc = []
+            for i in range(ROUND):
+                agg = psum_acc.tile([P, C], F32, name="agg%d" % i, tag="acc")
+                multiply(agg[:], own_codes, own_planes, s, "A", True, False)
+                multiply(agg[:], all_codes, all_planes, j0 + i, "B", False, False)
+                multiply(agg[:], codes, planes, i, "E", False, True)
+                nc.vector.bn_stats(out=stats[:, i, :, :].rearrange("p h k -> p (h k)"), in_=agg[:])
+                acc.append(agg)
+            rstd, shift = norm_factors(stats, ROUND)
+            result = normed.tile([P, ROUND, C], F32, tag="result")
+            for i in range(ROUND):
+                nc.scalar.activation(
+                    out=result[:, i, :], in_=acc[i][:], func=ACT.Relu,
+                    bias=shift[:, i : i + 1], scale=rstd[:, i : i + 1],
+                )
+            for i in range(0, ROUND, 2):
+                nc.gpsimd.tensor_tensor(
+                    out=result[:, i : i + 2, :], in0=result[:, i : i + 2, :],
+                    in1=edge_in[s][:, j0 + i : j0 + i + 2, :], op=ALU.add,
+                )
+            r0 = s * NODES + j0
+            nc.sync.dma_start(out=edge_out_rows[:, r0 : r0 + ROUND, :], in_=result[:])
+            return result
+
+        def gate_round(s, j0, result):
+            pairs = slice(j0 // 2, (j0 + ROUND) // 2)
+            nc.scalar.activation(
+                out=gate[s][:, pairs, :, :], in_=result[:].rearrange("p (a t) c -> p a c t", t=2),
+                func=ACT.Tanh, scale=0.5,
+            )
+            nc.scalar.activation(out=gate[s][:, pairs, :, :], in_=gate[s][:, pairs, :, :], func=ACT.Exp, scale=0.5)
+            nc.gpsimd.tensor_tensor(
+                out=weighted[s][:, pairs, :, :], in0=gate[s][:, pairs, :, :], in1=message_source[:, pairs, :, :],
+                op=ALU.mult,
+            )
+
+        def node_update(s):
+            total = nodes.tile([P, C], F32, tag="total")
+            message = nodes.tile([P, C], F32, tag="message")
+            quarter = C // 4
+            for first in range(0, C, quarter):
+                cols = slice(first, first + quarter)
+                nc.vector.tensor_reduce(
+                    out=total[:, cols], in_=gate[s][:, :, cols, :].rearrange("p a c t -> p c a t"),
+                    axis=AXIS.XY, op=ALU.add,
+                )
+                nc.vector.tensor_reduce(
+                    out=message[:, cols], in_=weighted[s][:, :, cols, :].rearrange("p a c t -> p c a t"),
+                    axis=AXIS.XY, op=ALU.add,
+                )
+            nc.vector.reciprocal(out=total[:], in_=total[:])
+            nc.vector.tensor_tensor(out=message[:], in0=message[:], in1=total[:], op=ALU.mult)
+            own = psum_acc.tile([P, C], F32, tag="acc")
+            multiply(own[:], own_codes, own_planes, s, "U", True, True)
+            x_new = nodes.tile([P, C], F32, tag="x_new")
+            nc.vector.tensor_tensor(out=x_new[:], in0=message[:], in1=own[:], op=ALU.add)
+            stats = small.tile([P, 1, 2, 3], F32, tag="node_stats")
+            nc.vector.bn_stats(out=stats[:, 0, :, :].rearrange("p h k -> p (h k)"), in_=x_new[:])
+            rstd, shift = norm_factors(stats, 1)
+            nc.vector.scalar_tensor_tensor(
+                out=x_new[:], in0=x_new[:], scalar=rstd[:, 0:1], in1=x_own[:, s, :], op0=ALU.mult, op1=ALU.add
+            )
+            nc.scalar.activation(out=x_new[:], in_=x_new[:], func=ACT.Relu, bias=shift[:, 0:1], scale=1.0)
+            nc.sync.dma_start(out=x_out_rows[:, s, :], in_=x_new[:])
+
+        load_edges(0)
+        load_edges(1)
+        for s in range(SLOTS):
+            if s + 2 < SLOTS:
+                load_edges(s + 2)
+            gate[s] = gates.tile([P, PAIRS, C, 2], F32, name="gate%d" % s, tag="gate")
+            weighted[s] = gated.tile([P, PAIRS, C, 2], F32, name="weighted%d" % s, tag="weighted")
+            for j0 in range(0, NODES, ROUND):
+                result = edge_round(s, j0)
+                if s == 0 and j0 == 0:
+                    message_sources()
+                gate_round(s, j0, result)
+            node_update(s)

@@ -17,9 +17,9 @@ GRAPHS, NODES, C = 64, 12, 512
 P = 128
 PACK = 4
 SLOTS = NODES // 2
-ROUND = 4
-ROUNDS_PER_SLOT = NODES // ROUND
-PAIRS = NODES // 2
+ROUND = 6
+PAIRS = ROUND // 2
+ROUNDS = SLOTS * NODES // ROUND
 BN_EPS = 1e-5
 WEIGHT_NAMES = ("A", "B", "E", "U", "V")
 
@@ -45,39 +45,56 @@ def tile_graphmodel_pa_kernel(
         keep = ctx.enter_context(tc.tile_pool(name="keep", bufs=1))
         edges = ctx.enter_context(tc.tile_pool(name="edges", bufs=3))
         stage = ctx.enter_context(tc.tile_pool(name="stage", bufs=2))
-        normed = ctx.enter_context(tc.tile_pool(name="normed", bufs=3))
+        normed = ctx.enter_context(tc.tile_pool(name="normed", bufs=2))
         gates = ctx.enter_context(tc.tile_pool(name="gates", bufs=2))
-        gated = ctx.enter_context(tc.tile_pool(name="gated", bufs=1))
+        gated = ctx.enter_context(tc.tile_pool(name="gated", bufs=2))
+        sums = ctx.enter_context(tc.tile_pool(name="sums", bufs=4))
         nodes = ctx.enter_context(tc.tile_pool(name="nodes", bufs=2))
-        small = ctx.enter_context(tc.tile_pool(name="small", bufs=4))
+        small = ctx.enter_context(tc.tile_pool(name="small", bufs=3))
         psum_flip = ctx.enter_context(tc.psum_pool(name="psum_flip", bufs=1))
-        psum_acc = ctx.enter_context(tc.psum_pool(name="psum_acc", bufs=6))
-        psum_sums = ctx.enter_context(tc.psum_pool(name="psum_sums", bufs=1))
+        psum_acc = ctx.enter_context(tc.psum_pool(name="psum_acc", bufs=ROUND))
+        psum_mean = ctx.enter_context(tc.psum_pool(name="psum_mean", bufs=1))
+        ctx.enter_context(tc.manual_schedule())
+
+        ident = keep.tile([P, P], F32)
+        make_identity(nc, ident[:])
 
         x_own = keep.tile([P, SLOTS, C], BF16)
-        nc.scalar.dma_start(out=x_own[:], in_=x_rows)
         x_all = edges.tile([P, NODES, C], BF16, tag="edge_in")
-        for h in range(2):
-            nc.scalar.dma_start(out=x_all[h:P:2, :, :], in_=x)
+        nc.scalar.dma_start(out=x_all[0:P:2, :, :], in_=x)
+        nc.sync.dma_start(out=x_all[1:P:2, :, :], in_=x)
+        nc.scalar.dma_start(out=x_own[:], in_=x_rows)
+
+        edge_in = {}
+
+        def load_edges(s):
+            edge_in[s] = edges.tile([P, NODES, C], BF16, name="edge_in%d" % s, tag="edge_in")
+            nc.sync.dma_start(out=edge_in[s][:], in_=edge_rows[:, s * NODES : (s + 1) * NODES, :])
 
         w_words = keep.tile([P, len(WEIGHT_NAMES), C], U32, align_bytes=64)
         w_planes = keep.tile([P, len(WEIGHT_NAMES), C], U8, align_bytes=64)
         nc.vector.memset(w_planes[:].bitcast(I32), 0)
-        for w in ("E", "A", "B", "V", "U"):
+
+        def load_weight(w):
             words, scales = given[w]
             k = WEIGHT_NAMES.index(w)
             for quadrant in range(4):
-                nc.sync.dma_start(
-                    out=w_planes[32 * quadrant : 32 * quadrant + 4, k, :].bitcast(I32),
-                    in_=scales[0, 4 * quadrant : 4 * quadrant + 4, :].bitcast(I32),
-                )
+                plane_rows = w_planes[32 * quadrant : 32 * quadrant + 4, k, :]
+                scale_rows = scales[0, 4 * quadrant : 4 * quadrant + 4, :]
+                if quadrant % 2 == 0:
+                    nc.sync.dma_start(out=plane_rows.bitcast(I32), in_=scale_rows.bitcast(I32))
+                else:
+                    nc.gpsimd.dma_start(out=plane_rows.bitcast(F32), in_=scale_rows.bitcast(F32))
             nc.sync.dma_start(
                 out=w_words[:, k, :].bitcast(I32),
                 in_=words[0].rearrange("p n t -> p (n t)").bitcast(I32),
             )
 
-        ident = keep.tile([P, P], F32)
-        make_identity(nc, ident[:])
+        load_edges(0)
+        for w in ("V", "U", "A", "B", "E"):
+            load_weight(w)
+        load_edges(1)
+
         own_parity = keep.tile([P, 2], F32)
         nc.vector.tensor_reduce(
             out=own_parity[:], in_=ident[:].rearrange("p (a t) -> p t a", t=2), axis=AXIS.X, op=ALU.add
@@ -85,28 +102,30 @@ def tile_graphmodel_pa_kernel(
         parity = keep.tile([P, P // 2, 2], F32)
         nc.vector.tensor_scalar(
             out=parity[:], in0=own_parity[:].unsqueeze(1).to_broadcast([P, P // 2, 2]),
-            scalar1=-1.0 / P, scalar2=None, op0=ALU.mult,
+            scalar1=1.0 / P, scalar2=None, op0=ALU.mult,
         )
-        minus_eps = keep.tile([P, ROUND, 2], F32)
-        nc.vector.memset(minus_eps[:, :, 0], -BN_EPS)
-        nc.vector.memset(minus_eps[:, :, 1], 0.0)
-        minus_half = keep.tile([P, ROUND], F32)
+        minus_half = keep.tile([P, ROUND + 1], F32)
         nc.vector.memset(minus_half[:], -0.5)
 
-        def quantise_rows(rows, count, codes, planes):
-            grouped = stage.tile([P, count, P, PACK], BF16, align_bytes=64, tag="grouped")
-            for first in range(0, count, 2):
-                flipped = psum_flip.tile([P, 2, 2, P], F32)
-                for i in range(2):
-                    words = rows[:, first + i, :].bitcast(F32)
-                    for u in range(2):
-                        nc.tensor.transpose(flipped[:, i, u, :], words[:, u : C // 2 : 2], ident[:])
-                nc.scalar.copy(
-                    out=grouped[:, first : first + 2, :, :].bitcast(F32),
-                    in_=flipped[:].rearrange("q i u r -> q i r u"),
-                )
+        def transpose_pair(rows, first, pool=psum_flip, tag="flipped"):
+            flipped = pool.tile([P, 2, 2, P], F32, tag=tag)
+            for i in range(2):
+                words = rows[:, first + i, :].bitcast(F32)
+                for u in range(2):
+                    nc.tensor.transpose(flipped[:, i, u, :], words[:, u : C // 2 : 2], ident[:])
+            return flipped
+
+        def regroup_pair(flipped, grouped, first, engine_copy=nc.scalar.copy):
+            engine_copy(
+                out=grouped[:, first : first + 2, :, :].bitcast(F32),
+                in_=flipped[:].rearrange("q i u r -> q i r u"),
+            )
+
+        def quantise(grouped, codes, planes, first, count):
+            cols = slice(first * P, (first + count) * P)
             nc.vector.quantize_mx(
-                out=codes.bitcast(FP8X4), scales=planes, in_=grouped[:].rearrange("q i r t -> q (i r t)")
+                out=codes[:, cols].bitcast(FP8X4), scales=planes[:, cols],
+                in_=grouped[:, first : first + count, :, :].rearrange("q i r t -> q (i r t)"),
             )
 
         def multiply(out, codes, planes, index, w, start, stop, cols=slice(0, C)):
@@ -121,147 +140,278 @@ def tile_graphmodel_pa_kernel(
                 stop=stop,
             )
 
-        def norm_factors(stats, count):
-            mean_sq = small.tile([P, count, 2], F32, tag="mean_sq")
-            nc.vector.tensor_tensor(out=mean_sq[:], in0=stats[:, :, :, 1], in1=stats[:, :, :, 1], op=ALU.mult)
-            nc.vector.scalar_tensor_tensor(
-                out=stats[:, :, :, 0], in0=stats[:, :, :, 2], scalar=2.0 / C, in1=mean_sq[:],
-                op0=ALU.mult, op1=ALU.add,
-            )
-            sums = psum_sums.tile([P, count, 2], F32, tag="sums")
-            for half in range(2):
-                nc.tensor.matmul(
-                    out=sums[:], lhsT=parity[:].rearrange("p a t -> p (a t)"), rhs=stats[:, :, half, 0:2],
-                    start=(half == 0), stop=(half == 1),
-                )
-            minus = small.tile([P, count, 2], F32, tag="minus")
-            nc.vector.tensor_tensor(out=minus[:], in0=sums[:], in1=minus_eps[:, :count, :], op=ALU.add)
-            square = small.tile([P, count], F32, tag="square")
-            nc.vector.tensor_tensor(out=square[:], in0=minus[:, :, 1], in1=minus[:, :, 1], op=ALU.mult)
-            var_eps = small.tile([P, count], F32, tag="var_eps")
-            nc.vector.scalar_tensor_tensor(
-                out=var_eps[:], in0=minus[:, :, 0], scalar=-1.0, in1=square[:], op0=ALU.mult, op1=ALU.subtract
-            )
-            rstd = small.tile([P, count], F32, tag="rstd")
-            nc.gpsimd.tensor_tensor(out=rstd[:], in0=var_eps[:], in1=minus_half[:, :count], op=ALU.pow)
-            shift = small.tile([P, count], F32, tag="shift")
-            nc.vector.tensor_tensor(out=shift[:], in0=minus[:, :, 1], in1=rstd[:], op=ALU.mult)
-            return rstd, shift
-
         all_codes = keep.tile([P, NODES * P], U32, align_bytes=64)
         all_planes = keep.tile([P, NODES * P], U8, align_bytes=64)
         own_codes = keep.tile([P, SLOTS * P], U32, align_bytes=64)
         own_planes = keep.tile([P, SLOTS * P], U8, align_bytes=64)
-        for first, count in ((0, 4), (4, 2)):
-            cols = slice(first * P, (first + count) * P)
-            quantise_rows(x_own[:, first : first + count, :], count, own_codes[:, cols], own_planes[:, cols])
-        for first in range(0, NODES, ROUND):
-            cols = slice(first * P, (first + ROUND) * P)
-            quantise_rows(x_all[:, first : first + ROUND, :], ROUND, all_codes[:, cols], all_planes[:, cols])
+        for rows, codes, planes, base in (
+            (x_all, all_codes, all_planes, 0), (x_own, own_codes, own_planes, 0), (x_all, all_codes, all_planes, ROUND),
+        ):
+            grouped = stage.tile([P, ROUND, P, PACK], BF16, align_bytes=64, tag="grouped")
+            for first in range(0, ROUND, 2):
+                flipped = transpose_pair(rows[:, base : base + ROUND, :], first, pool=psum_acc, tag="acc")
+                regroup_pair(flipped, grouped, first, engine_copy=nc.vector.tensor_copy if first == 2 else nc.scalar.copy)
+            part = slice(base * P, (base + ROUND) * P)
+            quantise(grouped, codes[:, part], planes[:, part], 0, 4)
+            quantise(grouped, codes[:, part], planes[:, part], 4, 2)
 
-        edge_in = {}
-        gate = {}
-        weighted = {}
-        message_source = keep.tile([P, PAIRS, C, 2], F32)
+        message_source = keep.tile([P, NODES // 2, C, 2], F32)
 
-        def load_edges(s):
-            edge_in[s] = edges.tile([P, NODES, C], BF16, name="edge_in%d" % s, tag="edge_in")
-            nc.sync.dma_start(out=edge_in[s][:], in_=edge_rows[:, s * NODES : (s + 1) * NODES, :])
-
-        def message_sources():
-            half = C // 2
-            for a in range(PAIRS):
-                for first in range(0, C, half):
-                    both = psum_acc.tile([P, 2, half], F32, tag="acc")
-                    for t in range(2):
-                        multiply(both[:, t, :], all_codes, all_planes, 2 * a + t, "V", True, True,
-                                 cols=slice(first, first + half))
+        half = C // 2
+        for a in range(NODES // 2):
+            for first in range(0, C, half):
+                both = psum_acc.tile([P, 2, half], F32, tag="acc")
+                for t in range(2):
+                    multiply(both[:, t, :], all_codes, all_planes, 2 * a + t, "V", True, True,
+                             cols=slice(first, first + half))
+                if first == 0:
                     nc.scalar.mul(
-                        out=message_source[:, a, first : first + half, :],
-                        in_=both[:].rearrange("p t c -> p c t"),
+                        out=message_source[:, a, first : first + half, :], in_=both[:].rearrange("p t c -> p c t"),
                         mul=1.0 / NODES,
                     )
+                else:
+                    nc.vector.tensor_scalar(
+                        out=message_source[:, a, first : first + half, :], in0=both[:].rearrange("p t c -> p c t"),
+                        scalar1=1.0 / NODES, scalar2=None, op0=ALU.mult,
+                    )
+        own_part = keep.tile([P, SLOTS, C], F32)
+        for s in range(SLOTS):
+            product = psum_acc.tile([P, C], F32, tag="acc")
+            multiply(product[:], own_codes, own_planes, s, "U", True, True)
+            if s % 2 == 0:
+                nc.scalar.copy(out=own_part[:, s, :], in_=product[:])
+            else:
+                nc.vector.tensor_copy(out=own_part[:, s, :], in_=product[:])
 
-        def edge_round(s, j0):
-            codes = stage.tile([P, ROUND * P], U32, align_bytes=64, tag="codes")
-            planes = stage.tile([P, ROUND * P], U8, align_bytes=64, tag="planes")
-            quantise_rows(edge_in[s][:, j0 : j0 + ROUND, :], ROUND, codes[:], planes[:])
-            stats = small.tile([P, ROUND, 2, 3], F32, tag="stats")
-            acc = []
-            for i in range(ROUND):
-                agg = psum_acc.tile([P, C], F32, name="agg%d" % i, tag="acc")
-                multiply(agg[:], own_codes, own_planes, s, "A", True, False)
-                multiply(agg[:], all_codes, all_planes, j0 + i, "B", False, False)
-                multiply(agg[:], codes, planes, i, "E", False, True)
-                nc.vector.bn_stats(out=stats[:, i, :, :].rearrange("p h k -> p (h k)"), in_=agg[:])
-                acc.append(agg)
-            rstd, shift = norm_factors(stats, ROUND)
-            result = normed.tile([P, ROUND, C], F32, tag="result")
-            for i in range(ROUND):
-                nc.scalar.activation(
-                    out=result[:, i, :], in_=acc[i][:], func=ACT.Relu,
-                    bias=shift[:, i : i + 1], scale=rstd[:, i : i + 1],
-                )
-            for i in range(0, ROUND, 2):
-                nc.gpsimd.tensor_tensor(
-                    out=result[:, i : i + 2, :], in0=result[:, i : i + 2, :],
-                    in1=edge_in[s][:, j0 + i : j0 + i + 2, :], op=ALU.add,
-                )
-            r0 = s * NODES + j0
-            nc.sync.dma_start(out=edge_out_rows[:, r0 : r0 + ROUND, :], in_=result[:])
-            return result
+        def live(n):
+            return 0 <= n < ROUNDS
 
-        def gate_round(s, j0, result):
-            pairs = slice(j0 // 2, (j0 + ROUND) // 2)
+        def place(n):
+            return n // 2, ROUND * (n % 2)
+
+        grouped_of, codes_of, planes_of, flipped_of = {}, {}, {}, {}
+        acc_of, stats_of, factors_of, result_of, gate_of, weighted_of = {}, {}, {}, {}, {}, {}
+        total_of, message_of, x_new_of = {}, {}, {}
+
+        def flip(n, pair):
+            s, j0 = place(n)
+            if pair == 0:
+                grouped_of[n] = stage.tile([P, ROUND, P, PACK], BF16, align_bytes=64, name="grouped%d" % n, tag="grouped")
+                codes_of[n] = stage.tile([P, ROUND * P], U32, align_bytes=64, name="codes%d" % n, tag="codes")
+                planes_of[n] = stage.tile([P, ROUND * P], U8, align_bytes=64, name="planes%d" % n, tag="planes")
+            flipped_of[n] = transpose_pair(edge_in[s][:, j0 : j0 + ROUND, :], 2 * pair)
+
+        def regroup(n, pair):
+            regroup_pair(flipped_of[n], grouped_of[n], 2 * pair)
+
+        def stats_tile(m):
+            if m not in stats_of:
+                stats_of[m] = small.tile([P, ROUND + 1, 2, 3], F32, name="stats%d" % m, tag="stats")
+            return stats_of[m]
+
+        def aggregate(n, i):
+            s, j0 = place(n)
+            agg = psum_acc.tile([P, C], F32, name="agg%d_%d" % (n, i), tag="acc")
+            multiply(agg[:], own_codes, own_planes, s, "A", True, False)
+            multiply(agg[:], all_codes, all_planes, j0 + i, "B", False, False)
+            multiply(agg[:], codes_of[n], planes_of[n], i, "E", False, True)
+            nc.vector.bn_stats(out=stats_tile(n)[:, i, :, :].rearrange("p h k -> p (h k)"), in_=agg[:])
+            acc_of[(n, i)] = agg
+
+        def node_of_chain(m):
+            return (m - 7) // 2 if m % 2 == 1 and 0 <= (m - 7) // 2 < SLOTS else None
+
+        def columns(m):
+            return 0 if live(m) else ROUND, ROUND if node_of_chain(m) is None else ROUND + 1
+
+        def factors_square(m):
+            lo, hi = columns(m)
+            nc.scalar.activation(out=stats_of[m][:, lo:hi, :, 0], in_=stats_of[m][:, lo:hi, :, 1], func=ACT.Square)
+
+        def factors_mean(m):
+            lo, hi = columns(m)
+            means = psum_mean.tile([P, hi - lo, 3], F32, tag="means")
+            for half in range(2):
+                nc.tensor.matmul(
+                    out=means[:], lhsT=parity[:].rearrange("p a t -> p (a t)"), rhs=stats_of[m][:, lo:hi, half, :],
+                    start=(half == 0), stop=(half == 1),
+                )
+            factors_of[m] = {"means": means}
+
+        def factors_rstd(m):
+            lo, hi = columns(m)
+            count = hi - lo
+            means = factors_of[m]["means"]
+            mean = small.tile([P, count], F32, tag="mean")
+            nc.vector.tensor_copy(out=mean[:], in_=means[:, :, 1])
+            spread = small.tile([P, count], F32, tag="spread")
+            nc.vector.tensor_tensor(out=spread[:], in0=means[:, :, 1], in1=mean[:], op=ALU.mult)
+            nc.vector.scalar_tensor_tensor(
+                out=spread[:], in0=means[:, :, 2], scalar=2.0 / C, in1=spread[:], op0=ALU.mult, op1=ALU.subtract
+            )
+            nc.vector.scalar_tensor_tensor(
+                out=spread[:], in0=means[:, :, 0], scalar=BN_EPS, in1=spread[:], op0=ALU.add, op1=ALU.add
+            )
+            rstd = small.tile([P, ROUND + 1], F32, tag="rstd")
+            nc.gpsimd.tensor_tensor(out=rstd[:, lo:hi], in0=spread[:], in1=minus_half[:, :count], op=ALU.pow)
+            factors_of[m]["rstd"] = rstd
+
+        def factors_shift(m):
+            lo, hi = columns(m)
+            shift = small.tile([P, ROUND + 1], F32, tag="shift")
+            nc.vector.scalar_tensor_tensor(
+                out=shift[:, lo:hi], in0=factors_of[m]["means"][:, :, 1], scalar=-1.0, in1=factors_of[m]["rstd"][:, lo:hi],
+                op0=ALU.mult, op1=ALU.mult,
+            )
+            factors_of[m]["shift"] = shift
+
+        def normalise(n, i):
+            if i == 0:
+                result_of[n] = normed.tile([P, ROUND, C], F32, name="result%d" % n, tag="result")
             nc.scalar.activation(
-                out=gate[s][:, pairs, :, :], in_=result[:].rearrange("p (a t) c -> p a c t", t=2),
+                out=result_of[n][:, i, :], in_=acc_of[(n, i)][:], func=ACT.Relu,
+                bias=factors_of[n]["shift"][:, i : i + 1], scale=factors_of[n]["rstd"][:, i : i + 1],
+            )
+
+        def residual(n, pair):
+            s, j0 = place(n)
+            two = slice(2 * pair, 2 * pair + 2)
+            nc.gpsimd.tensor_tensor(
+                out=result_of[n][:, two, :], in0=result_of[n][:, two, :],
+                in1=edge_in[s][:, j0 + 2 * pair : j0 + 2 * pair + 2, :], op=ALU.add,
+            )
+            r0 = s * NODES + j0 + 2 * pair
+            nc.sync.dma_start(out=edge_out_rows[:, r0 : r0 + 2, :], in_=result_of[n][:, two, :])
+
+        def squash(n, pair):
+            if pair == 0:
+                gate_of[n] = gates.tile([P, PAIRS, C, 2], F32, name="gate%d" % n, tag="gate")
+            nc.scalar.activation(
+                out=gate_of[n][:, pair, :, :],
+                in_=result_of[n][:, 2 * pair : 2 * pair + 2, :].rearrange("p t c -> p c t"),
                 func=ACT.Tanh, scale=0.5,
             )
-            nc.scalar.activation(out=gate[s][:, pairs, :, :], in_=gate[s][:, pairs, :, :], func=ACT.Exp, scale=0.5)
-            nc.gpsimd.tensor_tensor(
-                out=weighted[s][:, pairs, :, :], in0=gate[s][:, pairs, :, :], in1=message_source[:, pairs, :, :],
+
+        def exponent(n, pair):
+            nc.scalar.activation(out=gate_of[n][:, pair, :, :], in_=gate_of[n][:, pair, :, :], func=ACT.Exp, scale=0.5)
+
+        def weigh(n, pair):
+            if pair == 0:
+                weighted_of[n] = gated.tile([P, PAIRS, C, 2], F32, name="weighted%d" % n, tag="weighted")
+            a = (n % 2) * PAIRS + pair
+            engine = nc.vector if pair == PAIRS - 1 else nc.gpsimd
+            engine.tensor_tensor(
+                out=weighted_of[n][:, pair, :, :], in0=gate_of[n][:, pair, :, :], in1=message_source[:, a, :, :],
                 op=ALU.mult,
             )
 
-        def node_update(s):
-            total = nodes.tile([P, C], F32, tag="total")
-            message = nodes.tile([P, C], F32, tag="message")
-            quarter = C // 4
-            for first in range(0, C, quarter):
-                cols = slice(first, first + quarter)
-                nc.vector.tensor_reduce(
-                    out=total[:, cols], in_=gate[s][:, :, cols, :].rearrange("p a c t -> p c a t"),
-                    axis=AXIS.XY, op=ALU.add,
-                )
-                nc.vector.tensor_reduce(
-                    out=message[:, cols], in_=weighted[s][:, :, cols, :].rearrange("p a c t -> p c a t"),
-                    axis=AXIS.XY, op=ALU.add,
-                )
-            nc.vector.reciprocal(out=total[:], in_=total[:])
-            nc.vector.tensor_tensor(out=message[:], in0=message[:], in1=total[:], op=ALU.mult)
-            own = psum_acc.tile([P, C], F32, tag="acc")
-            multiply(own[:], own_codes, own_planes, s, "U", True, True)
-            x_new = nodes.tile([P, C], F32, tag="x_new")
-            nc.vector.tensor_tensor(out=x_new[:], in0=message[:], in1=own[:], op=ALU.add)
-            stats = small.tile([P, 1, 2, 3], F32, tag="node_stats")
-            nc.vector.bn_stats(out=stats[:, 0, :, :].rearrange("p h k -> p (h k)"), in_=x_new[:])
-            rstd, shift = norm_factors(stats, 1)
-            nc.vector.scalar_tensor_tensor(
-                out=x_new[:], in0=x_new[:], scalar=rstd[:, 0:1], in1=x_own[:, s, :], op0=ALU.mult, op1=ALU.add
+        def sum_over_senders(source, out, half):
+            cols = slice(half * C // 2, (half + 1) * C // 2)
+            nc.vector.tensor_reduce(
+                out=out[:, cols], in_=source[:, :, cols, :].rearrange("p a c t -> p c a t"), axis=AXIS.XY, op=ALU.add
             )
-            nc.scalar.activation(out=x_new[:], in_=x_new[:], func=ACT.Relu, bias=shift[:, 0:1], scale=1.0)
+
+        def sum_gates(n, half):
+            if half == 0:
+                total_of[n] = sums.tile([P, C], F32, name="total%d" % n, tag="total")
+            sum_over_senders(gate_of[n], total_of[n], half)
+
+        def sum_messages(n, half):
+            if half == 0:
+                message_of[n] = sums.tile([P, C], F32, name="message%d" % n, tag="message")
+            sum_over_senders(weighted_of[n], message_of[n], half)
+
+        def node_join(s):
+            nc.vector.tensor_tensor(out=total_of[2 * s][:], in0=total_of[2 * s][:], in1=total_of[2 * s + 1][:], op=ALU.add)
+            nc.vector.tensor_tensor(
+                out=message_of[2 * s][:], in0=message_of[2 * s][:], in1=message_of[2 * s + 1][:], op=ALU.add
+            )
+
+        def node_invert(s):
+            total = total_of[2 * s]
+            nc.scalar.activation(out=total[:], in_=total[:], func=ACT.Ln)
+            nc.scalar.activation(out=total[:], in_=total[:], func=ACT.Exp, scale=-1.0)
+
+        def node_sum(s):
+            message = message_of[2 * s]
+            nc.vector.tensor_tensor(out=message[:], in0=message[:], in1=total_of[2 * s][:], op=ALU.mult)
+            x_new = nodes.tile([P, C], F32, tag="x_new")
+            nc.vector.tensor_tensor(out=x_new[:], in0=message[:], in1=own_part[:, s, :], op=ALU.add)
+            nc.vector.bn_stats(out=stats_tile(2 * s + 7)[:, ROUND, :, :].rearrange("p h k -> p (h k)"), in_=x_new[:])
+            x_new_of[s] = x_new
+
+        def node_finish(s):
+            f = factors_of[2 * s + 7]
+            x_new = x_new_of[s]
+            nc.vector.scalar_tensor_tensor(
+                out=x_new[:], in0=x_new[:], scalar=f["rstd"][:, ROUND : ROUND + 1], in1=x_own[:, s, :],
+                op0=ALU.mult, op1=ALU.add,
+            )
+            nc.scalar.activation(
+                out=x_new[:], in_=x_new[:], func=ACT.Relu, bias=f["shift"][:, ROUND : ROUND + 1], scale=1.0
+            )
             nc.sync.dma_start(out=x_out_rows[:, s, :], in_=x_new[:])
 
-        load_edges(0)
-        load_edges(1)
-        for s in range(SLOTS):
-            if s + 2 < SLOTS:
-                load_edges(s + 2)
-            gate[s] = gates.tile([P, PAIRS, C, 2], F32, name="gate%d" % s, tag="gate")
-            weighted[s] = gated.tile([P, PAIRS, C, 2], F32, name="weighted%d" % s, tag="weighted")
-            for j0 in range(0, NODES, ROUND):
-                result = edge_round(s, j0)
-                if s == 0 and j0 == 0:
-                    message_sources()
-                gate_round(s, j0, result)
-            node_update(s)
+        def slot_ending(n):
+            return n // 2 if live(n) and n % 2 == 1 else None
+
+        for n in range(-2, ROUNDS + 6):
+            chain = n + 1
+            has_chain = columns(chain)[0] < columns(chain)[1]
+            if n % 2 == 0 and 2 <= (n + 4) // 2 < SLOTS:
+                load_edges((n + 4) // 2)
+            if live(n - 2):
+                sum_gates(n - 2, 0)
+                sum_gates(n - 2, 1)
+            for i in range(ROUND):
+                if live(n):
+                    normalise(n, i)
+                if live(n + 1):
+                    aggregate(n + 1, i)
+                if live(n) and i % 2 == 1:
+                    residual(n, i // 2)
+            if live(n + 2):
+                flip(n + 2, 0)
+            if live(n - 1):
+                squash(n - 1, 0)
+                exponent(n - 1, 0)
+                weigh(n - 1, 0)
+            if live(n + 2):
+                regroup(n + 2, 0)
+                flip(n + 2, 1)
+            if live(n - 2):
+                sum_messages(n - 2, 0)
+            if live(n - 1):
+                squash(n - 1, 1)
+                exponent(n - 1, 1)
+            if has_chain:
+                factors_square(chain)
+                factors_mean(chain)
+            if live(n - 2):
+                sum_messages(n - 2, 1)
+            if has_chain:
+                factors_rstd(chain)
+            if live(n - 1):
+                weigh(n - 1, 1)
+            if live(n + 2):
+                regroup(n + 2, 1)
+                flip(n + 2, 2)
+            if live(n - 1):
+                squash(n - 1, 2)
+                exponent(n - 1, 2)
+                weigh(n - 1, 2)
+            if live(n + 2):
+                regroup(n + 2, 2)
+            if slot_ending(n - 3) is not None:
+                node_invert(slot_ending(n - 3))
+            if has_chain:
+                factors_shift(chain)
+            if live(n + 2):
+                quantise(grouped_of[n + 2], codes_of[n + 2], planes_of[n + 2], 0, 4)
+                quantise(grouped_of[n + 2], codes_of[n + 2], planes_of[n + 2], 4, 2)
+            if slot_ending(n - 2) is not None:
+                node_join(slot_ending(n - 2))
+            if slot_ending(n - 4) is not None:
+                node_sum(slot_ending(n - 4))
+            if node_of_chain(chain) is not None:
+                node_finish(node_of_chain(chain))

@@ -17,9 +17,13 @@ GRAPHS, NODES, C = 64, 12, 512
 P = 128
 PACK = 4
 SLOTS = NODES // 2
-ROUND = 6
-PAIRS = ROUND // 2
-ROUNDS = SLOTS * NODES // ROUND
+UNIT = 2
+UNITS = SLOTS * NODES // UNIT
+UNITS_PER_SLOT = NODES // UNIT
+GROUP = 3
+GROUPS = UNITS // GROUP
+AHEAD = 3
+BATCH = 2
 BN_EPS = 1e-5
 WEIGHT_NAMES = ("A", "B", "E", "U", "V")
 
@@ -44,15 +48,16 @@ def tile_graphmodel_pa_kernel(
     with ExitStack() as ctx:
         keep = ctx.enter_context(tc.tile_pool(name="keep", bufs=1))
         edges = ctx.enter_context(tc.tile_pool(name="edges", bufs=3))
+        early = ctx.enter_context(tc.tile_pool(name="early", bufs=2))
         stage = ctx.enter_context(tc.tile_pool(name="stage", bufs=2))
-        normed = ctx.enter_context(tc.tile_pool(name="normed", bufs=2))
+        normed = ctx.enter_context(tc.tile_pool(name="normed", bufs=4))
         gates = ctx.enter_context(tc.tile_pool(name="gates", bufs=2))
         gated = ctx.enter_context(tc.tile_pool(name="gated", bufs=2))
         sums = ctx.enter_context(tc.tile_pool(name="sums", bufs=4))
         nodes = ctx.enter_context(tc.tile_pool(name="nodes", bufs=2))
-        small = ctx.enter_context(tc.tile_pool(name="small", bufs=3))
+        small = ctx.enter_context(tc.tile_pool(name="small", bufs=6))
         psum_flip = ctx.enter_context(tc.psum_pool(name="psum_flip", bufs=1))
-        psum_acc = ctx.enter_context(tc.psum_pool(name="psum_acc", bufs=ROUND))
+        psum_acc = ctx.enter_context(tc.psum_pool(name="psum_acc", bufs=AHEAD * UNIT))
         psum_mean = ctx.enter_context(tc.psum_pool(name="psum_mean", bufs=1))
         ctx.enter_context(tc.manual_schedule())
 
@@ -104,7 +109,7 @@ def tile_graphmodel_pa_kernel(
             out=parity[:], in0=own_parity[:].unsqueeze(1).to_broadcast([P, P // 2, 2]),
             scalar1=1.0 / P, scalar2=None, op0=ALU.mult,
         )
-        minus_half = keep.tile([P, ROUND + 1], F32)
+        minus_half = keep.tile([P, UNIT + 1], F32)
         nc.vector.memset(minus_half[:], -0.5)
 
         def transpose_pair(rows, first, pool=psum_flip, tag="flipped"):
@@ -145,15 +150,17 @@ def tile_graphmodel_pa_kernel(
         own_codes = keep.tile([P, SLOTS * P], U32, align_bytes=64)
         own_planes = keep.tile([P, SLOTS * P], U8, align_bytes=64)
         for rows, codes, planes, base in (
-            (x_all, all_codes, all_planes, 0), (x_own, own_codes, own_planes, 0), (x_all, all_codes, all_planes, ROUND),
+            (x_all, all_codes, all_planes, 0), (x_own, own_codes, own_planes, 0), (x_all, all_codes, all_planes, SLOTS),
         ):
-            grouped = stage.tile([P, ROUND, P, PACK], BF16, align_bytes=64, tag="grouped")
-            for first in range(0, ROUND, 2):
-                flipped = transpose_pair(rows[:, base : base + ROUND, :], first, pool=psum_acc, tag="acc")
+            grouped = early.tile([P, SLOTS, P, PACK], BF16, align_bytes=64, tag="grouped_x")
+            for first in range(0, SLOTS, 2):
+                flipped = transpose_pair(rows[:, base : base + SLOTS, :], first, pool=psum_acc, tag="acc")
                 regroup_pair(flipped, grouped, first, engine_copy=nc.vector.tensor_copy if first == 2 else nc.scalar.copy)
-            part = slice(base * P, (base + ROUND) * P)
+            part = slice(base * P, (base + SLOTS) * P)
             quantise(grouped, codes[:, part], planes[:, part], 0, 4)
             quantise(grouped, codes[:, part], planes[:, part], 4, 2)
+
+        load_edges(2)
 
         message_source = keep.tile([P, NODES // 2, C, 2], F32)
 
@@ -183,46 +190,55 @@ def tile_graphmodel_pa_kernel(
             else:
                 nc.vector.tensor_copy(out=own_part[:, s, :], in_=product[:])
 
-        def live(n):
-            return 0 <= n < ROUNDS
-
-        def place(n):
-            return n // 2, ROUND * (n % 2)
+        def live(u):
+            return 0 <= u < UNITS
 
         grouped_of, codes_of, planes_of, flipped_of = {}, {}, {}, {}
         acc_of, stats_of, factors_of, result_of, gate_of, weighted_of = {}, {}, {}, {}, {}, {}
         total_of, message_of, x_new_of = {}, {}, {}
 
-        def flip(n, pair):
-            s, j0 = place(n)
-            if pair == 0:
-                grouped_of[n] = stage.tile([P, ROUND, P, PACK], BF16, align_bytes=64, name="grouped%d" % n, tag="grouped")
-                codes_of[n] = stage.tile([P, ROUND * P], U32, align_bytes=64, name="codes%d" % n, tag="codes")
-                planes_of[n] = stage.tile([P, ROUND * P], U8, align_bytes=64, name="planes%d" % n, tag="planes")
-            flipped_of[n] = transpose_pair(edge_in[s][:, j0 : j0 + ROUND, :], 2 * pair)
+        def flip(u):
+            s, a = u // UNITS_PER_SLOT, u % UNITS_PER_SLOT
+            flipped_of[u] = transpose_pair(edge_in[s], UNIT * a)
 
-        def regroup(n, pair):
-            regroup_pair(flipped_of[n], grouped_of[n], 2 * pair)
+        def regroup(u):
+            b, k = u // BATCH, u % BATCH
+            if k == 0:
+                grouped_of[b] = stage.tile(
+                    [P, BATCH * UNIT, P, PACK], BF16, align_bytes=64, name="grouped%d" % b, tag="grouped"
+                )
+            regroup_pair(flipped_of[u], grouped_of[b], UNIT * k)
+
+        def quantise_batch(b):
+            codes_of[b] = stage.tile([P, BATCH * UNIT * P], U32, align_bytes=64, name="codes%d" % b, tag="codes")
+            planes_of[b] = stage.tile([P, BATCH * UNIT * P], U8, align_bytes=64, name="planes%d" % b, tag="planes")
+            quantise(grouped_of[b], codes_of[b], planes_of[b], 0, BATCH * UNIT)
 
         def stats_tile(m):
             if m not in stats_of:
-                stats_of[m] = small.tile([P, ROUND + 1, 2, 3], F32, name="stats%d" % m, tag="stats")
+                stats_of[m] = small.tile([P, UNIT + 1, 2, 3], F32, name="stats%d" % m, tag="stats")
             return stats_of[m]
 
-        def aggregate(n, i):
-            s, j0 = place(n)
-            agg = psum_acc.tile([P, C], F32, name="agg%d_%d" % (n, i), tag="acc")
-            multiply(agg[:], own_codes, own_planes, s, "A", True, False)
-            multiply(agg[:], all_codes, all_planes, j0 + i, "B", False, False)
-            multiply(agg[:], codes_of[n], planes_of[n], i, "E", False, True)
-            nc.vector.bn_stats(out=stats_tile(n)[:, i, :, :].rearrange("p h k -> p (h k)"), in_=agg[:])
-            acc_of[(n, i)] = agg
+        def aggregate(u):
+            s, a = u // UNITS_PER_SLOT, u % UNITS_PER_SLOT
+            for i in range(UNIT):
+                agg = psum_acc.tile([P, C], F32, name="agg%d_%d" % (u, i), tag="acc")
+                multiply(agg[:], own_codes, own_planes, s, "A", True, False)
+                multiply(agg[:], all_codes, all_planes, UNIT * a + i, "B", False, False)
+                multiply(agg[:], codes_of[u // BATCH], planes_of[u // BATCH], UNIT * (u % BATCH) + i, "E", False, True)
+                acc_of[(u, i)] = agg
 
-        def node_of_chain(m):
-            return (m - 7) // 2 if m % 2 == 1 and 0 <= (m - 7) // 2 < SLOTS else None
+        def statistics(u):
+            for i in range(UNIT):
+                nc.vector.bn_stats(out=stats_tile(u)[:, i, :, :].rearrange("p h k -> p (h k)"), in_=acc_of[(u, i)][:])
+
+        node_in_chain = {}
 
         def columns(m):
-            return 0 if live(m) else ROUND, ROUND if node_of_chain(m) is None else ROUND + 1
+            return 0 if live(m) else UNIT, UNIT + 1 if m in node_in_chain else UNIT
+
+        def has_chain(m):
+            return columns(m)[0] < columns(m)[1]
 
         def factors_square(m):
             lo, hi = columns(m)
@@ -238,71 +254,73 @@ def tile_graphmodel_pa_kernel(
                 )
             factors_of[m] = {"means": means}
 
-        def factors_rstd(m):
+        def factors_spread(m):
             lo, hi = columns(m)
             count = hi - lo
             means = factors_of[m]["means"]
-            mean = small.tile([P, count], F32, tag="mean")
-            nc.vector.tensor_copy(out=mean[:], in_=means[:, :, 1])
+            minus_mean = small.tile([P, UNIT + 1], F32, tag="minus_mean")
+            nc.vector.tensor_scalar(
+                out=minus_mean[:, lo:hi], in0=means[:, :, 1], scalar1=-1.0, scalar2=None, op0=ALU.mult
+            )
             spread = small.tile([P, count], F32, tag="spread")
-            nc.vector.tensor_tensor(out=spread[:], in0=means[:, :, 1], in1=mean[:], op=ALU.mult)
+            nc.vector.tensor_tensor(out=spread[:], in0=means[:, :, 1], in1=minus_mean[:, lo:hi], op=ALU.mult)
             nc.vector.scalar_tensor_tensor(
-                out=spread[:], in0=means[:, :, 2], scalar=2.0 / C, in1=spread[:], op0=ALU.mult, op1=ALU.subtract
+                out=spread[:], in0=means[:, :, 2], scalar=2.0 / C, in1=spread[:], op0=ALU.mult, op1=ALU.add
             )
             nc.vector.scalar_tensor_tensor(
                 out=spread[:], in0=means[:, :, 0], scalar=BN_EPS, in1=spread[:], op0=ALU.add, op1=ALU.add
             )
-            rstd = small.tile([P, ROUND + 1], F32, tag="rstd")
-            nc.gpsimd.tensor_tensor(out=rstd[:, lo:hi], in0=spread[:], in1=minus_half[:, :count], op=ALU.pow)
-            factors_of[m]["rstd"] = rstd
+            factors_of[m]["minus_mean"] = minus_mean
+            factors_of[m]["spread"] = spread
 
-        def factors_shift(m):
+        def factors_rstd(m):
             lo, hi = columns(m)
-            shift = small.tile([P, ROUND + 1], F32, tag="shift")
-            nc.vector.scalar_tensor_tensor(
-                out=shift[:, lo:hi], in0=factors_of[m]["means"][:, :, 1], scalar=-1.0, in1=factors_of[m]["rstd"][:, lo:hi],
-                op0=ALU.mult, op1=ALU.mult,
-            )
+            minus_mean, spread = factors_of[m]["minus_mean"], factors_of[m]["spread"]
+            rstd = small.tile([P, UNIT + 1], F32, tag="rstd")
+            nc.gpsimd.tensor_tensor(out=rstd[:, lo:hi], in0=spread[:], in1=minus_half[:, : hi - lo], op=ALU.pow)
+            shift = small.tile([P, UNIT + 1], F32, tag="shift")
+            nc.gpsimd.tensor_tensor(out=shift[:, lo:hi], in0=minus_mean[:, lo:hi], in1=rstd[:, lo:hi], op=ALU.mult)
+            factors_of[m]["rstd"] = rstd
             factors_of[m]["shift"] = shift
 
-        def normalise(n, i):
-            if i == 0:
-                result_of[n] = normed.tile([P, ROUND, C], F32, name="result%d" % n, tag="result")
-            nc.scalar.activation(
-                out=result_of[n][:, i, :], in_=acc_of[(n, i)][:], func=ACT.Relu,
-                bias=factors_of[n]["shift"][:, i : i + 1], scale=factors_of[n]["rstd"][:, i : i + 1],
-            )
+        def normalise(u):
+            result_of[u] = normed.tile([P, UNIT, C], F32, name="result%d" % u, tag="result")
+            for i in range(UNIT):
+                nc.scalar.activation(
+                    out=result_of[u][:, i, :], in_=acc_of[(u, i)][:], func=ACT.Relu,
+                    bias=factors_of[u]["shift"][:, i : i + 1], scale=factors_of[u]["rstd"][:, i : i + 1],
+                )
 
-        def residual(n, pair):
-            s, j0 = place(n)
-            two = slice(2 * pair, 2 * pair + 2)
+        def residual(u):
+            s, a = u // UNITS_PER_SLOT, u % UNITS_PER_SLOT
             nc.gpsimd.tensor_tensor(
-                out=result_of[n][:, two, :], in0=result_of[n][:, two, :],
-                in1=edge_in[s][:, j0 + 2 * pair : j0 + 2 * pair + 2, :], op=ALU.add,
+                out=result_of[u][:], in0=result_of[u][:], in1=edge_in[s][:, UNIT * a : UNIT * (a + 1), :], op=ALU.add
             )
-            r0 = s * NODES + j0 + 2 * pair
-            nc.sync.dma_start(out=edge_out_rows[:, r0 : r0 + 2, :], in_=result_of[n][:, two, :])
+            nc.sync.dma_start(out=edge_out_rows[:, UNIT * u : UNIT * (u + 1), :], in_=result_of[u][:])
 
-        def squash(n, pair):
-            if pair == 0:
-                gate_of[n] = gates.tile([P, PAIRS, C, 2], F32, name="gate%d" % n, tag="gate")
+        def squash(u):
+            g, k = u // GROUP, u % GROUP
+            if k == 0:
+                gate_of[g] = gates.tile([P, GROUP, C, UNIT], F32, name="gate%d" % g, tag="gate")
             nc.scalar.activation(
-                out=gate_of[n][:, pair, :, :],
-                in_=result_of[n][:, 2 * pair : 2 * pair + 2, :].rearrange("p t c -> p c t"),
-                func=ACT.Tanh, scale=0.5,
+                out=gate_of[g][:, k, :, :], in_=result_of[u][:].rearrange("p t c -> p c t"), func=ACT.Tanh, scale=0.5
             )
 
-        def exponent(n, pair):
-            nc.scalar.activation(out=gate_of[n][:, pair, :, :], in_=gate_of[n][:, pair, :, :], func=ACT.Exp, scale=0.5)
+        def exponent(u):
+            g, k = u // GROUP, u % GROUP
+            nc.scalar.activation(out=gate_of[g][:, k, :, :], in_=gate_of[g][:, k, :, :], func=ACT.Exp, scale=0.5)
 
-        def weigh(n, pair):
-            if pair == 0:
-                weighted_of[n] = gated.tile([P, PAIRS, C, 2], F32, name="weighted%d" % n, tag="weighted")
-            a = (n % 2) * PAIRS + pair
-            engine = nc.vector if pair == PAIRS - 1 else nc.gpsimd
+        def on_vector(u):
+            return u % 3 == 2
+
+        def weigh(u):
+            g, k = u // GROUP, u % GROUP
+            if k == 0:
+                weighted_of[g] = gated.tile([P, GROUP, C, UNIT], F32, name="weighted%d" % g, tag="weighted")
+            engine = nc.vector if on_vector(u) else nc.gpsimd
             engine.tensor_tensor(
-                out=weighted_of[n][:, pair, :, :], in0=gate_of[n][:, pair, :, :], in1=message_source[:, a, :, :],
-                op=ALU.mult,
+                out=weighted_of[g][:, k, :, :], in0=gate_of[g][:, k, :, :],
+                in1=message_source[:, u % UNITS_PER_SLOT, :, :], op=ALU.mult,
             )
 
         def sum_over_senders(source, out, half):
@@ -311,15 +329,15 @@ def tile_graphmodel_pa_kernel(
                 out=out[:, cols], in_=source[:, :, cols, :].rearrange("p a c t -> p c a t"), axis=AXIS.XY, op=ALU.add
             )
 
-        def sum_gates(n, half):
+        def sum_gates(g, half):
             if half == 0:
-                total_of[n] = sums.tile([P, C], F32, name="total%d" % n, tag="total")
-            sum_over_senders(gate_of[n], total_of[n], half)
+                total_of[g] = sums.tile([P, C], F32, name="total%d" % g, tag="total")
+            sum_over_senders(gate_of[g], total_of[g], half)
 
-        def sum_messages(n, half):
+        def sum_messages(g, half):
             if half == 0:
-                message_of[n] = sums.tile([P, C], F32, name="message%d" % n, tag="message")
-            sum_over_senders(weighted_of[n], message_of[n], half)
+                message_of[g] = sums.tile([P, C], F32, name="message%d" % g, tag="message")
+            sum_over_senders(weighted_of[g], message_of[g], half)
 
         def node_join(s):
             nc.vector.tensor_tensor(out=total_of[2 * s][:], in0=total_of[2 * s][:], in1=total_of[2 * s + 1][:], op=ALU.add)
@@ -332,86 +350,75 @@ def tile_graphmodel_pa_kernel(
             nc.scalar.activation(out=total[:], in_=total[:], func=ACT.Ln)
             nc.scalar.activation(out=total[:], in_=total[:], func=ACT.Exp, scale=-1.0)
 
-        def node_sum(s):
+        def node_sum(s, chain):
             message = message_of[2 * s]
             nc.vector.tensor_tensor(out=message[:], in0=message[:], in1=total_of[2 * s][:], op=ALU.mult)
             x_new = nodes.tile([P, C], F32, tag="x_new")
             nc.vector.tensor_tensor(out=x_new[:], in0=message[:], in1=own_part[:, s, :], op=ALU.add)
-            nc.vector.bn_stats(out=stats_tile(2 * s + 7)[:, ROUND, :, :].rearrange("p h k -> p (h k)"), in_=x_new[:])
+            nc.vector.bn_stats(out=stats_tile(chain)[:, UNIT, :, :].rearrange("p h k -> p (h k)"), in_=x_new[:])
             x_new_of[s] = x_new
+            node_in_chain[chain] = s
 
-        def node_finish(s):
-            f = factors_of[2 * s + 7]
-            x_new = x_new_of[s]
+        def node_scale(s, chain):
             nc.vector.scalar_tensor_tensor(
-                out=x_new[:], in0=x_new[:], scalar=f["rstd"][:, ROUND : ROUND + 1], in1=x_own[:, s, :],
-                op0=ALU.mult, op1=ALU.add,
+                out=x_new_of[s][:], in0=x_new_of[s][:], scalar=factors_of[chain]["rstd"][:, UNIT : UNIT + 1],
+                in1=x_own[:, s, :], op0=ALU.mult, op1=ALU.add,
             )
+
+        def node_finish(s, chain):
             nc.scalar.activation(
-                out=x_new[:], in_=x_new[:], func=ACT.Relu, bias=f["shift"][:, ROUND : ROUND + 1], scale=1.0
+                out=x_new_of[s][:], in_=x_new_of[s][:], func=ACT.Relu,
+                bias=factors_of[chain]["shift"][:, UNIT : UNIT + 1], scale=1.0,
             )
-            nc.sync.dma_start(out=x_out_rows[:, s, :], in_=x_new[:])
+            nc.sync.dma_start(out=x_out_rows[:, s, :], in_=x_new_of[s][:])
 
-        def slot_ending(n):
-            return n // 2 if live(n) and n % 2 == 1 else None
+        def group_ending(u):
+            return u // GROUP if live(u) and u % GROUP == GROUP - 1 else None
 
-        for n in range(-2, ROUNDS + 6):
-            chain = n + 1
-            has_chain = columns(chain)[0] < columns(chain)[1]
-            if n % 2 == 0 and 2 <= (n + 4) // 2 < SLOTS:
-                load_edges((n + 4) // 2)
+        def slot_ending(u):
+            return u // UNITS_PER_SLOT if live(u) and u % UNITS_PER_SLOT == UNITS_PER_SLOT - 1 else None
+
+        for n in range(-7, UNITS + 20):
+            if live(n):
+                normalise(n)
+            if has_chain(n + 1):
+                factors_rstd(n + 1)
+            if live(n + 3):
+                aggregate(n + 3)
+            if live(n - 1):
+                residual(n - 1)
+            if slot_ending(n - 1) is not None and slot_ending(n - 1) + 3 < SLOTS:
+                load_edges(slot_ending(n - 1) + 3)
+            if has_chain(n + 2):
+                factors_square(n + 2)
+                factors_mean(n + 2)
             if live(n - 2):
-                sum_gates(n - 2, 0)
-                sum_gates(n - 2, 1)
-            for i in range(ROUND):
-                if live(n):
-                    normalise(n, i)
-                if live(n + 1):
-                    aggregate(n + 1, i)
-                if live(n) and i % 2 == 1:
-                    residual(n, i // 2)
-            if live(n + 2):
-                flip(n + 2, 0)
-            if live(n - 1):
-                squash(n - 1, 0)
-                exponent(n - 1, 0)
-                weigh(n - 1, 0)
-            if live(n + 2):
-                regroup(n + 2, 0)
-                flip(n + 2, 1)
-            if live(n - 2):
-                sum_messages(n - 2, 0)
-            if live(n - 1):
-                squash(n - 1, 1)
-                exponent(n - 1, 1)
-            if has_chain:
-                factors_square(chain)
-                factors_mean(chain)
-            if live(n - 2):
-                sum_messages(n - 2, 1)
-            if has_chain:
-                factors_rstd(chain)
-            if live(n - 1):
-                weigh(n - 1, 1)
-            if live(n + 2):
-                regroup(n + 2, 1)
-                flip(n + 2, 2)
-            if live(n - 1):
-                squash(n - 1, 2)
-                exponent(n - 1, 2)
-                weigh(n - 1, 2)
-            if live(n + 2):
-                regroup(n + 2, 2)
-            if slot_ending(n - 3) is not None:
-                node_invert(slot_ending(n - 3))
-            if has_chain:
-                factors_shift(chain)
-            if live(n + 2):
-                quantise(grouped_of[n + 2], codes_of[n + 2], planes_of[n + 2], 0, 4)
-                quantise(grouped_of[n + 2], codes_of[n + 2], planes_of[n + 2], 4, 2)
-            if slot_ending(n - 2) is not None:
-                node_join(slot_ending(n - 2))
-            if slot_ending(n - 4) is not None:
-                node_sum(slot_ending(n - 4))
-            if node_of_chain(chain) is not None:
-                node_finish(node_of_chain(chain))
+                squash(n - 2)
+                exponent(n - 2)
+            if live(n + 4) and (n + 4) % BATCH == 0:
+                quantise_batch((n + 4) // BATCH)
+            if live(n - 3):
+                weigh(n - 3)
+            if slot_ending(n - 5) is not None:
+                node_join(slot_ending(n - 5))
+            if slot_ending(n - 9) is not None:
+                node_sum(slot_ending(n - 9), n + 4)
+            if slot_ending(n - 13) is not None:
+                node_scale(slot_ending(n - 13), n)
+            if live(n + 6):
+                regroup(n + 6)
+            if live(n + 7):
+                flip(n + 7)
+            for half in range(2):
+                if group_ending(n - 3) is not None:
+                    sum_gates(group_ending(n - 3), half)
+                if group_ending(n - 4) is not None:
+                    sum_messages(group_ending(n - 4), half)
+            if live(n + 3):
+                statistics(n + 3)
+            if has_chain(n + 2):
+                factors_spread(n + 2)
+            if slot_ending(n - 6) is not None:
+                node_invert(slot_ending(n - 6))
+            if slot_ending(n - 14) is not None:
+                node_finish(slot_ending(n - 14), n - 1)

@@ -109,6 +109,10 @@ def tile_graphmodel_pa_kernel(
             out=parity[:], in0=own_parity[:].unsqueeze(1).to_broadcast([P, P // 2, 2]),
             scalar1=1.0 / P, scalar2=None, op0=ALU.mult,
         )
+        parity_over_n = keep.tile([P, P], F32)
+        nc.vector.tensor_scalar(
+            out=parity_over_n[:], in0=parity[:].rearrange("p a t -> p (a t)"), scalar1=2.0 / C, scalar2=None, op0=ALU.mult
+        )
         minus_half = keep.tile([P, UNIT + 1], F32)
         nc.vector.memset(minus_half[:], -0.5)
 
@@ -228,9 +232,8 @@ def tile_graphmodel_pa_kernel(
                 multiply(agg[:], codes_of[u // BATCH], planes_of[u // BATCH], UNIT * (u % BATCH) + i, "E", False, True)
                 acc_of[(u, i)] = agg
 
-        def statistics(u):
-            for i in range(UNIT):
-                nc.vector.bn_stats(out=stats_tile(u)[:, i, :, :].rearrange("p h k -> p (h k)"), in_=acc_of[(u, i)][:])
+        def statistics(u, i):
+            nc.vector.bn_stats(out=stats_tile(u)[:, i, :, :].rearrange("p h k -> p (h k)"), in_=acc_of[(u, i)][:])
 
         node_in_chain = {}
 
@@ -246,41 +249,59 @@ def tile_graphmodel_pa_kernel(
 
         def factors_mean(m):
             lo, hi = columns(m)
-            means = psum_mean.tile([P, hi - lo, 3], F32, tag="means")
+            means = psum_mean.tile([P, hi - lo, 2], F32, tag="means")
             for half in range(2):
                 nc.tensor.matmul(
-                    out=means[:], lhsT=parity[:].rearrange("p a t -> p (a t)"), rhs=stats_of[m][:, lo:hi, half, :],
-                    start=(half == 0), stop=(half == 1),
+                    out=means[:], lhsT=parity[:].rearrange("p a t -> p (a t)"), rhs=stats_of[m][:, lo:hi, half, 0:2],
+                    start=(half == 0), stop=False,
+                )
+            for half in range(2):
+                nc.tensor.matmul(
+                    out=means[:, :, 0], lhsT=parity_over_n[:], rhs=stats_of[m][:, lo:hi, half, 2],
+                    start=False, stop=(half == 1),
                 )
             factors_of[m] = {"means": means}
 
-        def factors_spread(m):
+        def factors_minus_mean(m):
             lo, hi = columns(m)
-            count = hi - lo
-            means = factors_of[m]["means"]
             minus_mean = small.tile([P, UNIT + 1], F32, tag="minus_mean")
             nc.vector.tensor_scalar(
-                out=minus_mean[:, lo:hi], in0=means[:, :, 1], scalar1=-1.0, scalar2=None, op0=ALU.mult
-            )
-            spread = small.tile([P, count], F32, tag="spread")
-            nc.vector.tensor_tensor(out=spread[:], in0=means[:, :, 1], in1=minus_mean[:, lo:hi], op=ALU.mult)
-            nc.vector.scalar_tensor_tensor(
-                out=spread[:], in0=means[:, :, 2], scalar=2.0 / C, in1=spread[:], op0=ALU.mult, op1=ALU.add
-            )
-            nc.vector.scalar_tensor_tensor(
-                out=spread[:], in0=means[:, :, 0], scalar=BN_EPS, in1=spread[:], op0=ALU.add, op1=ALU.add
+                out=minus_mean[:, lo:hi], in0=factors_of[m]["means"][:, :, 1], scalar1=-1.0, scalar2=None, op0=ALU.mult
             )
             factors_of[m]["minus_mean"] = minus_mean
+
+        def factors_minus_square(m):
+            lo, hi = columns(m)
+            spread = small.tile([P, UNIT + 1], F32, tag="spread")
+            nc.vector.tensor_tensor(
+                out=spread[:, lo:hi], in0=factors_of[m]["means"][:, :, 1], in1=factors_of[m]["minus_mean"][:, lo:hi],
+                op=ALU.mult,
+            )
             factors_of[m]["spread"] = spread
+
+        def factors_spread(m):
+            lo, hi = columns(m)
+            spread = factors_of[m]["spread"]
+            nc.vector.scalar_tensor_tensor(
+                out=spread[:, lo:hi], in0=factors_of[m]["means"][:, :, 0], scalar=BN_EPS, in1=spread[:, lo:hi],
+                op0=ALU.add, op1=ALU.add,
+            )
 
         def factors_rstd(m):
             lo, hi = columns(m)
-            minus_mean, spread = factors_of[m]["minus_mean"], factors_of[m]["spread"]
             rstd = small.tile([P, UNIT + 1], F32, tag="rstd")
-            nc.gpsimd.tensor_tensor(out=rstd[:, lo:hi], in0=spread[:], in1=minus_half[:, : hi - lo], op=ALU.pow)
-            shift = small.tile([P, UNIT + 1], F32, tag="shift")
-            nc.gpsimd.tensor_tensor(out=shift[:, lo:hi], in0=minus_mean[:, lo:hi], in1=rstd[:, lo:hi], op=ALU.mult)
+            nc.gpsimd.tensor_tensor(
+                out=rstd[:, lo:hi], in0=factors_of[m]["spread"][:, lo:hi], in1=minus_half[:, lo:hi], op=ALU.pow
+            )
             factors_of[m]["rstd"] = rstd
+
+        def factors_shift(m):
+            lo, hi = columns(m)
+            shift = small.tile([P, UNIT + 1], F32, tag="shift")
+            nc.gpsimd.tensor_tensor(
+                out=shift[:, lo:hi], in0=factors_of[m]["minus_mean"][:, lo:hi], in1=factors_of[m]["rstd"][:, lo:hi],
+                op=ALU.mult,
+            )
             factors_of[m]["shift"] = shift
 
         def normalise(u):
@@ -350,13 +371,19 @@ def tile_graphmodel_pa_kernel(
             nc.scalar.activation(out=total[:], in_=total[:], func=ACT.Ln)
             nc.scalar.activation(out=total[:], in_=total[:], func=ACT.Exp, scale=-1.0)
 
-        def node_sum(s, chain):
-            message = message_of[2 * s]
-            nc.vector.tensor_tensor(out=message[:], in0=message[:], in1=total_of[2 * s][:], op=ALU.mult)
-            x_new = nodes.tile([P, C], F32, tag="x_new")
-            nc.vector.tensor_tensor(out=x_new[:], in0=message[:], in1=own_part[:, s, :], op=ALU.add)
-            nc.vector.bn_stats(out=stats_tile(chain)[:, UNIT, :, :].rearrange("p h k -> p (h k)"), in_=x_new[:])
-            x_new_of[s] = x_new
+        def node_message(s):
+            nc.vector.tensor_tensor(
+                out=message_of[2 * s][:], in0=message_of[2 * s][:], in1=total_of[2 * s][:], op=ALU.mult
+            )
+
+        def node_sum(s):
+            x_new_of[s] = nodes.tile([P, C], F32, name="x_new%d" % s, tag="x_new")
+            nc.vector.tensor_tensor(out=x_new_of[s][:], in0=message_of[2 * s][:], in1=own_part[:, s, :], op=ALU.add)
+
+        def node_statistics(s, chain):
+            nc.vector.bn_stats(
+                out=stats_tile(chain)[:, UNIT, :, :].rearrange("p h k -> p (h k)"), in_=x_new_of[s][:]
+            )
             node_in_chain[chain] = s
 
         def node_scale(s, chain):
@@ -378,46 +405,61 @@ def tile_graphmodel_pa_kernel(
         def slot_ending(u):
             return u // UNITS_PER_SLOT if live(u) and u % UNITS_PER_SLOT == UNITS_PER_SLOT - 1 else None
 
-        for n in range(-7, UNITS + 20):
+        for n in range(-7, UNITS + 22):
             if live(n):
                 normalise(n)
             if has_chain(n + 1):
                 factors_rstd(n + 1)
+                factors_shift(n + 1)
             if live(n + 3):
                 aggregate(n + 3)
             if live(n - 1):
                 residual(n - 1)
             if slot_ending(n - 1) is not None and slot_ending(n - 1) + 3 < SLOTS:
                 load_edges(slot_ending(n - 1) + 3)
+            if live(n - 2):
+                squash(n - 2)
             if has_chain(n + 2):
                 factors_square(n + 2)
                 factors_mean(n + 2)
-            if live(n - 2):
-                squash(n - 2)
-                exponent(n - 2)
-            if live(n + 4) and (n + 4) % BATCH == 0:
-                quantise_batch((n + 4) // BATCH)
-            if live(n - 3):
-                weigh(n - 3)
-            if slot_ending(n - 5) is not None:
-                node_join(slot_ending(n - 5))
-            if slot_ending(n - 9) is not None:
-                node_sum(slot_ending(n - 9), n + 4)
-            if slot_ending(n - 13) is not None:
-                node_scale(slot_ending(n - 13), n)
             if live(n + 6):
                 regroup(n + 6)
             if live(n + 7):
                 flip(n + 7)
-            for half in range(2):
-                if group_ending(n - 3) is not None:
-                    sum_gates(group_ending(n - 3), half)
-                if group_ending(n - 4) is not None:
-                    sum_messages(group_ending(n - 4), half)
+            if live(n - 2):
+                exponent(n - 2)
+            if slot_ending(n - 9) is not None:
+                node_message(slot_ending(n - 9))
+            if live(n + 4) and (n + 4) % BATCH == 0:
+                quantise_batch((n + 4) // BATCH)
+            if slot_ending(n - 9) is not None:
+                node_sum(slot_ending(n - 9))
+            if live(n - 3):
+                weigh(n - 3)
+            if slot_ending(n - 5) is not None:
+                node_join(slot_ending(n - 5))
+            if slot_ending(n - 13) is not None:
+                node_scale(slot_ending(n - 13), n)
+            if group_ending(n - 3) is not None:
+                sum_gates(group_ending(n - 3), 0)
+            if group_ending(n - 4) is not None:
+                sum_messages(group_ending(n - 4), 0)
+            if has_chain(n + 2):
+                factors_minus_mean(n + 2)
             if live(n + 3):
-                statistics(n + 3)
+                statistics(n + 3, 0)
+            if has_chain(n + 2):
+                factors_minus_square(n + 2)
+            if live(n + 3):
+                statistics(n + 3, 1)
+            if slot_ending(n - 9) is not None:
+                node_statistics(slot_ending(n - 9), n + 4)
             if has_chain(n + 2):
                 factors_spread(n + 2)
+            if group_ending(n - 3) is not None:
+                sum_gates(group_ending(n - 3), 1)
+            if group_ending(n - 4) is not None:
+                sum_messages(group_ending(n - 4), 1)
             if slot_ending(n - 6) is not None:
                 node_invert(slot_ending(n - 6))
             if slot_ending(n - 14) is not None:

@@ -53,7 +53,7 @@ def tile_graphmodel_pa_kernel(
         normed = ctx.enter_context(tc.tile_pool(name="normed", bufs=4))
         gates = ctx.enter_context(tc.tile_pool(name="gates", bufs=2))
         gated = ctx.enter_context(tc.tile_pool(name="gated", bufs=2))
-        sums = ctx.enter_context(tc.tile_pool(name="sums", bufs=4))
+        sums = ctx.enter_context(tc.tile_pool(name="sums", bufs=2))
         nodes = ctx.enter_context(tc.tile_pool(name="nodes", bufs=2))
         small = ctx.enter_context(tc.tile_pool(name="small", bufs=6))
         psum_flip = ctx.enter_context(tc.psum_pool(name="psum_flip", bufs=1))
@@ -96,7 +96,7 @@ def tile_graphmodel_pa_kernel(
             )
 
         load_edges(0)
-        for w in ("V", "U", "A", "B", "E"):
+        for w in ("V", "A", "B", "E", "U"):
             load_weight(w)
         load_edges(1)
 
@@ -168,38 +168,31 @@ def tile_graphmodel_pa_kernel(
 
         message_source = keep.tile([P, NODES // 2, C, 2], F32)
 
-        half = C // 2
-        for a in range(NODES // 2):
-            for first in range(0, C, half):
-                both = psum_acc.tile([P, 2, half], F32, tag="acc")
-                for t in range(2):
-                    multiply(both[:, t, :], all_codes, all_planes, 2 * a + t, "V", True, True,
-                             cols=slice(first, first + half))
-                if first == 0:
-                    nc.scalar.mul(
-                        out=message_source[:, a, first : first + half, :], in_=both[:].rearrange("p t c -> p c t"),
-                        mul=1.0 / NODES,
-                    )
-                else:
-                    nc.vector.tensor_scalar(
-                        out=message_source[:, a, first : first + half, :], in0=both[:].rearrange("p t c -> p c t"),
-                        scalar1=1.0 / NODES, scalar2=None, op0=ALU.mult,
-                    )
-        own_part = keep.tile([P, SLOTS, C], F32)
-        for s in range(SLOTS):
-            product = psum_acc.tile([P, C], F32, tag="acc")
-            multiply(product[:], own_codes, own_planes, s, "U", True, True)
-            if s % 2 == 0:
-                nc.scalar.copy(out=own_part[:, s, :], in_=product[:])
-            else:
-                nc.vector.tensor_copy(out=own_part[:, s, :], in_=product[:])
+        def message_sources():
+            half = C // 2
+            for a in range(NODES // 2):
+                for first in range(0, C, half) if not on_vector(a) else ():
+                    both = psum_acc.tile([P, 2, half], F32, tag="acc")
+                    for t in range(2):
+                        multiply(both[:, t, :], all_codes, all_planes, 2 * a + t, "V", True, True,
+                                 cols=slice(first, first + half))
+                    if first == 0:
+                        nc.scalar.mul(
+                            out=message_source[:, a, first : first + half, :], in_=both[:].rearrange("p t c -> p c t"),
+                            mul=1.0 / NODES,
+                        )
+                    else:
+                        nc.vector.tensor_scalar(
+                            out=message_source[:, a, first : first + half, :], in0=both[:].rearrange("p t c -> p c t"),
+                            scalar1=1.0 / NODES, scalar2=None, op0=ALU.mult,
+                        )
 
         def live(u):
             return 0 <= u < UNITS
 
         grouped_of, codes_of, planes_of, flipped_of = {}, {}, {}, {}
         acc_of, stats_of, factors_of, result_of, gate_of, weighted_of = {}, {}, {}, {}, {}, {}
-        total_of, message_of, x_new_of = {}, {}, {}
+        parts_of, joined_of, x_new_of = {}, {}, {}
 
         def flip(u):
             s, a = u // UNITS_PER_SLOT, u % UNITS_PER_SLOT
@@ -298,10 +291,11 @@ def tile_graphmodel_pa_kernel(
         def factors_shift(m):
             lo, hi = columns(m)
             shift = small.tile([P, UNIT + 1], F32, tag="shift")
-            nc.gpsimd.tensor_tensor(
-                out=shift[:, lo:hi], in0=factors_of[m]["minus_mean"][:, lo:hi], in1=factors_of[m]["rstd"][:, lo:hi],
-                op=ALU.mult,
-            )
+            for k in range(lo, hi):
+                nc.scalar.activation(
+                    out=shift[:, k : k + 1], in_=factors_of[m]["minus_mean"][:, k : k + 1], func=ACT.Copy,
+                    scale=factors_of[m]["rstd"][:, k : k + 1],
+                )
             factors_of[m]["shift"] = shift
 
         def normalise(u):
@@ -332,16 +326,26 @@ def tile_graphmodel_pa_kernel(
             nc.scalar.activation(out=gate_of[g][:, k, :, :], in_=gate_of[g][:, k, :, :], func=ACT.Exp, scale=0.5)
 
         def on_vector(u):
-            return u % 3 == 2
+            return u % GROUP == GROUP - 1
 
         def weigh(u):
             g, k = u // GROUP, u % GROUP
             if k == 0:
                 weighted_of[g] = gated.tile([P, GROUP, C, UNIT], F32, name="weighted%d" % g, tag="weighted")
-            engine = nc.vector if on_vector(u) else nc.gpsimd
-            engine.tensor_tensor(
+            nc.gpsimd.tensor_tensor(
                 out=weighted_of[g][:, k, :, :], in0=gate_of[g][:, k, :, :],
                 in1=message_source[:, u % UNITS_PER_SLOT, :, :], op=ALU.mult,
+            )
+
+        def weigh_from_psum(u, half):
+            g, k = u // GROUP, u % GROUP
+            cols = slice(half * C // 2, (half + 1) * C // 2)
+            source = psum_mean.tile([P, UNIT, C // 2], F32, tag="means")
+            for t in range(UNIT):
+                multiply(source[:, t, :], all_codes, all_planes, UNIT * (u % UNITS_PER_SLOT) + t, "V", True, True, cols=cols)
+            nc.vector.scalar_tensor_tensor(
+                out=weighted_of[g][:, k, cols, :], in0=source[:].rearrange("p t c -> p c t"), scalar=1.0 / NODES,
+                in1=gate_of[g][:, k, cols, :], op0=ALU.mult, op1=ALU.mult,
             )
 
         def sum_over_senders(source, out, half):
@@ -351,34 +355,35 @@ def tile_graphmodel_pa_kernel(
             )
 
         def sum_gates(g, half):
-            if half == 0:
-                total_of[g] = sums.tile([P, C], F32, name="total%d" % g, tag="total")
-            sum_over_senders(gate_of[g], total_of[g], half)
+            if g % 2 == 0 and half == 0:
+                parts_of[g // 2] = sums.tile([P, 2, 2, C], F32, name="parts%d" % (g // 2), tag="parts")
+            sum_over_senders(gate_of[g], parts_of[g // 2][:, 0, g % 2, :], half)
 
         def sum_messages(g, half):
-            if half == 0:
-                message_of[g] = sums.tile([P, C], F32, name="message%d" % g, tag="message")
-            sum_over_senders(weighted_of[g], message_of[g], half)
+            sum_over_senders(weighted_of[g], parts_of[g // 2][:, 1, g % 2, :], half)
 
-        def node_join(s):
-            nc.vector.tensor_tensor(out=total_of[2 * s][:], in0=total_of[2 * s][:], in1=total_of[2 * s + 1][:], op=ALU.add)
-            nc.vector.tensor_tensor(
-                out=message_of[2 * s][:], in0=message_of[2 * s][:], in1=message_of[2 * s + 1][:], op=ALU.add
+        def node_join(s, k):
+            if k == 0:
+                joined_of[s] = nodes.tile([P, 2, C], F32, name="joined%d" % s, tag="joined")
+            nc.vector.tensor_reduce(
+                out=joined_of[s][:, k, :], in_=parts_of[s][:, k, :, :].rearrange("p g c -> p c g"), axis=AXIS.X, op=ALU.add
             )
 
         def node_invert(s):
-            total = total_of[2 * s]
-            nc.scalar.activation(out=total[:], in_=total[:], func=ACT.Ln)
-            nc.scalar.activation(out=total[:], in_=total[:], func=ACT.Exp, scale=-1.0)
+            total = joined_of[s][:, 0, :]
+            nc.scalar.activation(out=total, in_=total, func=ACT.Ln)
+            nc.scalar.activation(out=total, in_=total, func=ACT.Exp, scale=-1.0)
 
         def node_message(s):
             nc.vector.tensor_tensor(
-                out=message_of[2 * s][:], in0=message_of[2 * s][:], in1=total_of[2 * s][:], op=ALU.mult
+                out=joined_of[s][:, 1, :], in0=joined_of[s][:, 1, :], in1=joined_of[s][:, 0, :], op=ALU.mult
             )
 
         def node_sum(s):
+            own = psum_flip.tile([P, C], F32, tag="flipped")
+            multiply(own[:], own_codes, own_planes, s, "U", True, True)
             x_new_of[s] = nodes.tile([P, C], F32, name="x_new%d" % s, tag="x_new")
-            nc.vector.tensor_tensor(out=x_new_of[s][:], in0=message_of[2 * s][:], in1=own_part[:, s, :], op=ALU.add)
+            nc.vector.tensor_tensor(out=x_new_of[s][:], in0=joined_of[s][:, 1, :], in1=own[:], op=ALU.add)
 
         def node_statistics(s, chain):
             nc.vector.bn_stats(
@@ -405,62 +410,64 @@ def tile_graphmodel_pa_kernel(
         def slot_ending(u):
             return u // UNITS_PER_SLOT if live(u) and u % UNITS_PER_SLOT == UNITS_PER_SLOT - 1 else None
 
-        for n in range(-7, UNITS + 22):
+        for n in range(-7, UNITS + 20):
+            if has_chain(n):
+                factors_shift(n)
             if live(n):
                 normalise(n)
             if has_chain(n + 1):
                 factors_rstd(n + 1)
-                factors_shift(n + 1)
             if live(n + 3):
                 aggregate(n + 3)
+            if live(n):
+                residual(n)
+            if slot_ending(n) is not None and slot_ending(n) + 3 < SLOTS:
+                load_edges(slot_ending(n) + 3)
             if live(n - 1):
-                residual(n - 1)
-            if slot_ending(n - 1) is not None and slot_ending(n - 1) + 3 < SLOTS:
-                load_edges(slot_ending(n - 1) + 3)
-            if live(n - 2):
-                squash(n - 2)
+                squash(n - 1)
             if has_chain(n + 2):
                 factors_square(n + 2)
                 factors_mean(n + 2)
             if live(n + 6):
                 regroup(n + 6)
-            if live(n + 7):
-                flip(n + 7)
-            if live(n - 2):
-                exponent(n - 2)
-            if slot_ending(n - 9) is not None:
-                node_message(slot_ending(n - 9))
+            if live(n - 1):
+                exponent(n - 1)
+            if slot_ending(n - 7) is not None:
+                node_message(slot_ending(n - 7))
             if live(n + 4) and (n + 4) % BATCH == 0:
                 quantise_batch((n + 4) // BATCH)
-            if slot_ending(n - 9) is not None:
-                node_sum(slot_ending(n - 9))
-            if live(n - 3):
-                weigh(n - 3)
-            if slot_ending(n - 5) is not None:
-                node_join(slot_ending(n - 5))
-            if slot_ending(n - 13) is not None:
-                node_scale(slot_ending(n - 13), n)
-            if group_ending(n - 3) is not None:
-                sum_gates(group_ending(n - 3), 0)
-            if group_ending(n - 4) is not None:
-                sum_messages(group_ending(n - 4), 0)
-            if has_chain(n + 2):
-                factors_minus_mean(n + 2)
+            if live(n - 2) and not on_vector(n - 2):
+                weigh(n - 2)
+            if slot_ending(n - 11) is not None:
+                node_scale(slot_ending(n - 11), n)
+            if slot_ending(n - 7) is not None:
+                node_sum(slot_ending(n - 7))
+            if live(n + 7):
+                flip(n + 7)
             if live(n + 3):
                 statistics(n + 3, 0)
-            if has_chain(n + 2):
-                factors_minus_square(n + 2)
-            if live(n + 3):
                 statistics(n + 3, 1)
-            if slot_ending(n - 9) is not None:
-                node_statistics(slot_ending(n - 9), n + 4)
+            if slot_ending(n - 7) is not None:
+                node_statistics(slot_ending(n - 7), n + 4)
+            if group_ending(n - 3) is not None:
+                sum_messages(group_ending(n - 3), 0)
             if has_chain(n + 2):
+                factors_minus_mean(n + 2)
+                factors_minus_square(n + 2)
                 factors_spread(n + 2)
             if group_ending(n - 3) is not None:
-                sum_gates(group_ending(n - 3), 1)
-            if group_ending(n - 4) is not None:
-                sum_messages(group_ending(n - 4), 1)
-            if slot_ending(n - 6) is not None:
-                node_invert(slot_ending(n - 6))
-            if slot_ending(n - 14) is not None:
-                node_finish(slot_ending(n - 14), n - 1)
+                sum_messages(group_ending(n - 3), 1)
+            if slot_ending(n - 3) is not None:
+                node_join(slot_ending(n - 3), 1)
+            for half in range(2):
+                if group_ending(n - 2) is not None:
+                    sum_gates(group_ending(n - 2), half)
+                    weigh_from_psum(n - 2, half)
+            if slot_ending(n - 2) is not None:
+                node_join(slot_ending(n - 2), 0)
+            if slot_ending(n - 5) is not None:
+                node_invert(slot_ending(n - 5))
+            if slot_ending(n - 12) is not None:
+                node_finish(slot_ending(n - 12), n - 1)
+            if n == -4:
+                message_sources()

@@ -20,9 +20,11 @@ SLOTS = NODES // 2
 UNIT = 2
 UNITS = SLOTS * NODES // UNIT
 UNITS_PER_SLOT = NODES // UNIT
-GROUP = 3
-GROUPS = UNITS // GROUP
-AHEAD = 3
+AHEAD = 2
+CHUNKS = C // P
+HALF_COUNT = C // 2
+HALF_ROOT = 16.0
+assert HALF_ROOT * HALF_ROOT == HALF_COUNT
 BATCH = 2
 BN_EPS = 1e-5
 WEIGHT_NAMES = ("A", "B", "E", "U", "V")
@@ -51,14 +53,14 @@ def tile_graphmodel_pa_kernel(
         early = ctx.enter_context(tc.tile_pool(name="early", bufs=2))
         stage = ctx.enter_context(tc.tile_pool(name="stage", bufs=2))
         normed = ctx.enter_context(tc.tile_pool(name="normed", bufs=4))
-        gates = ctx.enter_context(tc.tile_pool(name="gates", bufs=2))
+        gates = ctx.enter_context(tc.tile_pool(name="gates", bufs=3))
         gated = ctx.enter_context(tc.tile_pool(name="gated", bufs=2))
-        sums = ctx.enter_context(tc.tile_pool(name="sums", bufs=2))
         nodes = ctx.enter_context(tc.tile_pool(name="nodes", bufs=2))
         small = ctx.enter_context(tc.tile_pool(name="small", bufs=6))
         psum_flip = ctx.enter_context(tc.psum_pool(name="psum_flip", bufs=1))
         psum_acc = ctx.enter_context(tc.psum_pool(name="psum_acc", bufs=AHEAD * UNIT))
-        psum_mean = ctx.enter_context(tc.psum_pool(name="psum_mean", bufs=1))
+        psum_misc = ctx.enter_context(tc.psum_pool(name="psum_misc", bufs=1))
+        psum_sum = ctx.enter_context(tc.psum_pool(name="psum_sum", bufs=1))
         ctx.enter_context(tc.manual_schedule())
 
         ident = keep.tile([P, P], F32)
@@ -104,14 +106,10 @@ def tile_graphmodel_pa_kernel(
         nc.vector.tensor_reduce(
             out=own_parity[:], in_=ident[:].rearrange("p (a t) -> p t a", t=2), axis=AXIS.X, op=ALU.add
         )
-        parity = keep.tile([P, P // 2, 2], F32)
+        neg_parity = keep.tile([P, P // 2, 2], F32)
         nc.vector.tensor_scalar(
-            out=parity[:], in0=own_parity[:].unsqueeze(1).to_broadcast([P, P // 2, 2]),
-            scalar1=1.0 / P, scalar2=None, op0=ALU.mult,
-        )
-        parity_over_n = keep.tile([P, P], F32)
-        nc.vector.tensor_scalar(
-            out=parity_over_n[:], in0=parity[:].rearrange("p a t -> p (a t)"), scalar1=2.0 / C, scalar2=None, op0=ALU.mult
+            out=neg_parity[:], in0=own_parity[:].unsqueeze(1).to_broadcast([P, P // 2, 2]),
+            scalar1=-1.0 / (P * HALF_COUNT), scalar2=None, op0=ALU.mult,
         )
         minus_half = keep.tile([P, UNIT + 1], F32)
         nc.vector.memset(minus_half[:], -0.5)
@@ -166,33 +164,26 @@ def tile_graphmodel_pa_kernel(
 
         load_edges(2)
 
-        message_source = keep.tile([P, NODES // 2, C, 2], F32)
+        message_source = keep.tile([P, NODES, C], F32)
+        own_update = keep.tile([P, SLOTS, C], F32)
 
-        def message_sources():
-            half = C // 2
-            for a in range(NODES // 2):
-                for first in range(0, C, half) if not on_vector(a) else ():
-                    both = psum_acc.tile([P, 2, half], F32, tag="acc")
-                    for t in range(2):
-                        multiply(both[:, t, :], all_codes, all_planes, 2 * a + t, "V", True, True,
-                                 cols=slice(first, first + half))
-                    if first == 0:
-                        nc.scalar.mul(
-                            out=message_source[:, a, first : first + half, :], in_=both[:].rearrange("p t c -> p c t"),
-                            mul=1.0 / NODES,
-                        )
-                    else:
-                        nc.vector.tensor_scalar(
-                            out=message_source[:, a, first : first + half, :], in0=both[:].rearrange("p t c -> p c t"),
-                            scalar1=1.0 / NODES, scalar2=None, op0=ALU.mult,
-                        )
+        def node_products():
+            jobs = [(all_codes, all_planes, j, "V", message_source[:, j, :], 1.0 / NODES) for j in range(NODES)]
+            jobs += [(own_codes, own_planes, s, "U", own_update[:, s, :], 1.0) for s in range(SLOTS)]
+            for k, (codes, planes, index, w, out, factor) in enumerate(jobs):
+                product = psum_acc.tile([P, C], F32, tag="acc")
+                multiply(product[:], codes, planes, index, w, True, True)
+                if k % 2 == 0:
+                    nc.scalar.mul(out=out, in_=product[:], mul=factor)
+                else:
+                    nc.vector.tensor_scalar(out=out, in0=product[:], scalar1=factor, scalar2=None, op0=ALU.mult)
 
         def live(u):
             return 0 <= u < UNITS
 
         grouped_of, codes_of, planes_of, flipped_of = {}, {}, {}, {}
         acc_of, stats_of, factors_of, result_of, gate_of, weighted_of = {}, {}, {}, {}, {}, {}
-        parts_of, joined_of, x_new_of = {}, {}, {}
+        turned_of, x_new_of = {}, {}
 
         def flip(u):
             s, a = u // UNITS_PER_SLOT, u % UNITS_PER_SLOT
@@ -238,236 +229,172 @@ def tile_graphmodel_pa_kernel(
 
         def factors_square(m):
             lo, hi = columns(m)
-            nc.scalar.activation(out=stats_of[m][:, lo:hi, :, 0], in_=stats_of[m][:, lo:hi, :, 1], func=ACT.Square)
+            nc.scalar.activation(
+                out=stats_of[m][:, lo:hi, :, 0], in_=stats_of[m][:, lo:hi, :, 1], func=ACT.Square, scale=HALF_ROOT
+            )
 
         def factors_mean(m):
             lo, hi = columns(m)
-            means = psum_mean.tile([P, hi - lo, 2], F32, tag="means")
-            for half in range(2):
-                nc.tensor.matmul(
-                    out=means[:], lhsT=parity[:].rearrange("p a t -> p (a t)"), rhs=stats_of[m][:, lo:hi, half, 0:2],
-                    start=(half == 0), stop=False,
-                )
-            for half in range(2):
-                nc.tensor.matmul(
-                    out=means[:, :, 0], lhsT=parity_over_n[:], rhs=stats_of[m][:, lo:hi, half, 2],
-                    start=False, stop=(half == 1),
-                )
+            means = psum_misc.tile([P, hi - lo, 2, 3], F32, tag="misc")
+            nc.tensor.matmul(
+                out=means[:].rearrange("p c h k -> p (c h k)"), lhsT=neg_parity[:].rearrange("p a t -> p (a t)"),
+                rhs=stats_of[m][:, lo:hi, :, :].rearrange("p c h k -> p (c h k)"), start=True, stop=True,
+            )
             factors_of[m] = {"means": means}
 
-        def factors_minus_mean(m):
+        def factors_join(m):
             lo, hi = columns(m)
-            minus_mean = small.tile([P, UNIT + 1], F32, tag="minus_mean")
-            nc.vector.tensor_scalar(
-                out=minus_mean[:, lo:hi], in0=factors_of[m]["means"][:, :, 1], scalar1=-1.0, scalar2=None, op0=ALU.mult
+            joined = small.tile([P, UNIT + 1, 3], F32, tag="joined")
+            nc.vector.tensor_reduce(
+                out=joined[:, lo:hi, :], in_=factors_of[m]["means"][:].rearrange("p c h k -> p c k h"), axis=AXIS.X, op=ALU.add
             )
-            factors_of[m]["minus_mean"] = minus_mean
-
-        def factors_minus_square(m):
-            lo, hi = columns(m)
-            spread = small.tile([P, UNIT + 1], F32, tag="spread")
-            nc.vector.tensor_tensor(
-                out=spread[:, lo:hi], in0=factors_of[m]["means"][:, :, 1], in1=factors_of[m]["minus_mean"][:, lo:hi],
-                op=ALU.mult,
-            )
-            factors_of[m]["spread"] = spread
-
-        def factors_spread(m):
-            lo, hi = columns(m)
-            spread = factors_of[m]["spread"]
-            nc.vector.scalar_tensor_tensor(
-                out=spread[:, lo:hi], in0=factors_of[m]["means"][:, :, 0], scalar=BN_EPS, in1=spread[:, lo:hi],
-                op0=ALU.add, op1=ALU.add,
-            )
+            factors_of[m]["joined"] = joined
 
         def factors_rstd(m):
             lo, hi = columns(m)
-            rstd = small.tile([P, UNIT + 1], F32, tag="rstd")
-            nc.gpsimd.tensor_tensor(
-                out=rstd[:, lo:hi], in0=factors_of[m]["spread"][:, lo:hi], in1=minus_half[:, lo:hi], op=ALU.pow
+            joined = factors_of[m]["joined"]
+            n2 = float(HALF_COUNT * HALF_COUNT)
+            square = small.tile([P, UNIT + 1], F32, tag="square")
+            nc.gpsimd.tensor_tensor(out=square[:, lo:hi], in0=joined[:, lo:hi, 1], in1=joined[:, lo:hi, 1], op=ALU.mult)
+            second = small.tile([P, UNIT + 1], F32, tag="second")
+            nc.gpsimd.tensor_tensor(out=second[:, lo:hi], in0=joined[:, lo:hi, 0], in1=joined[:, lo:hi, 2], op=ALU.add)
+            nc.gpsimd.tensor_scalar(
+                out=second[:, lo:hi], in0=second[:, lo:hi], scalar1=-1.0 / n2, scalar2=BN_EPS / n2, op0=ALU.mult, op1=ALU.add
             )
-            factors_of[m]["rstd"] = rstd
-
-        def factors_shift(m):
-            lo, hi = columns(m)
-            shift = small.tile([P, UNIT + 1], F32, tag="shift")
-            for k in range(lo, hi):
-                nc.scalar.activation(
-                    out=shift[:, k : k + 1], in_=factors_of[m]["minus_mean"][:, k : k + 1], func=ACT.Copy,
-                    scale=factors_of[m]["rstd"][:, k : k + 1],
+            nc.gpsimd.tensor_tensor(out=second[:, lo:hi], in0=second[:, lo:hi], in1=square[:, lo:hi], op=ALU.subtract)
+            slope = small.tile([P, UNIT + 1], F32, tag="slope")
+            nc.gpsimd.tensor_tensor(out=slope[:, lo:hi], in0=second[:, lo:hi], in1=minus_half[:, lo:hi], op=ALU.pow)
+            factors_of[m]["slope"] = slope
+            if m in node_in_chain:
+                last = small.tile([P, 2], F32, tag="last")
+                nc.gpsimd.tensor_scalar(
+                    out=last[:, 0:1], in0=slope[:, UNIT : UNIT + 1], scalar1=1.0 / HALF_COUNT, scalar2=0.0, op0=ALU.mult, op1=ALU.add
                 )
-            factors_of[m]["shift"] = shift
+                nc.gpsimd.tensor_tensor(out=last[:, 1:2], in0=slope[:, UNIT : UNIT + 1], in1=joined[:, UNIT, 1:2], op=ALU.mult)
+                factors_of[m]["last"] = last
 
         def normalise(u):
             result_of[u] = normed.tile([P, UNIT, C], F32, name="result%d" % u, tag="result")
             for i in range(UNIT):
                 nc.scalar.activation(
                     out=result_of[u][:, i, :], in_=acc_of[(u, i)][:], func=ACT.Relu,
-                    bias=factors_of[u]["shift"][:, i : i + 1], scale=factors_of[u]["rstd"][:, i : i + 1],
+                    bias=factors_of[u]["joined"][:, i, 1:2], scale=1.0 / HALF_COUNT,
                 )
 
         def residual(u):
             s, a = u // UNITS_PER_SLOT, u % UNITS_PER_SLOT
-            nc.gpsimd.tensor_tensor(
-                out=result_of[u][:], in0=result_of[u][:], in1=edge_in[s][:, UNIT * a : UNIT * (a + 1), :], op=ALU.add
-            )
+            for i in range(UNIT):
+                nc.vector.scalar_tensor_tensor(
+                    out=result_of[u][:, i, :], in0=result_of[u][:, i, :], scalar=factors_of[u]["slope"][:, i : i + 1],
+                    in1=edge_in[s][:, UNIT * a + i, :], op0=ALU.mult, op1=ALU.add,
+                )
             nc.sync.dma_start(out=edge_out_rows[:, UNIT * u : UNIT * (u + 1), :], in_=result_of[u][:])
 
         def squash(u):
-            g, k = u // GROUP, u % GROUP
-            if k == 0:
-                gate_of[g] = gates.tile([P, GROUP, C, UNIT], F32, name="gate%d" % g, tag="gate")
-            nc.scalar.activation(
-                out=gate_of[g][:, k, :, :], in_=result_of[u][:].rearrange("p t c -> p c t"), func=ACT.Tanh, scale=0.5
-            )
+            gate_of[u] = gates.tile([P, UNIT, C], F32, name="gate%d" % u, tag="gate")
+            nc.scalar.activation(out=gate_of[u][:], in_=result_of[u][:], func=ACT.Tanh, scale=0.5)
 
         def exponent(u):
-            g, k = u // GROUP, u % GROUP
-            nc.scalar.activation(out=gate_of[g][:, k, :, :], in_=gate_of[g][:, k, :, :], func=ACT.Exp, scale=0.5)
-
-        def on_vector(u):
-            return u % GROUP == GROUP - 1
+            nc.scalar.activation(out=gate_of[u][:], in_=gate_of[u][:], func=ACT.Exp, scale=0.5)
 
         def weigh(u):
-            g, k = u // GROUP, u % GROUP
-            if k == 0:
-                weighted_of[g] = gated.tile([P, GROUP, C, UNIT], F32, name="weighted%d" % g, tag="weighted")
-            nc.gpsimd.tensor_tensor(
-                out=weighted_of[g][:, k, :, :], in0=gate_of[g][:, k, :, :],
-                in1=message_source[:, u % UNITS_PER_SLOT, :, :], op=ALU.mult,
-            )
-
-        def weigh_from_psum(u, half):
-            g, k = u // GROUP, u % GROUP
-            cols = slice(half * C // 2, (half + 1) * C // 2)
-            source = psum_mean.tile([P, UNIT, C // 2], F32, tag="means")
-            for t in range(UNIT):
-                multiply(source[:, t, :], all_codes, all_planes, UNIT * (u % UNITS_PER_SLOT) + t, "V", True, True, cols=cols)
-            nc.vector.scalar_tensor_tensor(
-                out=weighted_of[g][:, k, cols, :], in0=source[:].rearrange("p t c -> p c t"), scalar=1.0 / NODES,
-                in1=gate_of[g][:, k, cols, :], op0=ALU.mult, op1=ALU.mult,
-            )
-
-        def sum_over_senders(source, out, half):
-            cols = slice(half * C // 2, (half + 1) * C // 2)
-            nc.vector.tensor_reduce(
-                out=out[:, cols], in_=source[:, :, cols, :].rearrange("p a c t -> p c a t"), axis=AXIS.XY, op=ALU.add
-            )
-
-        def sum_gates(g, half):
-            if g % 2 == 0 and half == 0:
-                parts_of[g // 2] = sums.tile([P, 2, 2, C], F32, name="parts%d" % (g // 2), tag="parts")
-            sum_over_senders(gate_of[g], parts_of[g // 2][:, 0, g % 2, :], half)
-
-        def sum_messages(g, half):
-            sum_over_senders(weighted_of[g], parts_of[g // 2][:, 1, g % 2, :], half)
-
-        def node_join(s, k):
-            if k == 0:
-                joined_of[s] = nodes.tile([P, 2, C], F32, name="joined%d" % s, tag="joined")
-            nc.vector.tensor_reduce(
-                out=joined_of[s][:, k, :], in_=parts_of[s][:, k, :, :].rearrange("p g c -> p c g"), axis=AXIS.X, op=ALU.add
-            )
-
-        def node_invert(s):
-            total = joined_of[s][:, 0, :]
-            nc.scalar.activation(out=total, in_=total, func=ACT.Ln)
-            nc.scalar.activation(out=total, in_=total, func=ACT.Exp, scale=-1.0)
-
-        def node_message(s):
+            a = u % UNITS_PER_SLOT
+            weighted_of[u] = gated.tile([P, UNIT, C], F32, name="weighted%d" % u, tag="weighted")
             nc.vector.tensor_tensor(
-                out=joined_of[s][:, 1, :], in0=joined_of[s][:, 1, :], in1=joined_of[s][:, 0, :], op=ALU.mult
+                out=weighted_of[u][:], in0=gate_of[u][:], in1=message_source[:, UNIT * a : UNIT * (a + 1), :], op=ALU.mult
             )
 
-        def node_sum(s):
-            own = psum_flip.tile([P, C], F32, tag="flipped")
-            multiply(own[:], own_codes, own_planes, s, "U", True, True)
+        def add_up(u):
+            s, a = u // UNITS_PER_SLOT, u % UNITS_PER_SLOT
+            if a == 0:
+                turned_of[s] = (
+                    psum_sum.tile([P, CHUNKS, P], F32, name="total%d" % s, tag="total"),
+                    psum_sum.tile([P, CHUNKS, P], F32, name="message%d" % s, tag="message"),
+                )
+            for turned, rows in zip(turned_of[s], (gate_of[u], weighted_of[u])):
+                for i in range(UNIT):
+                    for q in range(CHUNKS):
+                        nc.tensor.matmul(
+                            out=turned[:, q, :], lhsT=rows[:, i, q * P : (q + 1) * P], rhs=ident[:], is_transpose=True,
+                            start=(a == 0 and i == 0 and q == 0),
+                            stop=(a == UNITS_PER_SLOT - 1 and i == UNIT - 1 and q == CHUNKS - 1),
+                        )
+
+        def node_divide(s):
+            total, message = turned_of[s]
+            inverse = nodes.tile([P, CHUNKS, P], F32, tag="inverse")
+            nc.vector.reciprocal(out=inverse[:], in_=total[:])
+            nc.vector.tensor_tensor(out=inverse[:], in0=message[:], in1=inverse[:], op=ALU.mult)
+            turned_of[s] = inverse
+
+        def node_back(s):
+            back = psum_misc.tile([P, CHUNKS, P], F32, tag="misc")
+            for q in range(CHUNKS):
+                nc.tensor.transpose(back[:, q, :], turned_of[s][:, q, :], ident[:])
+            turned_of[s] = back
+
+        def node_sum(s, chain):
             x_new_of[s] = nodes.tile([P, C], F32, name="x_new%d" % s, tag="x_new")
-            nc.vector.tensor_tensor(out=x_new_of[s][:], in0=joined_of[s][:, 1, :], in1=own[:], op=ALU.add)
-
-        def node_statistics(s, chain):
-            nc.vector.bn_stats(
-                out=stats_tile(chain)[:, UNIT, :, :].rearrange("p h k -> p (h k)"), in_=x_new_of[s][:]
+            nc.vector.tensor_tensor(
+                out=x_new_of[s][:], in0=turned_of[s][:].rearrange("p q c -> p (q c)"), in1=own_update[:, s, :], op=ALU.add
             )
+            nc.vector.bn_stats(out=stats_tile(chain)[:, UNIT, :, :].rearrange("p h k -> p (h k)"), in_=x_new_of[s][:])
             node_in_chain[chain] = s
 
         def node_scale(s, chain):
             nc.vector.scalar_tensor_tensor(
-                out=x_new_of[s][:], in0=x_new_of[s][:], scalar=factors_of[chain]["rstd"][:, UNIT : UNIT + 1],
+                out=x_new_of[s][:], in0=x_new_of[s][:], scalar=factors_of[chain]["last"][:, 0:1],
                 in1=x_own[:, s, :], op0=ALU.mult, op1=ALU.add,
             )
 
         def node_finish(s, chain):
             nc.scalar.activation(
-                out=x_new_of[s][:], in_=x_new_of[s][:], func=ACT.Relu,
-                bias=factors_of[chain]["shift"][:, UNIT : UNIT + 1], scale=1.0,
+                out=x_new_of[s][:], in_=x_new_of[s][:], func=ACT.Relu, bias=factors_of[chain]["last"][:, 1:2], scale=1.0
             )
             nc.sync.dma_start(out=x_out_rows[:, s, :], in_=x_new_of[s][:])
-
-        def group_ending(u):
-            return u // GROUP if live(u) and u % GROUP == GROUP - 1 else None
 
         def slot_ending(u):
             return u // UNITS_PER_SLOT if live(u) and u % UNITS_PER_SLOT == UNITS_PER_SLOT - 1 else None
 
-        for n in range(-7, UNITS + 20):
+        node_products()
+        for n in range(-4, UNITS + 9):
+            if has_chain(n - 1):
+                factors_join(n - 1)
+                factors_rstd(n - 1)
+            if live(n - 1):
+                normalise(n - 1)
+            if live(n):
+                aggregate(n)
+            if slot_ending(n - 4) is not None:
+                node_divide(slot_ending(n - 4))
+                node_back(slot_ending(n - 4))
+            if live(n - 3):
+                weigh(n - 3)
+            if live(n + 3):
+                regroup(n + 3)
+            if live(n + 4):
+                flip(n + 4)
+            if live(n - 3):
+                add_up(n - 3)
+            if live(n):
+                statistics(n, 0)
+                statistics(n, 1)
+            if live(n - 2):
+                squash(n - 2)
             if has_chain(n):
-                factors_shift(n)
-            if live(n):
-                normalise(n)
-            if has_chain(n + 1):
-                factors_rstd(n + 1)
-            if live(n + 3):
-                aggregate(n + 3)
-            if live(n):
-                residual(n)
-            if slot_ending(n) is not None and slot_ending(n) + 3 < SLOTS:
-                load_edges(slot_ending(n) + 3)
+                factors_square(n)
+                factors_mean(n)
             if live(n - 1):
-                squash(n - 1)
-            if has_chain(n + 2):
-                factors_square(n + 2)
-                factors_mean(n + 2)
-            if live(n + 6):
-                regroup(n + 6)
-            if live(n - 1):
-                exponent(n - 1)
+                residual(n - 1)
+            if slot_ending(n - 1) is not None and slot_ending(n - 1) + 3 < SLOTS:
+                load_edges(slot_ending(n - 1) + 3)
+            if live(n - 2):
+                exponent(n - 2)
+            if live(n + 2) and (n + 2) % BATCH == 0:
+                quantise_batch((n + 2) // BATCH)
+            if slot_ending(n - 4) is not None:
+                node_sum(slot_ending(n - 4), n + 1)
+            if slot_ending(n - 6) is not None:
+                node_scale(slot_ending(n - 6), n - 1)
             if slot_ending(n - 7) is not None:
-                node_message(slot_ending(n - 7))
-            if live(n + 4) and (n + 4) % BATCH == 0:
-                quantise_batch((n + 4) // BATCH)
-            if live(n - 2) and not on_vector(n - 2):
-                weigh(n - 2)
-            if slot_ending(n - 11) is not None:
-                node_scale(slot_ending(n - 11), n)
-            if slot_ending(n - 7) is not None:
-                node_sum(slot_ending(n - 7))
-            if live(n + 7):
-                flip(n + 7)
-            if live(n + 3):
-                statistics(n + 3, 0)
-                statistics(n + 3, 1)
-            if slot_ending(n - 7) is not None:
-                node_statistics(slot_ending(n - 7), n + 4)
-            if group_ending(n - 3) is not None:
-                sum_messages(group_ending(n - 3), 0)
-            if has_chain(n + 2):
-                factors_minus_mean(n + 2)
-                factors_minus_square(n + 2)
-                factors_spread(n + 2)
-            if group_ending(n - 3) is not None:
-                sum_messages(group_ending(n - 3), 1)
-            if slot_ending(n - 3) is not None:
-                node_join(slot_ending(n - 3), 1)
-            for half in range(2):
-                if group_ending(n - 2) is not None:
-                    sum_gates(group_ending(n - 2), half)
-                    weigh_from_psum(n - 2, half)
-            if slot_ending(n - 2) is not None:
-                node_join(slot_ending(n - 2), 0)
-            if slot_ending(n - 5) is not None:
-                node_invert(slot_ending(n - 5))
-            if slot_ending(n - 12) is not None:
-                node_finish(slot_ending(n - 12), n - 1)
-            if n == -4:
-                message_sources()
+                node_finish(slot_ending(n - 7), n - 2)

@@ -52,7 +52,7 @@ def tile_graphmodel_pa_kernel(
         edges = ctx.enter_context(tc.tile_pool(name="edges", bufs=3))
         early = ctx.enter_context(tc.tile_pool(name="early", bufs=2))
         stage = ctx.enter_context(tc.tile_pool(name="stage", bufs=2))
-        normed = ctx.enter_context(tc.tile_pool(name="normed", bufs=4))
+        normed = ctx.enter_context(tc.tile_pool(name="normed", bufs=5))
         gates = ctx.enter_context(tc.tile_pool(name="gates", bufs=3))
         gated = ctx.enter_context(tc.tile_pool(name="gated", bufs=2))
         nodes = ctx.enter_context(tc.tile_pool(name="nodes", bufs=2))
@@ -113,6 +113,8 @@ def tile_graphmodel_pa_kernel(
         )
         minus_half = keep.tile([P, UNIT + 1], F32)
         nc.vector.memset(minus_half[:], -0.5)
+        minus_one = keep.tile([P, CHUNKS, P], F32)
+        nc.vector.memset(minus_one[:], -1.0)
 
         def transpose_pair(rows, first, pool=psum_flip, tag="flipped"):
             flipped = pool.tile([P, 2, 2, P], F32, tag=tag)
@@ -320,12 +322,18 @@ def tile_graphmodel_pa_kernel(
                             stop=(a == UNITS_PER_SLOT - 1 and i == UNIT - 1 and q == CHUNKS - 1),
                         )
 
-        def node_divide(s):
+        def node_fetch(s):
             total, message = turned_of[s]
-            inverse = nodes.tile([P, CHUNKS, P], F32, tag="inverse")
-            nc.vector.reciprocal(out=inverse[:], in_=total[:])
-            nc.vector.tensor_tensor(out=inverse[:], in0=message[:], in1=inverse[:], op=ALU.mult)
-            turned_of[s] = inverse
+            fetched = nodes.tile([P, 2, CHUNKS, P], F32, tag="fetched")
+            nc.scalar.copy(out=fetched[:, 0, :, :], in_=total[:])
+            nc.scalar.copy(out=fetched[:, 1, :, :], in_=message[:])
+            turned_of[s] = fetched
+
+        def node_divide(s):
+            fetched = turned_of[s]
+            nc.gpsimd.tensor_tensor(out=fetched[:, 0, :, :], in0=fetched[:, 0, :, :], in1=minus_one[:], op=ALU.pow)
+            nc.gpsimd.tensor_tensor(out=fetched[:, 1, :, :], in0=fetched[:, 1, :, :], in1=fetched[:, 0, :, :], op=ALU.mult)
+            turned_of[s] = fetched[:, 1, :, :]
 
         def node_back(s):
             back = psum_misc.tile([P, CHUNKS, P], F32, tag="misc")
@@ -357,7 +365,7 @@ def tile_graphmodel_pa_kernel(
             return u // UNITS_PER_SLOT if live(u) and u % UNITS_PER_SLOT == UNITS_PER_SLOT - 1 else None
 
         node_products()
-        for n in range(-4, UNITS + 9):
+        for n in range(-4, UNITS + 11):
             if has_chain(n - 1):
                 factors_join(n - 1)
                 factors_rstd(n - 1)
@@ -365,36 +373,38 @@ def tile_graphmodel_pa_kernel(
                 normalise(n - 1)
             if live(n):
                 aggregate(n)
-            if slot_ending(n - 4) is not None:
-                node_divide(slot_ending(n - 4))
-                node_back(slot_ending(n - 4))
-            if live(n - 3):
-                weigh(n - 3)
+            if slot_ending(n - 5) is not None:
+                node_fetch(slot_ending(n - 5))
+                node_divide(slot_ending(n - 5))
+            if live(n - 4):
+                weigh(n - 4)
             if live(n + 3):
                 regroup(n + 3)
+            if slot_ending(n - 6) is not None:
+                node_back(slot_ending(n - 6))
             if live(n + 4):
                 flip(n + 4)
-            if live(n - 3):
-                add_up(n - 3)
+            if live(n - 4):
+                add_up(n - 4)
             if live(n):
                 statistics(n, 0)
                 statistics(n, 1)
-            if live(n - 2):
-                squash(n - 2)
+            if live(n - 3):
+                squash(n - 3)
             if has_chain(n):
                 factors_square(n)
                 factors_mean(n)
-            if live(n - 1):
-                residual(n - 1)
-            if slot_ending(n - 1) is not None and slot_ending(n - 1) + 3 < SLOTS:
-                load_edges(slot_ending(n - 1) + 3)
             if live(n - 2):
-                exponent(n - 2)
+                residual(n - 2)
+            if slot_ending(n - 2) is not None and slot_ending(n - 2) + 3 < SLOTS:
+                load_edges(slot_ending(n - 2) + 3)
+            if live(n - 3):
+                exponent(n - 3)
             if live(n + 2) and (n + 2) % BATCH == 0:
                 quantise_batch((n + 2) // BATCH)
-            if slot_ending(n - 4) is not None:
-                node_sum(slot_ending(n - 4), n + 1)
             if slot_ending(n - 6) is not None:
-                node_scale(slot_ending(n - 6), n - 1)
-            if slot_ending(n - 7) is not None:
-                node_finish(slot_ending(n - 7), n - 2)
+                node_sum(slot_ending(n - 6), n + 1)
+            if slot_ending(n - 8) is not None:
+                node_scale(slot_ending(n - 8), n - 1)
+            if slot_ending(n - 9) is not None:
+                node_finish(slot_ending(n - 9), n - 2)

@@ -27,6 +27,8 @@ HALF_ROOT = 16.0
 assert HALF_ROOT * HALF_ROOT == HALF_COUNT
 BATCH = 2
 BN_EPS = 1e-5
+RV_MOD, RV_CNT, RV_FROM = 4, 1, 0
+LOADS_AHEAD = 5
 WEIGHT_NAMES = ("A", "B", "E", "U", "V")
 
 FLOPS = 2 * C * C * (GRAPHS * NODES * NODES + 4 * GRAPHS * NODES)
@@ -49,13 +51,13 @@ def tile_graphmodel_pa_kernel(
 
     with ExitStack() as ctx:
         keep = ctx.enter_context(tc.tile_pool(name="keep", bufs=1))
-        edges = ctx.enter_context(tc.tile_pool(name="edges", bufs=3))
+        edges = ctx.enter_context(tc.tile_pool(name="edges", bufs=9))
         early = ctx.enter_context(tc.tile_pool(name="early", bufs=2))
         stage = ctx.enter_context(tc.tile_pool(name="stage", bufs=2))
         normed = ctx.enter_context(tc.tile_pool(name="normed", bufs=5))
         gates = ctx.enter_context(tc.tile_pool(name="gates", bufs=3))
         gated = ctx.enter_context(tc.tile_pool(name="gated", bufs=2))
-        nodes = ctx.enter_context(tc.tile_pool(name="nodes", bufs=2))
+        nodes = ctx.enter_context(tc.tile_pool(name="nodes", bufs=3))
         small = ctx.enter_context(tc.tile_pool(name="small", bufs=6))
         psum_flip = ctx.enter_context(tc.psum_pool(name="psum_flip", bufs=1))
         psum_acc = ctx.enter_context(tc.psum_pool(name="psum_acc", bufs=AHEAD * UNIT))
@@ -67,16 +69,18 @@ def tile_graphmodel_pa_kernel(
         make_identity(nc, ident[:])
 
         x_own = keep.tile([P, SLOTS, C], BF16)
-        x_all = edges.tile([P, NODES, C], BF16, tag="edge_in")
-        nc.scalar.dma_start(out=x_all[0:P:2, :, :], in_=x)
-        nc.sync.dma_start(out=x_all[1:P:2, :, :], in_=x)
-        nc.scalar.dma_start(out=x_own[:], in_=x_rows)
+        x_all = [keep.tile([P, SLOTS, C], BF16, name="x_all%d" % g) for g in range(2)]
+
+        def load_x_all(g):
+            nc.scalar.dma_start(out=x_all[g][0:P:2, :, :], in_=x[:, g * SLOTS : (g + 1) * SLOTS, :])
+            nc.sync.dma_start(out=x_all[g][1:P:2, :, :], in_=x[:, g * SLOTS : (g + 1) * SLOTS, :])
 
         edge_in = {}
+        WIDE = BATCH * UNIT
 
-        def load_edges(s):
-            edge_in[s] = edges.tile([P, NODES, C], BF16, name="edge_in%d" % s, tag="edge_in")
-            nc.sync.dma_start(out=edge_in[s][:], in_=edge_rows[:, s * NODES : (s + 1) * NODES, :])
+        def load_edges(b):
+            edge_in[b] = edges.tile([P, WIDE, C], BF16, name="edge_in%d" % b, tag="edge_in")
+            nc.sync.dma_start(out=edge_in[b][:], in_=edge_rows[:, b * WIDE : (b + 1) * WIDE, :])
 
         w_words = keep.tile([P, len(WEIGHT_NAMES), C], U32, align_bytes=64)
         w_planes = keep.tile([P, len(WEIGHT_NAMES), C], U8, align_bytes=64)
@@ -88,19 +92,23 @@ def tile_graphmodel_pa_kernel(
             for quadrant in range(4):
                 plane_rows = w_planes[32 * quadrant : 32 * quadrant + 4, k, :]
                 scale_rows = scales[0, 4 * quadrant : 4 * quadrant + 4, :]
-                if quadrant % 2 == 0:
-                    nc.sync.dma_start(out=plane_rows.bitcast(I32), in_=scale_rows.bitcast(I32))
-                else:
-                    nc.gpsimd.dma_start(out=plane_rows.bitcast(F32), in_=scale_rows.bitcast(F32))
+                nc.sync.dma_start(out=plane_rows.bitcast(I32), in_=scale_rows.bitcast(I32))
             nc.sync.dma_start(
                 out=w_words[:, k, :].bitcast(I32),
                 in_=words[0].rearrange("p n t -> p (n t)").bitcast(I32),
             )
 
-        load_edges(0)
-        for w in ("V", "A", "B", "E", "U"):
+        load_x_all(0)
+        nc.scalar.dma_start(out=x_own[:], in_=x_rows)
+        for w in ("A", "B", "E"):
             load_weight(w)
+        load_edges(0)
+        load_weight("V")
         load_edges(1)
+        load_x_all(1)
+        for b in range(2, LOADS_AHEAD):
+            load_edges(b)
+        load_weight("U")
 
         own_parity = keep.tile([P, 2], F32)
         nc.vector.tensor_reduce(
@@ -113,8 +121,9 @@ def tile_graphmodel_pa_kernel(
         )
         minus_half = keep.tile([P, UNIT + 1], F32)
         nc.vector.memset(minus_half[:], -0.5)
-        minus_one = keep.tile([P, CHUNKS, P], F32)
-        nc.vector.memset(minus_one[:], -1.0)
+        warm = keep.tile([P, 1], F32)
+        nc.vector.memset(warm[:], 0.0)
+        nc.scalar.activation(out=warm[:], in_=warm[:], func=ACT.Tanh)
 
         def transpose_pair(rows, first, pool=psum_flip, tag="flipped"):
             flipped = pool.tile([P, 2, 2, P], F32, tag=tag)
@@ -153,32 +162,57 @@ def tile_graphmodel_pa_kernel(
         all_planes = keep.tile([P, NODES * P], U8, align_bytes=64)
         own_codes = keep.tile([P, SLOTS * P], U32, align_bytes=64)
         own_planes = keep.tile([P, SLOTS * P], U8, align_bytes=64)
-        for rows, codes, planes, base in (
-            (x_all, all_codes, all_planes, 0), (x_own, own_codes, own_planes, 0), (x_all, all_codes, all_planes, SLOTS),
-        ):
-            grouped = early.tile([P, SLOTS, P, PACK], BF16, align_bytes=64, tag="grouped_x")
-            for first in range(0, SLOTS, 2):
-                flipped = transpose_pair(rows[:, base : base + SLOTS, :], first, pool=psum_acc, tag="acc")
-                regroup_pair(flipped, grouped, first, engine_copy=nc.vector.tensor_copy if first == 2 else nc.scalar.copy)
-            part = slice(base * P, (base + SLOTS) * P)
-            quantise(grouped, codes[:, part], planes[:, part], 0, 4)
-            quantise(grouped, codes[:, part], planes[:, part], 4, 2)
+        grouped_x = {}
 
-        load_edges(2)
+        def x_pair(g, first, pool, tag, engine_copy):
+            rows = (x_all[0], x_own, x_all[1])[g]
+            if first == 0:
+                grouped_x[g] = early.tile([P, SLOTS, P, PACK], BF16, align_bytes=64, name="grouped_x%d" % g, tag="grouped_x")
+            flipped = transpose_pair(rows, first, pool=pool, tag=tag)
+            regroup_pair(flipped, grouped_x[g], first, engine_copy=engine_copy)
+
+        def x_quantise_pair(g, first):
+            codes, planes, base = ((all_codes, all_planes, 0), (own_codes, own_planes, 0), (all_codes, all_planes, SLOTS))[g]
+            part = slice(base * P, (base + SLOTS) * P)
+            quantise(grouped_x[g], codes[:, part], planes[:, part], first, 2)
+
+        def x_quantise(g):
+            codes, planes, base = ((all_codes, all_planes, 0), (own_codes, own_planes, 0), (all_codes, all_planes, SLOTS))[g]
+            part = slice(base * P, (base + SLOTS) * P)
+            quantise(grouped_x[g], codes[:, part], planes[:, part], 0, 4)
+            quantise(grouped_x[g], codes[:, part], planes[:, part], 4, 2)
+
+        for g in range(2):
+            for first in range(0, SLOTS, 2):
+                x_pair(g, first, psum_acc, "acc", nc.vector.tensor_copy if first == 2 else nc.scalar.copy)
+            x_quantise(g)
 
         message_source = keep.tile([P, NODES, C], F32)
-        own_update = keep.tile([P, SLOTS, C], F32)
+        own_turned = keep.tile([P, SLOTS, CHUNKS, P], F32)
+        sums = keep.tile([P, SLOTS - 1, 2, CHUNKS, P], F32)
 
-        def node_products():
-            jobs = [(all_codes, all_planes, j, "V", message_source[:, j, :], 1.0 / NODES) for j in range(NODES)]
-            jobs += [(own_codes, own_planes, s, "U", own_update[:, s, :], 1.0) for s in range(SLOTS)]
-            for k, (codes, planes, index, w, out, factor) in enumerate(jobs):
-                product = psum_acc.tile([P, C], F32, tag="acc")
-                multiply(product[:], codes, planes, index, w, True, True)
-                if k % 2 == 0:
-                    nc.scalar.mul(out=out, in_=product[:], mul=factor)
-                else:
-                    nc.vector.tensor_scalar(out=out, in0=product[:], scalar1=factor, scalar2=None, op0=ALU.mult)
+        def node_product(w, index, k):
+            if w == "V":
+                product = psum_sum.tile([P, C], F32, name="product%s%d" % (w, index), tag="turned%d" % k)
+            else:
+                product = psum_acc.tile([P, C], F32, name="product%s%d" % (w, index), tag="acc")
+            if w == "V":
+                multiply(product[:], all_codes, all_planes, index, "V", True, True)
+                out, factor = message_source[:, index, :], 1.0 / NODES
+            else:
+                for q in range(CHUNKS):
+                    cols, rows = slice(q * P, (q + 1) * P), slice(index * P, (index + 1) * P)
+                    nc.tensor.matmul_mx(
+                        out=product[:, cols],
+                        lhsT=w_words[:, WEIGHT_NAMES.index("U"), cols].bitcast(FP8X4),
+                        lhsT_scale=w_planes[:, WEIGHT_NAMES.index("U"), cols],
+                        rhs=own_codes[:, rows].bitcast(FP8X4), rhs_scale=own_planes[:, rows], start=True, stop=True,
+                    )
+                out, factor = own_turned[:, index, :, :].rearrange("p q r -> p (q r)"), 1.0
+            if k == 0:
+                nc.scalar.mul(out=out, in_=product[:], mul=factor)
+            else:
+                nc.vector.tensor_scalar(out=out, in0=product[:], scalar1=factor, scalar2=None, op0=ALU.mult)
 
         def live(u):
             return 0 <= u < UNITS
@@ -187,9 +221,11 @@ def tile_graphmodel_pa_kernel(
         acc_of, stats_of, factors_of, result_of, gate_of, weighted_of = {}, {}, {}, {}, {}, {}
         turned_of, x_new_of = {}, {}
 
+        def regroup_on_vector(u):
+            return u % RV_MOD < RV_CNT and u >= RV_FROM
+
         def flip(u):
-            s, a = u // UNITS_PER_SLOT, u % UNITS_PER_SLOT
-            flipped_of[u] = transpose_pair(edge_in[s], UNIT * a)
+            flipped_of[u] = transpose_pair(edge_in[u // BATCH], UNIT * (u % BATCH))
 
         def regroup(u):
             b, k = u // BATCH, u % BATCH
@@ -197,7 +233,7 @@ def tile_graphmodel_pa_kernel(
                 grouped_of[b] = stage.tile(
                     [P, BATCH * UNIT, P, PACK], BF16, align_bytes=64, name="grouped%d" % b, tag="grouped"
                 )
-            regroup_pair(flipped_of[u], grouped_of[b], UNIT * k)
+            regroup_pair(flipped_of[u], grouped_of[b], UNIT * k, engine_copy=nc.vector.tensor_copy if regroup_on_vector(u) else nc.scalar.copy)
 
         def quantise_batch(b):
             codes_of[b] = stage.tile([P, BATCH * UNIT * P], U32, align_bytes=64, name="codes%d" % b, tag="codes")
@@ -209,14 +245,13 @@ def tile_graphmodel_pa_kernel(
                 stats_of[m] = small.tile([P, UNIT + 1, 2, 3], F32, name="stats%d" % m, tag="stats")
             return stats_of[m]
 
-        def aggregate(u):
+        def aggregate(u, i):
             s, a = u // UNITS_PER_SLOT, u % UNITS_PER_SLOT
-            for i in range(UNIT):
-                agg = psum_acc.tile([P, C], F32, name="agg%d_%d" % (u, i), tag="acc")
-                multiply(agg[:], own_codes, own_planes, s, "A", True, False)
-                multiply(agg[:], all_codes, all_planes, UNIT * a + i, "B", False, False)
-                multiply(agg[:], codes_of[u // BATCH], planes_of[u // BATCH], UNIT * (u % BATCH) + i, "E", False, True)
-                acc_of[(u, i)] = agg
+            agg = psum_acc.tile([P, C], F32, name="agg%d_%d" % (u, i), tag="acc")
+            multiply(agg[:], own_codes, own_planes, s, "A", True, False)
+            multiply(agg[:], all_codes, all_planes, UNIT * a + i, "B", False, False)
+            multiply(agg[:], codes_of[u // BATCH], planes_of[u // BATCH], UNIT * (u % BATCH) + i, "E", False, True)
+            acc_of[(u, i)] = agg
 
         def statistics(u, i):
             nc.vector.bn_stats(out=stats_tile(u)[:, i, :, :].rearrange("p h k -> p (h k)"), in_=acc_of[(u, i)][:])
@@ -288,7 +323,7 @@ def tile_graphmodel_pa_kernel(
             for i in range(UNIT):
                 nc.vector.scalar_tensor_tensor(
                     out=result_of[u][:, i, :], in0=result_of[u][:, i, :], scalar=factors_of[u]["slope"][:, i : i + 1],
-                    in1=edge_in[s][:, UNIT * a + i, :], op0=ALU.mult, op1=ALU.add,
+                    in1=edge_in[u // BATCH][:, UNIT * (u % BATCH) + i, :], op0=ALU.mult, op1=ALU.add,
                 )
             nc.sync.dma_start(out=edge_out_rows[:, UNIT * u : UNIT * (u + 1), :], in_=result_of[u][:])
 
@@ -306,105 +341,163 @@ def tile_graphmodel_pa_kernel(
                 out=weighted_of[u][:], in0=gate_of[u][:], in1=message_source[:, UNIT * a : UNIT * (a + 1), :], op=ALU.mult
             )
 
-        def add_up(u):
+        def add_up(u, k):
             s, a = u // UNITS_PER_SLOT, u % UNITS_PER_SLOT
             if a == 0:
-                turned_of[s] = (
-                    psum_sum.tile([P, CHUNKS, P], F32, name="total%d" % s, tag="total"),
-                    psum_sum.tile([P, CHUNKS, P], F32, name="message%d" % s, tag="message"),
-                )
-            for turned, rows in zip(turned_of[s], (gate_of[u], weighted_of[u])):
-                for i in range(UNIT):
-                    for q in range(CHUNKS):
-                        nc.tensor.matmul(
-                            out=turned[:, q, :], lhsT=rows[:, i, q * P : (q + 1) * P], rhs=ident[:], is_transpose=True,
-                            start=(a == 0 and i == 0 and q == 0),
-                            stop=(a == UNITS_PER_SLOT - 1 and i == UNIT - 1 and q == CHUNKS - 1),
-                        )
+                turned_of[(s, k)] = psum_sum.tile([P, CHUNKS, P], F32, name="turned%d_%d" % (s, k), tag="turned%d" % k)
+            turned, rows = turned_of[(s, k)], (gate_of[u], weighted_of[u])[k]
+            for i in range(UNIT):
+                for q in range(CHUNKS):
+                    nc.tensor.matmul(
+                        out=turned[:, q, :], lhsT=rows[:, i, q * P : (q + 1) * P], rhs=ident[:], is_transpose=True,
+                        start=(a == 0 and i == 0 and q == 0),
+                        stop=(a == UNITS_PER_SLOT - 1 and i == UNIT - 1 and q == CHUNKS - 1),
+                    )
 
         def node_fetch(s):
-            total, message = turned_of[s]
-            fetched = nodes.tile([P, 2, CHUNKS, P], F32, tag="fetched")
-            nc.scalar.copy(out=fetched[:, 0, :, :], in_=total[:])
-            nc.scalar.copy(out=fetched[:, 1, :, :], in_=message[:])
-            turned_of[s] = fetched
+            nc.scalar.copy(out=sums[:, s, 0, :, :], in_=turned_of[(s, 0)][:])
+            nc.vector.tensor_copy(out=sums[:, s, 1, :, :], in_=turned_of[(s, 1)][:])
+
+        share_of, last = {}, {}
+
+        def node_invert(s):
+            inverse = nodes.tile([P, CHUNKS, P], F32, name="inverse%d" % s, tag="inverse")
+            total = sums[:, s, 0, :, :] if s < SLOTS - 1 else turned_of[(s, 0)][:]
+            nc.scalar.activation(out=inverse[:], in_=total, func=ACT.Abs_reciprocal_sqrt)
+            nc.scalar.activation(out=inverse[:], in_=inverse[:], func=ACT.Square)
+            share_of[s] = inverse
 
         def node_divide(s):
-            fetched = turned_of[s]
-            nc.gpsimd.tensor_tensor(out=fetched[:, 0, :, :], in0=fetched[:, 0, :, :], in1=minus_one[:], op=ALU.pow)
-            nc.gpsimd.tensor_tensor(out=fetched[:, 1, :, :], in0=fetched[:, 1, :, :], in1=fetched[:, 0, :, :], op=ALU.mult)
-            turned_of[s] = fetched[:, 1, :, :]
+            message = sums[:, s, 1, :, :] if s < SLOTS - 1 else turned_of[(s, 1)][:]
+            nc.vector.tensor_tensor(out=share_of[s][:], in0=message, in1=share_of[s][:], op=ALU.mult)
 
-        def node_back(s):
-            back = psum_misc.tile([P, CHUNKS, P], F32, tag="misc")
-            for q in range(CHUNKS):
-                nc.tensor.transpose(back[:, q, :], turned_of[s][:, q, :], ident[:])
-            turned_of[s] = back
+        def node_sum(s):
+            pool, tag = (((psum_acc, "acc"),) * 4 + ((psum_flip, "flipped"), (psum_sum, "turned0")))[s]
+            x_new_of[s] = pool.tile([P, CHUNKS, P], F32, name="x_new%d" % s, tag=tag)
+            for k, rows in enumerate((share_of[s], own_turned[:, s, :, :])):
+                for q in range(CHUNKS):
+                    nc.tensor.matmul(
+                        out=x_new_of[s][:, q, :], lhsT=rows[:, q, :], rhs=ident[:], is_transpose=True,
+                        start=(k == 0 and q == 0), stop=(k == 1 and q == CHUNKS - 1),
+                    )
 
-        def node_sum(s, chain):
-            x_new_of[s] = nodes.tile([P, C], F32, name="x_new%d" % s, tag="x_new")
-            nc.vector.tensor_tensor(
-                out=x_new_of[s][:], in0=turned_of[s][:].rearrange("p q c -> p (q c)"), in1=own_update[:, s, :], op=ALU.add
+        def node_statistics(s):
+            nc.vector.bn_stats(
+                out=last["stats"][:, s, :, :].rearrange("p h k -> p (h k)"), in_=x_new_of[s][:].rearrange("p q c -> p (q c)")
             )
-            nc.vector.bn_stats(out=stats_tile(chain)[:, UNIT, :, :].rearrange("p h k -> p (h k)"), in_=x_new_of[s][:])
-            node_in_chain[chain] = s
 
-        def node_scale(s, chain):
+        def node_factors():
+            stats, n2 = last["stats"], float(HALF_COUNT * HALF_COUNT)
+            nc.scalar.activation(out=stats[:, :, :, 0], in_=stats[:, :, :, 1], func=ACT.Square, scale=HALF_ROOT)
+            means = psum_misc.tile([P, SLOTS, 2, 3], F32, tag="misc")
+            nc.tensor.matmul(
+                out=means[:].rearrange("p c h k -> p (c h k)"), lhsT=neg_parity[:].rearrange("p a t -> p (a t)"),
+                rhs=stats[:].rearrange("p c h k -> p (c h k)"), start=True, stop=True,
+            )
+            joined = keep.tile([P, SLOTS, 3], F32)
+            nc.vector.tensor_reduce(out=joined[:], in_=means[:].rearrange("p c h k -> p c k h"), axis=AXIS.X, op=ALU.add)
+            work = keep.tile([P, 4, SLOTS], F32)
+            nc.vector.tensor_tensor(out=work[:, 0, :], in0=joined[:, :, 0], in1=joined[:, :, 2], op=ALU.add)
+            nc.vector.tensor_tensor(out=work[:, 1, :], in0=joined[:, :, 1], in1=joined[:, :, 1], op=ALU.mult)
+            nc.vector.tensor_scalar(
+                out=work[:, 0, :], in0=work[:, 0, :], scalar1=-1.0 / n2, scalar2=BN_EPS / n2, op0=ALU.mult, op1=ALU.add
+            )
+            nc.vector.tensor_tensor(out=work[:, 0, :], in0=work[:, 0, :], in1=work[:, 1, :], op=ALU.subtract)
+            nc.scalar.activation(out=work[:, 2, :], in_=work[:, 0, :], func=ACT.Abs_reciprocal_sqrt, scale=n2)
             nc.vector.scalar_tensor_tensor(
-                out=x_new_of[s][:], in0=x_new_of[s][:], scalar=factors_of[chain]["last"][:, 0:1],
+                out=work[:, 3, :], in0=joined[:, :, 1], scalar=float(HALF_COUNT), in1=work[:, 2, :], op0=ALU.mult, op1=ALU.mult
+            )
+            last["rstd"], last["shift"] = work[:, 2, :], work[:, 3, :]
+
+        def node_scale(s):
+            last[s] = nodes.tile([P, C], F32, name="x_out%d" % s, tag="x_out")
+            nc.vector.scalar_tensor_tensor(
+                out=last[s][:], in0=x_new_of[s][:].rearrange("p q c -> p (q c)"), scalar=last["rstd"][:, s : s + 1],
                 in1=x_own[:, s, :], op0=ALU.mult, op1=ALU.add,
             )
 
-        def node_finish(s, chain):
-            nc.scalar.activation(
-                out=x_new_of[s][:], in_=x_new_of[s][:], func=ACT.Relu, bias=factors_of[chain]["last"][:, 1:2], scale=1.0
-            )
-            nc.sync.dma_start(out=x_out_rows[:, s, :], in_=x_new_of[s][:])
+        def node_finish(s):
+            nc.scalar.activation(out=last[s][:], in_=last[s][:], func=ACT.Relu, bias=last["shift"][:, s : s + 1], scale=1.0)
+            nc.sync.dma_start(out=x_out_rows[:, s, :], in_=last[s][:])
 
         def slot_ending(u):
             return u // UNITS_PER_SLOT if live(u) and u % UNITS_PER_SLOT == UNITS_PER_SLOT - 1 else None
 
-        node_products()
-        for n in range(-4, UNITS + 11):
+        extras = {
+            -1: [("V", 0), ("V", 1), ("V", 2), ("V", 3)],
+            0: [("X", 0), ("V", 4), ("V", 5)], 1: [("X", 2), ("V", 6), ("V", 7)], 2: [("X", 4), ("V", 8), ("V", 9)],
+            3: [("V", 10), ("V", 11)],
+            UNITS + 1: [("U", 0), ("U", 1)], UNITS + 2: [("U", 2), ("U", 3)], UNITS + 3: [("U", 4), ("U", 5)],
+        }
+        used = {"count": 0}
+
+        def extra(n, place):
+            todo = extras.get(n, [])
+            for kind, index in todo[place : place + 1] if place < 2 else todo[2:]:
+                k = used["count"] % 2
+                used["count"] += 1
+                if kind == "X":
+                    x_pair(2, index, psum_sum, "turned%d" % k, nc.vector.tensor_copy)
+                    x_quantise_pair(2, index)
+                else:
+                    node_product(kind, index, k)
+
+        for n in range(-3, UNITS + 4):
+            if has_chain(n - 1):
+                factors_square(n - 1)
+            if live(n):
+                aggregate(n, 0)
+            if has_chain(n - 1):
+                factors_mean(n - 1)
+            if slot_ending(n - 5) is not None:
+                node_fetch(slot_ending(n - 5))
+            if live(n - 4):
+                weigh(n - 4)
             if has_chain(n - 1):
                 factors_join(n - 1)
                 factors_rstd(n - 1)
-            if live(n - 1):
-                normalise(n - 1)
-            if live(n):
-                aggregate(n)
-            if slot_ending(n - 5) is not None:
-                node_fetch(slot_ending(n - 5))
-                node_divide(slot_ending(n - 5))
-            if live(n - 4):
-                weigh(n - 4)
-            if live(n + 3):
-                regroup(n + 3)
-            if slot_ending(n - 6) is not None:
-                node_back(slot_ending(n - 6))
-            if live(n + 4):
-                flip(n + 4)
-            if live(n - 4):
-                add_up(n - 4)
-            if live(n):
-                statistics(n, 0)
-                statistics(n, 1)
             if live(n - 3):
                 squash(n - 3)
-            if has_chain(n):
-                factors_square(n)
-                factors_mean(n)
+            if live(n - 1):
+                normalise(n - 1)
+            extra(n, 0)
+            if live(n + 3):
+                flip(n + 3)
+            if live(n - 4):
+                add_up(n - 4, 0)
+            if live(n):
+                statistics(n, 0)
             if live(n - 2):
                 residual(n - 2)
-            if slot_ending(n - 2) is not None and slot_ending(n - 2) + 3 < SLOTS:
-                load_edges(slot_ending(n - 2) + 3)
+            if n >= 0 and n % BATCH == 0 and n // BATCH + LOADS_AHEAD < UNITS // BATCH:
+                load_edges(n // BATCH + LOADS_AHEAD)
+            if live(n):
+                aggregate(n, 1)
+            if live(n + 3):
+                regroup(n + 3)
+            extra(n, 1)
+            if live(n - 4):
+                add_up(n - 4, 1)
             if live(n - 3):
                 exponent(n - 3)
-            if live(n + 2) and (n + 2) % BATCH == 0:
-                quantise_batch((n + 2) // BATCH)
-            if slot_ending(n - 6) is not None:
-                node_sum(slot_ending(n - 6), n + 1)
-            if slot_ending(n - 8) is not None:
-                node_scale(slot_ending(n - 8), n - 1)
-            if slot_ending(n - 9) is not None:
-                node_finish(slot_ending(n - 9), n - 2)
+            if live(n):
+                statistics(n, 1)
+            if live(n + 3) and (n + 3) % BATCH == BATCH - 1:
+                quantise_batch((n + 3) // BATCH)
+            extra(n, 2)
+
+        last["stats"] = keep.tile([P, SLOTS, 2, 3], F32, name="last_stats")
+        for s in range(SLOTS + 2):
+            if s < SLOTS:
+                node_invert(s)
+            if 0 <= s - 1 < SLOTS:
+                node_divide(s - 1)
+                node_sum(s - 1)
+            if 0 <= s - 2 < SLOTS:
+                node_statistics(s - 2)
+        node_factors()
+        for s in range(SLOTS + 1):
+            if s < SLOTS:
+                node_scale(s)
+            if s >= 1:
+                node_finish(s - 1)

@@ -55,7 +55,7 @@ def tile_graphmodel_pa_kernel(
         early = ctx.enter_context(tc.tile_pool(name="early", bufs=2))
         stage = ctx.enter_context(tc.tile_pool(name="stage", bufs=2))
         normed = ctx.enter_context(tc.tile_pool(name="normed", bufs=5))
-        gates = ctx.enter_context(tc.tile_pool(name="gates", bufs=3))
+        gates = ctx.enter_context(tc.tile_pool(name="gates", bufs=4))
         gated = ctx.enter_context(tc.tile_pool(name="gated", bufs=2))
         nodes = ctx.enter_context(tc.tile_pool(name="nodes", bufs=3))
         small = ctx.enter_context(tc.tile_pool(name="small", bufs=6))
@@ -99,12 +99,12 @@ def tile_graphmodel_pa_kernel(
             )
 
         load_x_all(0)
+        load_edges(0)
         nc.scalar.dma_start(out=x_own[:], in_=x_rows)
         for w in ("A", "B", "E"):
             load_weight(w)
-        load_edges(0)
-        load_weight("V")
         load_edges(1)
+        load_weight("V")
         load_x_all(1)
         for b in range(2, LOADS_AHEAD):
             load_edges(b)
@@ -182,17 +182,19 @@ def tile_graphmodel_pa_kernel(
             quantise(grouped_x[g], codes[:, part], planes[:, part], 0, 4)
             quantise(grouped_x[g], codes[:, part], planes[:, part], 4, 2)
 
-        for g in range(2):
+        def x_group(g):
             for first in range(0, SLOTS, 2):
                 x_pair(g, first, psum_acc, "acc", nc.vector.tensor_copy if first == 2 else nc.scalar.copy)
             x_quantise(g)
+
+        x_group(0)
 
         message_source = keep.tile([P, NODES, C], F32)
         own_turned = keep.tile([P, SLOTS, CHUNKS, P], F32)
         sums = keep.tile([P, SLOTS - 1, 2, CHUNKS, P], F32)
 
-        def node_product(w, index, k):
-            if w == "V":
+        def node_product(w, index, k, early=False):
+            if w == "V" and not early:
                 product = psum_sum.tile([P, C], F32, name="product%s%d" % (w, index), tag="turned%d" % k)
             else:
                 product = psum_acc.tile([P, C], F32, name="product%s%d" % (w, index), tag="acc")
@@ -209,7 +211,7 @@ def tile_graphmodel_pa_kernel(
                         rhs=own_codes[:, rows].bitcast(FP8X4), rhs_scale=own_planes[:, rows], start=True, stop=True,
                     )
                 out, factor = own_turned[:, index, :, :].rearrange("p q r -> p (q r)"), 1.0
-            if k == 0:
+            if k == 0 and w == "V":
                 nc.scalar.mul(out=out, in_=product[:], mul=factor)
             else:
                 nc.vector.tensor_scalar(out=out, in0=product[:], scalar1=factor, scalar2=None, op0=ALU.mult)
@@ -355,16 +357,18 @@ def tile_graphmodel_pa_kernel(
                     )
 
         def node_fetch(s):
-            nc.scalar.copy(out=sums[:, s, 0, :, :], in_=turned_of[(s, 0)][:])
+            nc.scalar.activation(out=sums[:, s, 0, :, :], in_=turned_of[(s, 0)][:], func=ACT.Square)
             nc.vector.tensor_copy(out=sums[:, s, 1, :, :], in_=turned_of[(s, 1)][:])
 
         share_of, last = {}, {}
 
         def node_invert(s):
             inverse = nodes.tile([P, CHUNKS, P], F32, name="inverse%d" % s, tag="inverse")
-            total = sums[:, s, 0, :, :] if s < SLOTS - 1 else turned_of[(s, 0)][:]
-            nc.scalar.activation(out=inverse[:], in_=total, func=ACT.Abs_reciprocal_sqrt)
-            nc.scalar.activation(out=inverse[:], in_=inverse[:], func=ACT.Square)
+            if s < SLOTS - 1:
+                nc.scalar.activation(out=inverse[:], in_=sums[:, s, 0, :, :], func=ACT.Abs_reciprocal_sqrt)
+            else:
+                nc.scalar.activation(out=inverse[:], in_=turned_of[(s, 0)][:], func=ACT.Square)
+                nc.scalar.activation(out=inverse[:], in_=inverse[:], func=ACT.Abs_reciprocal_sqrt)
             share_of[s] = inverse
 
         def node_divide(s):
@@ -386,26 +390,27 @@ def tile_graphmodel_pa_kernel(
                 out=last["stats"][:, s, :, :].rearrange("p h k -> p (h k)"), in_=x_new_of[s][:].rearrange("p q c -> p (q c)")
             )
 
-        def node_factors():
-            stats, n2 = last["stats"], float(HALF_COUNT * HALF_COUNT)
-            nc.scalar.activation(out=stats[:, :, :, 0], in_=stats[:, :, :, 1], func=ACT.Square, scale=HALF_ROOT)
-            means = psum_misc.tile([P, SLOTS, 2, 3], F32, tag="misc")
+        def node_factors(lo, hi):
+            stats, joined, work, n2 = last["stats"], last["joined"], last["work"], float(HALF_COUNT * HALF_COUNT)
+            nc.scalar.activation(out=stats[:, lo:hi, :, 0], in_=stats[:, lo:hi, :, 1], func=ACT.Square, scale=HALF_ROOT)
+            means = psum_misc.tile([P, hi - lo, 2, 3], F32, tag="misc")
             nc.tensor.matmul(
                 out=means[:].rearrange("p c h k -> p (c h k)"), lhsT=neg_parity[:].rearrange("p a t -> p (a t)"),
-                rhs=stats[:].rearrange("p c h k -> p (c h k)"), start=True, stop=True,
+                rhs=stats[:, lo:hi, :, :].rearrange("p c h k -> p (c h k)"), start=True, stop=True,
             )
-            joined = keep.tile([P, SLOTS, 3], F32)
-            nc.vector.tensor_reduce(out=joined[:], in_=means[:].rearrange("p c h k -> p c k h"), axis=AXIS.X, op=ALU.add)
-            work = keep.tile([P, 4, SLOTS], F32)
-            nc.vector.tensor_tensor(out=work[:, 0, :], in0=joined[:, :, 0], in1=joined[:, :, 2], op=ALU.add)
-            nc.vector.tensor_tensor(out=work[:, 1, :], in0=joined[:, :, 1], in1=joined[:, :, 1], op=ALU.mult)
+            nc.vector.tensor_reduce(
+                out=joined[:, lo:hi, :], in_=means[:].rearrange("p c h k -> p c k h"), axis=AXIS.X, op=ALU.add
+            )
+            nc.vector.tensor_tensor(out=work[:, 0, lo:hi], in0=joined[:, lo:hi, 0], in1=joined[:, lo:hi, 2], op=ALU.add)
+            nc.vector.tensor_tensor(out=work[:, 1, lo:hi], in0=joined[:, lo:hi, 1], in1=joined[:, lo:hi, 1], op=ALU.mult)
             nc.vector.tensor_scalar(
-                out=work[:, 0, :], in0=work[:, 0, :], scalar1=-1.0 / n2, scalar2=BN_EPS / n2, op0=ALU.mult, op1=ALU.add
+                out=work[:, 0, lo:hi], in0=work[:, 0, lo:hi], scalar1=-1.0 / n2, scalar2=BN_EPS / n2, op0=ALU.mult, op1=ALU.add
             )
-            nc.vector.tensor_tensor(out=work[:, 0, :], in0=work[:, 0, :], in1=work[:, 1, :], op=ALU.subtract)
-            nc.scalar.activation(out=work[:, 2, :], in_=work[:, 0, :], func=ACT.Abs_reciprocal_sqrt, scale=n2)
+            nc.vector.tensor_tensor(out=work[:, 0, lo:hi], in0=work[:, 0, lo:hi], in1=work[:, 1, lo:hi], op=ALU.subtract)
+            nc.scalar.activation(out=work[:, 2, lo:hi], in_=work[:, 0, lo:hi], func=ACT.Abs_reciprocal_sqrt, scale=n2)
             nc.vector.scalar_tensor_tensor(
-                out=work[:, 3, :], in0=joined[:, :, 1], scalar=float(HALF_COUNT), in1=work[:, 2, :], op0=ALU.mult, op1=ALU.mult
+                out=work[:, 3, lo:hi], in0=joined[:, lo:hi, 1], scalar=float(HALF_COUNT), in1=work[:, 2, lo:hi],
+                op0=ALU.mult, op1=ALU.mult,
             )
             last["rstd"], last["shift"] = work[:, 2, :], work[:, 3, :]
 
@@ -424,6 +429,7 @@ def tile_graphmodel_pa_kernel(
             return u // UNITS_PER_SLOT if live(u) and u % UNITS_PER_SLOT == UNITS_PER_SLOT - 1 else None
 
         extras = {
+            -2: [("G", 1)],
             -1: [("V", 0), ("V", 1), ("V", 2), ("V", 3)],
             0: [("X", 0), ("V", 4), ("V", 5)], 1: [("X", 2), ("V", 6), ("V", 7)], 2: [("X", 4), ("V", 8), ("V", 9)],
             3: [("V", 10), ("V", 11)],
@@ -436,23 +442,25 @@ def tile_graphmodel_pa_kernel(
             for kind, index in todo[place : place + 1] if place < 2 else todo[2:]:
                 k = used["count"] % 2
                 used["count"] += 1
-                if kind == "X":
+                if kind == "G":
+                    x_group(index)
+                elif kind == "X":
                     x_pair(2, index, psum_sum, "turned%d" % k, nc.vector.tensor_copy)
                     x_quantise_pair(2, index)
                 else:
-                    node_product(kind, index, k)
+                    node_product(kind, index, k, early=n < 0)
 
-        for n in range(-3, UNITS + 4):
+        for n in range(-3, UNITS + 5):
             if has_chain(n - 1):
                 factors_square(n - 1)
             if live(n):
                 aggregate(n, 0)
             if has_chain(n - 1):
                 factors_mean(n - 1)
-            if slot_ending(n - 5) is not None:
-                node_fetch(slot_ending(n - 5))
-            if live(n - 4):
-                weigh(n - 4)
+            if slot_ending(n - 6) is not None and slot_ending(n - 6) < SLOTS - 1:
+                node_fetch(slot_ending(n - 6))
+            if live(n - 5):
+                weigh(n - 5)
             if has_chain(n - 1):
                 factors_join(n - 1)
                 factors_rstd(n - 1)
@@ -463,8 +471,8 @@ def tile_graphmodel_pa_kernel(
             extra(n, 0)
             if live(n + 3):
                 flip(n + 3)
-            if live(n - 4):
-                add_up(n - 4, 0)
+            if live(n - 5):
+                add_up(n - 5, 0)
             if live(n):
                 statistics(n, 0)
             if live(n - 2):
@@ -476,8 +484,8 @@ def tile_graphmodel_pa_kernel(
             if live(n + 3):
                 regroup(n + 3)
             extra(n, 1)
-            if live(n - 4):
-                add_up(n - 4, 1)
+            if live(n - 5):
+                add_up(n - 5, 1)
             if live(n - 3):
                 exponent(n - 3)
             if live(n):
@@ -487,6 +495,9 @@ def tile_graphmodel_pa_kernel(
             extra(n, 2)
 
         last["stats"] = keep.tile([P, SLOTS, 2, 3], F32, name="last_stats")
+        last["joined"] = keep.tile([P, SLOTS, 3], F32, name="last_joined")
+        last["work"] = keep.tile([P, 4, SLOTS], F32, name="last_work")
+        FIRST = SLOTS // 2
         for s in range(SLOTS + 2):
             if s < SLOTS:
                 node_invert(s)
@@ -495,9 +506,16 @@ def tile_graphmodel_pa_kernel(
                 node_sum(s - 1)
             if 0 <= s - 2 < SLOTS:
                 node_statistics(s - 2)
-        node_factors()
-        for s in range(SLOTS + 1):
+            if s - 2 == FIRST - 1:
+                node_factors(0, FIRST)
+            if 0 <= s - 2 - FIRST < FIRST:
+                node_scale(s - 2 - FIRST)
+            if 0 <= s - 3 - FIRST < FIRST:
+                node_finish(s - 3 - FIRST)
+        node_finish(FIRST - 1)
+        node_factors(FIRST, SLOTS)
+        for s in range(FIRST, SLOTS + 1):
             if s < SLOTS:
                 node_scale(s)
-            if s >= 1:
+            if s > FIRST:
                 node_finish(s - 1)

@@ -455,6 +455,8 @@ def tile_graphmodel_pa_kernel(
                 factors_square(n - 1)
             if live(n):
                 aggregate(n, 0)
+            if live(n):
+                aggregate(n, 1)
             if has_chain(n - 1):
                 factors_mean(n - 1)
             if slot_ending(n - 6) is not None and slot_ending(n - 6) < SLOTS - 1:
@@ -479,8 +481,6 @@ def tile_graphmodel_pa_kernel(
                 residual(n - 2)
             if n >= 0 and n % BATCH == 0 and n // BATCH + LOADS_AHEAD < UNITS // BATCH:
                 load_edges(n // BATCH + LOADS_AHEAD)
-            if live(n):
-                aggregate(n, 1)
             if live(n + 3):
                 regroup(n + 3)
             extra(n, 1)

@@ -28,6 +28,7 @@ assert HALF_ROOT * HALF_ROOT == HALF_COUNT
 BATCH = 2
 BN_EPS = 1e-5
 RV_MOD, RV_CNT, RV_FROM = 4, 1, 0
+CHAIN = 2
 LOADS_AHEAD = 5
 WEIGHT_NAMES = ("A", "B", "E", "U", "V")
 
@@ -54,7 +55,7 @@ def tile_graphmodel_pa_kernel(
         edges = ctx.enter_context(tc.tile_pool(name="edges", bufs=9))
         early = ctx.enter_context(tc.tile_pool(name="early", bufs=2))
         stage = ctx.enter_context(tc.tile_pool(name="stage", bufs=2))
-        normed = ctx.enter_context(tc.tile_pool(name="normed", bufs=5))
+        normed = ctx.enter_context(tc.tile_pool(name="normed", bufs=6))
         gates = ctx.enter_context(tc.tile_pool(name="gates", bufs=4))
         gated = ctx.enter_context(tc.tile_pool(name="gated", bufs=2))
         nodes = ctx.enter_context(tc.tile_pool(name="nodes", bufs=3))
@@ -119,7 +120,7 @@ def tile_graphmodel_pa_kernel(
             out=neg_parity[:], in0=own_parity[:].unsqueeze(1).to_broadcast([P, P // 2, 2]),
             scalar1=-1.0 / (P * HALF_COUNT), scalar2=None, op0=ALU.mult,
         )
-        minus_half = keep.tile([P, UNIT + 1], F32)
+        minus_half = keep.tile([P, CHAIN * UNIT], F32)
         nc.vector.memset(minus_half[:], -0.5)
         warm = keep.tile([P, 1], F32)
         nc.vector.memset(warm[:], 0.0)
@@ -258,73 +259,61 @@ def tile_graphmodel_pa_kernel(
         def statistics(u, i):
             nc.vector.bn_stats(out=stats_tile(u)[:, i, :, :].rearrange("p h k -> p (h k)"), in_=acc_of[(u, i)][:])
 
-        node_in_chain = {}
-
-        def columns(m):
-            return 0 if live(m) else UNIT, UNIT + 1 if m in node_in_chain else UNIT
+        joined_of, slope_of = {}, {}
 
         def has_chain(m):
-            return columns(m)[0] < columns(m)[1]
+            return live(m)
 
         def factors_square(m):
-            lo, hi = columns(m)
             nc.scalar.activation(
-                out=stats_of[m][:, lo:hi, :, 0], in_=stats_of[m][:, lo:hi, :, 1], func=ACT.Square, scale=HALF_ROOT
+                out=stats_of[m][:, 0:UNIT, :, 0], in_=stats_of[m][:, 0:UNIT, :, 1], func=ACT.Square, scale=HALF_ROOT
             )
 
         def factors_mean(m):
-            lo, hi = columns(m)
-            means = psum_misc.tile([P, hi - lo, 2, 3], F32, tag="misc")
+            means = psum_misc.tile([P, UNIT, 2, 3], F32, tag="misc")
             nc.tensor.matmul(
                 out=means[:].rearrange("p c h k -> p (c h k)"), lhsT=neg_parity[:].rearrange("p a t -> p (a t)"),
-                rhs=stats_of[m][:, lo:hi, :, :].rearrange("p c h k -> p (c h k)"), start=True, stop=True,
+                rhs=stats_of[m][:, 0:UNIT, :, :].rearrange("p c h k -> p (c h k)"), start=True, stop=True,
             )
             factors_of[m] = {"means": means}
 
         def factors_join(m):
-            lo, hi = columns(m)
-            joined = small.tile([P, UNIT + 1, 3], F32, tag="joined")
+            g, k = m // CHAIN, m % CHAIN
+            if k == 0:
+                joined_of[g] = small.tile([P, CHAIN * UNIT, 3], F32, name="joined%d" % g, tag="joined")
             nc.vector.tensor_reduce(
-                out=joined[:, lo:hi, :], in_=factors_of[m]["means"][:].rearrange("p c h k -> p c k h"), axis=AXIS.X, op=ALU.add
+                out=joined_of[g][:, k * UNIT : (k + 1) * UNIT, :], in_=factors_of[m]["means"][:].rearrange("p c h k -> p c k h"),
+                axis=AXIS.X, op=ALU.add,
             )
-            factors_of[m]["joined"] = joined
 
         def factors_rstd(m):
-            lo, hi = columns(m)
-            joined = factors_of[m]["joined"]
+            if m % CHAIN != CHAIN - 1:
+                return
+            g = m // CHAIN
+            joined = joined_of[g]
             n2 = float(HALF_COUNT * HALF_COUNT)
-            square = small.tile([P, UNIT + 1], F32, tag="square")
-            nc.gpsimd.tensor_tensor(out=square[:, lo:hi], in0=joined[:, lo:hi, 1], in1=joined[:, lo:hi, 1], op=ALU.mult)
-            second = small.tile([P, UNIT + 1], F32, tag="second")
-            nc.gpsimd.tensor_tensor(out=second[:, lo:hi], in0=joined[:, lo:hi, 0], in1=joined[:, lo:hi, 2], op=ALU.add)
-            nc.gpsimd.tensor_scalar(
-                out=second[:, lo:hi], in0=second[:, lo:hi], scalar1=-1.0 / n2, scalar2=BN_EPS / n2, op0=ALU.mult, op1=ALU.add
-            )
-            nc.gpsimd.tensor_tensor(out=second[:, lo:hi], in0=second[:, lo:hi], in1=square[:, lo:hi], op=ALU.subtract)
-            slope = small.tile([P, UNIT + 1], F32, tag="slope")
-            nc.gpsimd.tensor_tensor(out=slope[:, lo:hi], in0=second[:, lo:hi], in1=minus_half[:, lo:hi], op=ALU.pow)
-            factors_of[m]["slope"] = slope
-            if m in node_in_chain:
-                last = small.tile([P, 2], F32, tag="last")
-                nc.gpsimd.tensor_scalar(
-                    out=last[:, 0:1], in0=slope[:, UNIT : UNIT + 1], scalar1=1.0 / HALF_COUNT, scalar2=0.0, op0=ALU.mult, op1=ALU.add
-                )
-                nc.gpsimd.tensor_tensor(out=last[:, 1:2], in0=slope[:, UNIT : UNIT + 1], in1=joined[:, UNIT, 1:2], op=ALU.mult)
-                factors_of[m]["last"] = last
+            square = small.tile([P, CHAIN * UNIT], F32, tag="square")
+            nc.gpsimd.tensor_tensor(out=square[:], in0=joined[:, :, 1], in1=joined[:, :, 1], op=ALU.mult)
+            second = small.tile([P, CHAIN * UNIT], F32, tag="second")
+            nc.gpsimd.tensor_tensor(out=second[:], in0=joined[:, :, 0], in1=joined[:, :, 2], op=ALU.add)
+            nc.gpsimd.tensor_scalar(out=second[:], in0=second[:], scalar1=-1.0 / n2, scalar2=BN_EPS / n2, op0=ALU.mult, op1=ALU.add)
+            nc.gpsimd.tensor_tensor(out=second[:], in0=second[:], in1=square[:], op=ALU.subtract)
+            slope_of[g] = small.tile([P, CHAIN * UNIT], F32, name="slope%d" % g, tag="slope")
+            nc.gpsimd.tensor_tensor(out=slope_of[g][:], in0=second[:], in1=minus_half[:], op=ALU.pow)
 
         def normalise(u):
             result_of[u] = normed.tile([P, UNIT, C], F32, name="result%d" % u, tag="result")
             for i in range(UNIT):
                 nc.scalar.activation(
                     out=result_of[u][:, i, :], in_=acc_of[(u, i)][:], func=ACT.Relu,
-                    bias=factors_of[u]["joined"][:, i, 1:2], scale=1.0 / HALF_COUNT,
+                    bias=joined_of[u // CHAIN][:, (u % CHAIN) * UNIT + i, 1:2], scale=1.0 / HALF_COUNT,
                 )
 
         def residual(u):
-            s, a = u // UNITS_PER_SLOT, u % UNITS_PER_SLOT
             for i in range(UNIT):
+                column = (u % CHAIN) * UNIT + i
                 nc.vector.scalar_tensor_tensor(
-                    out=result_of[u][:, i, :], in0=result_of[u][:, i, :], scalar=factors_of[u]["slope"][:, i : i + 1],
+                    out=result_of[u][:, i, :], in0=result_of[u][:, i, :], scalar=slope_of[u // CHAIN][:, column : column + 1],
                     in1=edge_in[u // BATCH][:, UNIT * (u % BATCH) + i, :], op0=ALU.mult, op1=ALU.add,
                 )
             nc.sync.dma_start(out=edge_out_rows[:, UNIT * u : UNIT * (u + 1), :], in_=result_of[u][:])
@@ -450,7 +439,7 @@ def tile_graphmodel_pa_kernel(
                 else:
                     node_product(kind, index, k, early=n < 0)
 
-        for n in range(-3, UNITS + 5):
+        for n in range(-3, UNITS + 6):
             if has_chain(n - 1):
                 factors_square(n - 1)
             if live(n):
@@ -459,35 +448,35 @@ def tile_graphmodel_pa_kernel(
                 aggregate(n, 1)
             if has_chain(n - 1):
                 factors_mean(n - 1)
-            if slot_ending(n - 6) is not None and slot_ending(n - 6) < SLOTS - 1:
-                node_fetch(slot_ending(n - 6))
-            if live(n - 5):
-                weigh(n - 5)
+            if slot_ending(n - 7) is not None and slot_ending(n - 7) < SLOTS - 1:
+                node_fetch(slot_ending(n - 7))
+            if live(n - 6):
+                weigh(n - 6)
             if has_chain(n - 1):
                 factors_join(n - 1)
                 factors_rstd(n - 1)
-            if live(n - 3):
-                squash(n - 3)
+            if live(n - 4):
+                squash(n - 4)
             if live(n - 1):
                 normalise(n - 1)
             extra(n, 0)
             if live(n + 3):
                 flip(n + 3)
-            if live(n - 5):
-                add_up(n - 5, 0)
+            if live(n - 6):
+                add_up(n - 6, 0)
             if live(n):
                 statistics(n, 0)
-            if live(n - 2):
-                residual(n - 2)
+            if live(n - 3):
+                residual(n - 3)
             if n >= 0 and n % BATCH == 0 and n // BATCH + LOADS_AHEAD < UNITS // BATCH:
                 load_edges(n // BATCH + LOADS_AHEAD)
             if live(n + 3):
                 regroup(n + 3)
             extra(n, 1)
-            if live(n - 5):
-                add_up(n - 5, 1)
-            if live(n - 3):
-                exponent(n - 3)
+            if live(n - 6):
+                add_up(n - 6, 1)
+            if live(n - 4):
+                exponent(n - 4)
             if live(n):
                 statistics(n, 1)
             if live(n + 3) and (n + 3) % BATCH == BATCH - 1:

@@ -60,6 +60,7 @@ def tile_graphmodel_pa_kernel(
         gated = ctx.enter_context(tc.tile_pool(name="gated", bufs=2))
         nodes = ctx.enter_context(tc.tile_pool(name="nodes", bufs=3))
         small = ctx.enter_context(tc.tile_pool(name="small", bufs=6))
+        xouts = ctx.enter_context(tc.tile_pool(name="xouts", bufs=6))
         psum_flip = ctx.enter_context(tc.psum_pool(name="psum_flip", bufs=1))
         psum_acc = ctx.enter_context(tc.psum_pool(name="psum_acc", bufs=AHEAD * UNIT))
         psum_misc = ctx.enter_context(tc.psum_pool(name="psum_misc", bufs=1))
@@ -379,16 +380,19 @@ def tile_graphmodel_pa_kernel(
                 out=last["stats"][:, s, :, :].rearrange("p h k -> p (h k)"), in_=x_new_of[s][:].rearrange("p q c -> p (q c)")
             )
 
-        def node_factors(lo, hi):
-            stats, joined, work, n2 = last["stats"], last["joined"], last["work"], float(HALF_COUNT * HALF_COUNT)
+        def node_means(lo, hi):
+            stats = last["stats"]
             nc.scalar.activation(out=stats[:, lo:hi, :, 0], in_=stats[:, lo:hi, :, 1], func=ACT.Square, scale=HALF_ROOT)
-            means = psum_misc.tile([P, hi - lo, 2, 3], F32, tag="misc")
+            last["means"] = psum_misc.tile([P, hi - lo, 2, 3], F32, name="last_means%d" % lo, tag="misc")
             nc.tensor.matmul(
-                out=means[:].rearrange("p c h k -> p (c h k)"), lhsT=neg_parity[:].rearrange("p a t -> p (a t)"),
+                out=last["means"][:].rearrange("p c h k -> p (c h k)"), lhsT=neg_parity[:].rearrange("p a t -> p (a t)"),
                 rhs=stats[:, lo:hi, :, :].rearrange("p c h k -> p (c h k)"), start=True, stop=True,
             )
+
+        def node_rstd(lo, hi):
+            joined, work, n2 = last["joined"], last["work"], float(HALF_COUNT * HALF_COUNT)
             nc.vector.tensor_reduce(
-                out=joined[:, lo:hi, :], in_=means[:].rearrange("p c h k -> p c k h"), axis=AXIS.X, op=ALU.add
+                out=joined[:, lo:hi, :], in_=last["means"][:].rearrange("p c h k -> p c k h"), axis=AXIS.X, op=ALU.add
             )
             nc.vector.tensor_tensor(out=work[:, 0, lo:hi], in0=joined[:, lo:hi, 0], in1=joined[:, lo:hi, 2], op=ALU.add)
             nc.vector.tensor_tensor(out=work[:, 1, lo:hi], in0=joined[:, lo:hi, 1], in1=joined[:, lo:hi, 1], op=ALU.mult)
@@ -397,6 +401,9 @@ def tile_graphmodel_pa_kernel(
             )
             nc.vector.tensor_tensor(out=work[:, 0, lo:hi], in0=work[:, 0, lo:hi], in1=work[:, 1, lo:hi], op=ALU.subtract)
             nc.scalar.activation(out=work[:, 2, lo:hi], in_=work[:, 0, lo:hi], func=ACT.Abs_reciprocal_sqrt, scale=n2)
+
+        def node_shift(lo, hi):
+            joined, work = last["joined"], last["work"]
             nc.vector.scalar_tensor_tensor(
                 out=work[:, 3, lo:hi], in0=joined[:, lo:hi, 1], scalar=float(HALF_COUNT), in1=work[:, 2, lo:hi],
                 op0=ALU.mult, op1=ALU.mult,
@@ -404,7 +411,7 @@ def tile_graphmodel_pa_kernel(
             last["rstd"], last["shift"] = work[:, 2, :], work[:, 3, :]
 
         def node_scale(s):
-            last[s] = nodes.tile([P, C], F32, name="x_out%d" % s, tag="x_out")
+            last[s] = xouts.tile([P, C], F32, name="x_out%d" % s, tag="x_out")
             nc.vector.scalar_tensor_tensor(
                 out=last[s][:], in0=x_new_of[s][:].rearrange("p q c -> p (q c)"), scalar=last["rstd"][:, s : s + 1],
                 in1=x_own[:, s, :], op0=ALU.mult, op1=ALU.add,
@@ -487,22 +494,33 @@ def tile_graphmodel_pa_kernel(
         last["joined"] = keep.tile([P, SLOTS, 3], F32, name="last_joined")
         last["work"] = keep.tile([P, 4, SLOTS], F32, name="last_work")
         FIRST = SLOTS // 2
-        for s in range(SLOTS + 2):
-            if s < SLOTS:
-                node_invert(s)
-            if 0 <= s - 1 < SLOTS:
+        for s in range(FIRST + 2):
+            node_invert(s)
+            if s >= 1:
                 node_divide(s - 1)
                 node_sum(s - 1)
-            if 0 <= s - 2 < SLOTS:
+            if s >= 2:
                 node_statistics(s - 2)
-            if s - 2 == FIRST - 1:
-                node_factors(0, FIRST)
-            if 0 <= s - 2 - FIRST < FIRST:
-                node_scale(s - 2 - FIRST)
-            if 0 <= s - 3 - FIRST < FIRST:
-                node_finish(s - 3 - FIRST)
-        node_finish(FIRST - 1)
-        node_factors(FIRST, SLOTS)
+        node_means(0, FIRST)
+        node_invert(5)
+        node_divide(4)
+        node_sum(4)
+        node_statistics(3)
+        node_rstd(0, FIRST)
+        node_divide(5)
+        node_sum(5)
+        node_statistics(4)
+        node_shift(0, FIRST)
+        node_scale(0)
+        node_statistics(5)
+        node_means(FIRST, SLOTS)
+        node_finish(0)
+        node_scale(1)
+        node_rstd(FIRST, SLOTS)
+        node_finish(1)
+        node_scale(2)
+        node_shift(FIRST, SLOTS)
+        node_finish(2)
         for s in range(FIRST, SLOTS + 1):
             if s < SLOTS:
                 node_scale(s)

@@ -27,7 +27,7 @@ HALF_ROOT = 16.0
 assert HALF_ROOT * HALF_ROOT == HALF_COUNT
 BATCH = 2
 BN_EPS = 1e-5
-RV_MOD, RV_CNT, RV_FROM = 4, 1, 0
+RV_MOD, RV_CNT, RV_FROM = 4, 0, 0
 CHAIN = 2
 LOADS_AHEAD = 5
 WEIGHT_NAMES = ("A", "B", "E", "U", "V")
@@ -361,6 +361,19 @@ def tile_graphmodel_pa_kernel(
                 nc.scalar.activation(out=inverse[:], in_=inverse[:], func=ACT.Abs_reciprocal_sqrt)
             share_of[s] = inverse
 
+        def node_own(s):
+            product = psum_misc.tile([P, CHUNKS, P], F32, name="own%d" % s, tag="misc")
+            rows = slice(s * P, (s + 1) * P)
+            for q in range(CHUNKS):
+                cols = slice(q * P, (q + 1) * P)
+                nc.tensor.matmul_mx(
+                    out=product[:, q, :],
+                    lhsT=w_words[:, WEIGHT_NAMES.index("U"), cols].bitcast(FP8X4),
+                    lhsT_scale=w_planes[:, WEIGHT_NAMES.index("U"), cols],
+                    rhs=own_codes[:, rows].bitcast(FP8X4), rhs_scale=own_planes[:, rows], start=True, stop=True,
+                )
+            nc.scalar.copy(out=own_turned[:, s, :, :], in_=product[:])
+
         def node_divide(s):
             message = sums[:, s, 1, :, :] if s < SLOTS - 1 else turned_of[(s, 1)][:]
             nc.vector.tensor_tensor(out=share_of[s][:], in0=message, in1=share_of[s][:], op=ALU.mult)
@@ -429,7 +442,7 @@ def tile_graphmodel_pa_kernel(
             -1: [("V", 0), ("V", 1), ("V", 2), ("V", 3)],
             0: [("X", 0), ("V", 4), ("V", 5)], 1: [("X", 2), ("V", 6), ("V", 7)], 2: [("X", 4), ("V", 8), ("V", 9)],
             3: [("V", 10), ("V", 11)],
-            UNITS + 1: [("U", 0), ("U", 1)], UNITS + 2: [("U", 2), ("U", 3)], UNITS + 3: [("U", 4), ("U", 5)],
+            UNITS + 1: [("U", 0)], UNITS + 2: [("U", 1)], UNITS + 3: [("U", 2)],
         }
         used = {"count": 0}
 
@@ -496,6 +509,9 @@ def tile_graphmodel_pa_kernel(
         FIRST = SLOTS // 2
         for s in range(FIRST + 2):
             node_invert(s)
+            if s >= 1:
+                if s + 2 < SLOTS:
+                    node_own(s + 2)
             if s >= 1:
                 node_divide(s - 1)
                 node_sum(s - 1)

@@ -101,14 +101,13 @@ def tile_graphmodel_pa_kernel(
             )
 
         load_x_all(0)
-        load_edges(0)
         nc.scalar.dma_start(out=x_own[:], in_=x_rows)
+        load_weight("V")
+        load_edges(0)
+        load_x_all(1)
         for w in ("A", "B", "E"):
             load_weight(w)
-        load_edges(1)
-        load_weight("V")
-        load_x_all(1)
-        for b in range(2, LOADS_AHEAD):
+        for b in range(1, LOADS_AHEAD):
             load_edges(b)
         load_weight("U")
 
@@ -173,11 +172,6 @@ def tile_graphmodel_pa_kernel(
             flipped = transpose_pair(rows, first, pool=pool, tag=tag)
             regroup_pair(flipped, grouped_x[g], first, engine_copy=engine_copy)
 
-        def x_quantise_pair(g, first):
-            codes, planes, base = ((all_codes, all_planes, 0), (own_codes, own_planes, 0), (all_codes, all_planes, SLOTS))[g]
-            part = slice(base * P, (base + SLOTS) * P)
-            quantise(grouped_x[g], codes[:, part], planes[:, part], first, 2)
-
         def x_quantise(g):
             codes, planes, base = ((all_codes, all_planes, 0), (own_codes, own_planes, 0), (all_codes, all_planes, SLOTS))[g]
             part = slice(base * P, (base + SLOTS) * P)
@@ -189,15 +183,13 @@ def tile_graphmodel_pa_kernel(
                 x_pair(g, first, psum_acc, "acc", nc.vector.tensor_copy if first == 2 else nc.scalar.copy)
             x_quantise(g)
 
-        x_group(0)
-
         message_source = keep.tile([P, NODES, C], F32)
         own_turned = keep.tile([P, SLOTS, CHUNKS, P], F32)
         sums = keep.tile([P, SLOTS - 1, 2, CHUNKS, P], F32)
 
-        def node_product(w, index, k, early=False):
-            if w == "V" and not early:
-                product = psum_sum.tile([P, C], F32, name="product%s%d" % (w, index), tag="turned%d" % k)
+        def node_product(w, index, k):
+            if k == 2:
+                product = psum_sum.tile([P, C], F32, name="product%s%d" % (w, index), tag="turned%d" % (index % 2))
             else:
                 product = psum_acc.tile([P, C], F32, name="product%s%d" % (w, index), tag="acc")
             if w == "V":
@@ -213,7 +205,7 @@ def tile_graphmodel_pa_kernel(
                         rhs=own_codes[:, rows].bitcast(FP8X4), rhs_scale=own_planes[:, rows], start=True, stop=True,
                     )
                 out, factor = own_turned[:, index, :, :].rearrange("p q r -> p (q r)"), 1.0
-            if k == 0 and w == "V":
+            if k != 1 and w == "V":
                 nc.scalar.mul(out=out, in_=product[:], mul=factor)
             else:
                 nc.vector.tensor_scalar(out=out, in0=product[:], scalar1=factor, scalar2=None, op0=ALU.mult)
@@ -228,8 +220,8 @@ def tile_graphmodel_pa_kernel(
         def regroup_on_vector(u):
             return u % RV_MOD < RV_CNT and u >= RV_FROM
 
-        def flip(u):
-            flipped_of[u] = transpose_pair(edge_in[u // BATCH], UNIT * (u % BATCH))
+        def flip(u, pool=psum_flip, tag="flipped"):
+            flipped_of[u] = transpose_pair(edge_in[u // BATCH], UNIT * (u % BATCH), pool=pool, tag=tag)
 
         def regroup(u):
             b, k = u // BATCH, u % BATCH
@@ -251,7 +243,10 @@ def tile_graphmodel_pa_kernel(
 
         def aggregate(u, i):
             s, a = u // UNITS_PER_SLOT, u % UNITS_PER_SLOT
-            agg = psum_acc.tile([P, C], F32, name="agg%d_%d" % (u, i), tag="acc")
+            if u < UNITS_PER_SLOT and u % 3 == 2:
+                agg = psum_sum.tile([P, C], F32, name="agg%d_%d" % (u, i), tag="turned%d" % i)
+            else:
+                agg = psum_acc.tile([P, C], F32, name="agg%d_%d" % (u, i), tag="acc")
             multiply(agg[:], own_codes, own_planes, s, "A", True, False)
             multiply(agg[:], all_codes, all_planes, UNIT * a + i, "B", False, False)
             multiply(agg[:], codes_of[u // BATCH], planes_of[u // BATCH], UNIT * (u % BATCH) + i, "E", False, True)
@@ -302,22 +297,22 @@ def tile_graphmodel_pa_kernel(
             slope_of[g] = small.tile([P, CHAIN * UNIT], F32, name="slope%d" % g, tag="slope")
             nc.gpsimd.tensor_tensor(out=slope_of[g][:], in0=second[:], in1=minus_half[:], op=ALU.pow)
 
-        def normalise(u):
-            result_of[u] = normed.tile([P, UNIT, C], F32, name="result%d" % u, tag="result")
-            for i in range(UNIT):
-                nc.scalar.activation(
-                    out=result_of[u][:, i, :], in_=acc_of[(u, i)][:], func=ACT.Relu,
-                    bias=joined_of[u // CHAIN][:, (u % CHAIN) * UNIT + i, 1:2], scale=1.0 / HALF_COUNT,
-                )
+        def normalise(u, i):
+            if i == 0:
+                result_of[u] = normed.tile([P, UNIT, C], F32, name="result%d" % u, tag="result")
+            nc.scalar.activation(
+                out=result_of[u][:, i, :], in_=acc_of[(u, i)][:], func=ACT.Relu,
+                bias=joined_of[u // CHAIN][:, (u % CHAIN) * UNIT + i, 1:2], scale=1.0 / HALF_COUNT,
+            )
 
-        def residual(u):
-            for i in range(UNIT):
-                column = (u % CHAIN) * UNIT + i
-                nc.vector.scalar_tensor_tensor(
-                    out=result_of[u][:, i, :], in0=result_of[u][:, i, :], scalar=slope_of[u // CHAIN][:, column : column + 1],
-                    in1=edge_in[u // BATCH][:, UNIT * (u % BATCH) + i, :], op0=ALU.mult, op1=ALU.add,
-                )
-            nc.sync.dma_start(out=edge_out_rows[:, UNIT * u : UNIT * (u + 1), :], in_=result_of[u][:])
+        def residual(u, i):
+            column = (u % CHAIN) * UNIT + i
+            nc.vector.scalar_tensor_tensor(
+                out=result_of[u][:, i, :], in0=result_of[u][:, i, :], scalar=slope_of[u // CHAIN][:, column : column + 1],
+                in1=edge_in[u // BATCH][:, UNIT * (u % BATCH) + i, :], op0=ALU.mult, op1=ALU.add,
+            )
+            if i == UNIT - 1:
+                nc.sync.dma_start(out=edge_out_rows[:, UNIT * u : UNIT * (u + 1), :], in_=result_of[u][:])
 
         def squash(u):
             gate_of[u] = gates.tile([P, UNIT, C], F32, name="gate%d" % u, tag="gate")
@@ -437,71 +432,68 @@ def tile_graphmodel_pa_kernel(
         def slot_ending(u):
             return u // UNITS_PER_SLOT if live(u) and u % UNITS_PER_SLOT == UNITS_PER_SLOT - 1 else None
 
-        extras = {
-            -2: [("G", 1)],
-            -1: [("V", 0), ("V", 1), ("V", 2), ("V", 3)],
-            0: [("X", 0), ("V", 4), ("V", 5)], 1: [("X", 2), ("V", 6), ("V", 7)], 2: [("X", 4), ("V", 8), ("V", 9)],
-            3: [("V", 10), ("V", 11)],
-            UNITS + 1: [("U", 0)], UNITS + 2: [("U", 1)], UNITS + 3: [("U", 2)],
-        }
-        used = {"count": 0}
+        x_group(0)
+        x_group(1)
+        for u in range(BATCH):
+            flip(u, psum_sum, "turned%d" % u)
+            regroup(u)
+        quantise_batch(0)
+        x_group(2)
+        for j in range(NODES):
+            node_product("V", j, (0, 1, 2)[j % 3])
+        flip(2)
+        regroup(2)
 
-        def extra(n, place):
-            todo = extras.get(n, [])
-            for kind, index in todo[place : place + 1] if place < 2 else todo[2:]:
-                k = used["count"] % 2
-                used["count"] += 1
-                if kind == "G":
-                    x_group(index)
-                elif kind == "X":
-                    x_pair(2, index, psum_sum, "turned%d" % k, nc.vector.tensor_copy)
-                    x_quantise_pair(2, index)
-                else:
-                    node_product(kind, index, k, early=n < 0)
+        def extra(n):
+            if UNITS < n < UNITS + 4:
+                node_product("U", n - UNITS - 1, 0)
 
-        for n in range(-3, UNITS + 6):
-            if has_chain(n - 1):
+        for n in range(UNITS + 8):
+            if n % BATCH == 0 and n // BATCH + LOADS_AHEAD < UNITS // BATCH:
+                load_edges(n // BATCH + LOADS_AHEAD)
+            if live(n - 7):
+                weigh(n - 7)
+            if live(n - 1):
+                statistics(n - 1, 0)
+            if live(n - 2):
+                normalise(n - 2, 0)
+            if live(n - 1):
+                statistics(n - 1, 1)
+            if slot_ending(n - 8) is not None and slot_ending(n - 8) < SLOTS - 1:
+                node_fetch(slot_ending(n - 8))
+            if live(n + 3):
+                flip(n + 3)
+            if live(n - 4):
+                residual(n - 4, 0)
+            if live(n - 2):
+                normalise(n - 2, 1)
+            if live(n - 1):
                 factors_square(n - 1)
             if live(n):
                 aggregate(n, 0)
-            if live(n):
-                aggregate(n, 1)
-            if has_chain(n - 1):
-                factors_mean(n - 1)
-            if slot_ending(n - 7) is not None and slot_ending(n - 7) < SLOTS - 1:
-                node_fetch(slot_ending(n - 7))
-            if live(n - 6):
-                weigh(n - 6)
-            if has_chain(n - 1):
-                factors_join(n - 1)
-                factors_rstd(n - 1)
-            if live(n - 4):
-                squash(n - 4)
+            extra(n)
             if live(n - 1):
-                normalise(n - 1)
-            extra(n, 0)
-            if live(n + 3):
-                flip(n + 3)
-            if live(n - 6):
-                add_up(n - 6, 0)
-            if live(n):
-                statistics(n, 0)
-            if live(n - 3):
-                residual(n - 3)
-            if n >= 0 and n % BATCH == 0 and n // BATCH + LOADS_AHEAD < UNITS // BATCH:
-                load_edges(n // BATCH + LOADS_AHEAD)
+                factors_mean(n - 1)
+            if live(n - 4):
+                residual(n - 4, 1)
             if live(n + 3):
                 regroup(n + 3)
-            extra(n, 1)
-            if live(n - 6):
-                add_up(n - 6, 1)
-            if live(n - 4):
-                exponent(n - 4)
+            if live(n - 2):
+                factors_rstd(n - 2)
             if live(n):
-                statistics(n, 1)
+                aggregate(n, 1)
+            if live(n - 7):
+                add_up(n - 7, 0)
+            if live(n - 5):
+                exponent(n - 5)
+            if live(n - 4):
+                squash(n - 4)
             if live(n + 3) and (n + 3) % BATCH == BATCH - 1:
                 quantise_batch((n + 3) // BATCH)
-            extra(n, 2)
+            if live(n - 7):
+                add_up(n - 7, 1)
+            if live(n - 1):
+                factors_join(n - 1)
 
         last["stats"] = keep.tile([P, SLOTS, 2, 3], F32, name="last_stats")
         last["joined"] = keep.tile([P, SLOTS, 3], F32, name="last_joined")

@@ -282,20 +282,29 @@ def tile_graphmodel_pa_kernel(
                 axis=AXIS.X, op=ALU.add,
             )
 
-        def factors_rstd(m):
+        parts_of = {}
+
+        def factors_parts(m):
             if m % CHAIN != CHAIN - 1:
                 return
-            g = m // CHAIN
-            joined = joined_of[g]
-            n2 = float(HALF_COUNT * HALF_COUNT)
-            square = small.tile([P, CHAIN * UNIT], F32, tag="square")
-            nc.gpsimd.tensor_tensor(out=square[:], in0=joined[:, :, 1], in1=joined[:, :, 1], op=ALU.mult)
-            second = small.tile([P, CHAIN * UNIT], F32, tag="second")
-            nc.gpsimd.tensor_tensor(out=second[:], in0=joined[:, :, 0], in1=joined[:, :, 2], op=ALU.add)
-            nc.gpsimd.tensor_scalar(out=second[:], in0=second[:], scalar1=-1.0 / n2, scalar2=BN_EPS / n2, op0=ALU.mult, op1=ALU.add)
-            nc.gpsimd.tensor_tensor(out=second[:], in0=second[:], in1=square[:], op=ALU.subtract)
+            joined = joined_of[m // CHAIN]
+            parts = small.tile([P, 3, CHAIN * UNIT], F32, name="parts%d" % m, tag="parts")
+            parts_of[m // CHAIN] = parts
+            nc.vector.tensor_tensor(out=parts[:, 0, :], in0=joined[:, :, 1], in1=joined[:, :, 1], op=ALU.mult)
+            nc.vector.scalar_tensor_tensor(
+                out=parts[:, 1, :], in0=joined[:, :, 0], scalar=-BN_EPS, in1=joined[:, :, 2], op0=ALU.add, op1=ALU.add
+            )
+
+        def factors_slope(m):
+            if m % CHAIN != CHAIN - 1:
+                return
+            g, n2 = m // CHAIN, float(HALF_COUNT * HALF_COUNT)
+            parts = parts_of[g]
+            nc.vector.scalar_tensor_tensor(
+                out=parts[:, 2, :], in0=parts[:, 1, :], scalar=-1.0 / n2, in1=parts[:, 0, :], op0=ALU.mult, op1=ALU.subtract
+            )
             slope_of[g] = small.tile([P, CHAIN * UNIT], F32, name="slope%d" % g, tag="slope")
-            nc.gpsimd.tensor_tensor(out=slope_of[g][:], in0=second[:], in1=minus_half[:], op=ALU.pow)
+            nc.gpsimd.tensor_tensor(out=slope_of[g][:], in0=parts[:, 2, :], in1=minus_half[:], op=ALU.pow)
 
         def normalise(u, i):
             if i == 0:
@@ -451,14 +460,20 @@ def tile_graphmodel_pa_kernel(
         for n in range(UNITS + 8):
             if n % BATCH == 0 and n // BATCH + LOADS_AHEAD < UNITS // BATCH:
                 load_edges(n // BATCH + LOADS_AHEAD)
-            if live(n - 7):
-                weigh(n - 7)
+            if live(n - 3):
+                factors_slope(n - 3)
+            if live(n - 2):
+                factors_join(n - 2)
             if live(n - 1):
                 statistics(n - 1, 0)
             if live(n - 2):
                 normalise(n - 2, 0)
             if live(n - 1):
                 statistics(n - 1, 1)
+            if live(n - 7):
+                weigh(n - 7)
+            if live(n - 2):
+                factors_parts(n - 2)
             if slot_ending(n - 8) is not None and slot_ending(n - 8) < SLOTS - 1:
                 node_fetch(slot_ending(n - 8))
             if live(n + 3):
@@ -478,8 +493,6 @@ def tile_graphmodel_pa_kernel(
                 residual(n - 4, 1)
             if live(n + 3):
                 regroup(n + 3)
-            if live(n - 2):
-                factors_rstd(n - 2)
             if live(n):
                 aggregate(n, 1)
             if live(n - 7):
@@ -492,8 +505,6 @@ def tile_graphmodel_pa_kernel(
                 quantise_batch((n + 3) // BATCH)
             if live(n - 7):
                 add_up(n - 7, 1)
-            if live(n - 1):
-                factors_join(n - 1)
 
         last["stats"] = keep.tile([P, SLOTS, 2, 3], F32, name="last_stats")
         last["joined"] = keep.tile([P, SLOTS, 3], F32, name="last_joined")

@@ -70,12 +70,10 @@ def tile_graphmodel_pa_kernel(
         ident = keep.tile([P, P], F32)
         make_identity(nc, ident[:])
 
-        x_own = keep.tile([P, SLOTS, C], BF16)
-        x_all = [keep.tile([P, SLOTS, C], BF16, name="x_all%d" % g) for g in range(2)]
+        x_own = [keep.tile([P, 2, C], BF16, name="x_own%d" % g) for g in range(SLOTS // 2)]
 
-        def load_x_all(g):
-            nc.scalar.dma_start(out=x_all[g][0:P:2, :, :], in_=x[:, g * SLOTS : (g + 1) * SLOTS, :])
-            nc.sync.dma_start(out=x_all[g][1:P:2, :, :], in_=x[:, g * SLOTS : (g + 1) * SLOTS, :])
+        def load_x(g, queue):
+            queue.dma_start(out=x_own[g][:], in_=x_rows[:, 2 * g : 2 * g + 2, :])
 
         edge_in = {}
         WIDE = BATCH * UNIT
@@ -100,12 +98,11 @@ def tile_graphmodel_pa_kernel(
                 in_=words[0].rearrange("p n t -> p (n t)").bitcast(I32),
             )
 
-        load_x_all(0)
-        nc.scalar.dma_start(out=x_own[:], in_=x_rows)
-        load_weight("V")
+        load_x(0, nc.scalar)
+        load_x(1, nc.sync)
+        load_x(2, nc.scalar)
         load_edges(0)
-        load_x_all(1)
-        for w in ("A", "B", "E"):
+        for w in ("V", "A", "B", "E"):
             load_weight(w)
         for b in range(1, LOADS_AHEAD):
             load_edges(b)
@@ -159,56 +156,57 @@ def tile_graphmodel_pa_kernel(
                 stop=stop,
             )
 
-        all_codes = keep.tile([P, NODES * P], U32, align_bytes=64)
-        all_planes = keep.tile([P, NODES * P], U8, align_bytes=64)
         own_codes = keep.tile([P, SLOTS * P], U32, align_bytes=64)
         own_planes = keep.tile([P, SLOTS * P], U8, align_bytes=64)
-        grouped_x = {}
+        all_codes = keep.tile([P, NODES * P], U32, align_bytes=64)
+        all_planes = keep.tile([P, NODES * P], U8, align_bytes=64)
 
-        def x_pair(g, first, pool, tag, engine_copy):
-            rows = (x_all[0], x_own, x_all[1])[g]
-            if first == 0:
-                grouped_x[g] = early.tile([P, SLOTS, P, PACK], BF16, align_bytes=64, name="grouped_x%d" % g, tag="grouped_x")
-            flipped = transpose_pair(rows, first, pool=pool, tag=tag)
-            regroup_pair(flipped, grouped_x[g], first, engine_copy=engine_copy)
+        def x_pair(g, engine_copy):
+            grouped = early.tile([P, 2, P, PACK], BF16, align_bytes=64, name="grouped_x%d" % g, tag="grouped_x")
+            flipped = transpose_pair(x_own[g], 0, pool=psum_acc, tag="acc")
+            regroup_pair(flipped, grouped, 0, engine_copy=engine_copy)
+            part = slice(2 * g * P, (2 * g + 2) * P)
+            quantise(grouped, own_codes[:, part], own_planes[:, part], 0, 2)
 
-        def x_quantise(g):
-            codes, planes, base = ((all_codes, all_planes, 0), (own_codes, own_planes, 0), (all_codes, all_planes, SLOTS))[g]
-            part = slice(base * P, (base + SLOTS) * P)
-            quantise(grouped_x[g], codes[:, part], planes[:, part], 0, 4)
-            quantise(grouped_x[g], codes[:, part], planes[:, part], 4, 2)
-
-        def x_group(g):
-            for first in range(0, SLOTS, 2):
-                x_pair(g, first, psum_acc, "acc", nc.vector.tensor_copy if first == 2 else nc.scalar.copy)
-            x_quantise(g)
+        def spread(h):
+            nodes_of_half = slice(h * SLOTS * P, (h + 1) * SLOTS * P)
+            for e in range(2):
+                for all_of, own, dtype in ((all_codes, own_codes, I32), (all_planes, own_planes, U8)):
+                    nc.vector.tensor_copy(
+                        out=all_of[:, nodes_of_half].bitcast(dtype).rearrange("q (n e) -> q n e", e=2)[:, :, e],
+                        in_=own[:].bitcast(dtype).rearrange("q (n h) -> q n h", h=2)[:, :, h],
+                    )
 
         message_source = keep.tile([P, NODES, C], F32)
         own_turned = keep.tile([P, SLOTS, CHUNKS, P], F32)
         sums = keep.tile([P, SLOTS - 1, 2, CHUNKS, P], F32)
 
-        def node_product(w, index, k):
-            if k == 2:
-                product = psum_sum.tile([P, C], F32, name="product%s%d" % (w, index), tag="turned%d" % (index % 2))
+        def message_product(j):
+            pool, tag = (psum_sum, "turned%d" % (j // 3 % 2)) if j % 3 == 2 else (psum_acc, "acc")
+            product = pool.tile([P, C], F32, name="message%d" % j, tag=tag)
+            multiply(product[:], all_codes, all_planes, j, "V", True, True)
+            if j % 2 == 0:
+                nc.scalar.mul(out=message_source[:, j, :], in_=product[:], mul=1.0 / NODES)
             else:
-                product = psum_acc.tile([P, C], F32, name="product%s%d" % (w, index), tag="acc")
-            if w == "V":
-                multiply(product[:], all_codes, all_planes, index, "V", True, True)
-                out, factor = message_source[:, index, :], 1.0 / NODES
-            else:
-                for q in range(CHUNKS):
-                    cols, rows = slice(q * P, (q + 1) * P), slice(index * P, (index + 1) * P)
-                    nc.tensor.matmul_mx(
-                        out=product[:, cols],
-                        lhsT=w_words[:, WEIGHT_NAMES.index("U"), cols].bitcast(FP8X4),
-                        lhsT_scale=w_planes[:, WEIGHT_NAMES.index("U"), cols],
-                        rhs=own_codes[:, rows].bitcast(FP8X4), rhs_scale=own_planes[:, rows], start=True, stop=True,
-                    )
-                out, factor = own_turned[:, index, :, :].rearrange("p q r -> p (q r)"), 1.0
-            if k != 1 and w == "V":
-                nc.scalar.mul(out=out, in_=product[:], mul=factor)
-            else:
-                nc.vector.tensor_scalar(out=out, in0=product[:], scalar1=factor, scalar2=None, op0=ALU.mult)
+                nc.vector.tensor_scalar(
+                    out=message_source[:, j, :], in0=product[:], scalar1=1.0 / NODES, scalar2=None, op0=ALU.mult
+                )
+
+        def own_product(s, pool=psum_misc, tag="misc"):
+            k, rows = WEIGHT_NAMES.index("U"), slice(s * P, (s + 1) * P)
+            product = pool.tile([P, CHUNKS, P], F32, name="own%d" % s, tag=tag)
+            for q in range(CHUNKS):
+                cols = slice(q * P, (q + 1) * P)
+                nc.tensor.matmul_mx(
+                    out=product[:, q, :], lhsT=w_words[:, k, cols].bitcast(FP8X4), lhsT_scale=w_planes[:, k, cols],
+                    rhs=own_codes[:, rows].bitcast(FP8X4), rhs_scale=own_planes[:, rows], start=True, stop=True,
+                )
+            own_of[s] = product
+
+        def own_fetch(s, engine_copy):
+            engine_copy(out=own_turned[:, s, :, :], in_=own_of[s][:])
+
+        own_of = {}
 
         def live(u):
             return 0 <= u < UNITS
@@ -341,7 +339,7 @@ def tile_graphmodel_pa_kernel(
             s, a = u // UNITS_PER_SLOT, u % UNITS_PER_SLOT
             if a == 0:
                 turned_of[(s, k)] = psum_sum.tile([P, CHUNKS, P], F32, name="turned%d_%d" % (s, k), tag="turned%d" % k)
-            turned, rows = turned_of[(s, k)], (gate_of[u], weighted_of[u])[k]
+            turned, rows = turned_of[(s, k)], (weighted_of if k else gate_of)[u]
             for i in range(UNIT):
                 for q in range(CHUNKS):
                     nc.tensor.matmul(
@@ -364,19 +362,6 @@ def tile_graphmodel_pa_kernel(
                 nc.scalar.activation(out=inverse[:], in_=turned_of[(s, 0)][:], func=ACT.Square)
                 nc.scalar.activation(out=inverse[:], in_=inverse[:], func=ACT.Abs_reciprocal_sqrt)
             share_of[s] = inverse
-
-        def node_own(s):
-            product = psum_misc.tile([P, CHUNKS, P], F32, name="own%d" % s, tag="misc")
-            rows = slice(s * P, (s + 1) * P)
-            for q in range(CHUNKS):
-                cols = slice(q * P, (q + 1) * P)
-                nc.tensor.matmul_mx(
-                    out=product[:, q, :],
-                    lhsT=w_words[:, WEIGHT_NAMES.index("U"), cols].bitcast(FP8X4),
-                    lhsT_scale=w_planes[:, WEIGHT_NAMES.index("U"), cols],
-                    rhs=own_codes[:, rows].bitcast(FP8X4), rhs_scale=own_planes[:, rows], start=True, stop=True,
-                )
-            nc.scalar.copy(out=own_turned[:, s, :, :], in_=product[:])
 
         def node_divide(s):
             message = sums[:, s, 1, :, :] if s < SLOTS - 1 else turned_of[(s, 1)][:]
@@ -431,7 +416,7 @@ def tile_graphmodel_pa_kernel(
             last[s] = xouts.tile([P, C], F32, name="x_out%d" % s, tag="x_out")
             nc.vector.scalar_tensor_tensor(
                 out=last[s][:], in0=x_new_of[s][:].rearrange("p q c -> p (q c)"), scalar=last["rstd"][:, s : s + 1],
-                in1=x_own[:, s, :], op0=ALU.mult, op1=ALU.add,
+                in1=x_own[s // 2][:, s % 2, :], op0=ALU.mult, op1=ALU.add,
             )
 
         def node_finish(s):
@@ -441,34 +426,37 @@ def tile_graphmodel_pa_kernel(
         def slot_ending(u):
             return u // UNITS_PER_SLOT if live(u) and u % UNITS_PER_SLOT == UNITS_PER_SLOT - 1 else None
 
-        x_group(0)
-        x_group(1)
+        for g in range(SLOTS // 2):
+            x_pair(g, nc.vector.tensor_copy if g == 1 else nc.scalar.copy)
         for u in range(BATCH):
             flip(u, psum_sum, "turned%d" % u)
             regroup(u)
+        spread(0)
         quantise_batch(0)
-        x_group(2)
+        spread(1)
         for j in range(NODES):
-            node_product("V", j, (0, 1, 2)[j % 3])
-        flip(2)
-        regroup(2)
+            message_product(j)
+        for i in range(UNIT):
+            aggregate(0, i)
+            statistics(0, i)
+        for u in range(BATCH, 2 * BATCH):
+            flip(u, psum_sum, "turned%d" % (u % 2))
+            regroup(u)
+        quantise_batch(1)
+        load_edges(LOADS_AHEAD)
 
-        def extra(n):
-            if UNITS < n < UNITS + 4:
-                node_product("U", n - UNITS - 1, 0)
-
-        for n in range(UNITS + 8):
+        for n in range(1, UNITS + 8):
             if n % BATCH == 0 and n // BATCH + LOADS_AHEAD < UNITS // BATCH:
                 load_edges(n // BATCH + LOADS_AHEAD)
             if live(n - 3):
                 factors_slope(n - 3)
             if live(n - 2):
                 factors_join(n - 2)
-            if live(n - 1):
+            if 1 < n and live(n - 1):
                 statistics(n - 1, 0)
             if live(n - 2):
                 normalise(n - 2, 0)
-            if live(n - 1):
+            if 1 < n and live(n - 1):
                 statistics(n - 1, 1)
             if live(n - 7):
                 weigh(n - 7)
@@ -486,7 +474,9 @@ def tile_graphmodel_pa_kernel(
                 factors_square(n - 1)
             if live(n):
                 aggregate(n, 0)
-            extra(n)
+            if UNITS < n < UNITS + 4:
+                own_product(n - UNITS - 1, psum_acc, "acc")
+                own_fetch(n - UNITS - 1, nc.vector.tensor_copy)
             if live(n - 1):
                 factors_mean(n - 1)
             if live(n - 4):
@@ -514,7 +504,8 @@ def tile_graphmodel_pa_kernel(
             node_invert(s)
             if s >= 1:
                 if s + 2 < SLOTS:
-                    node_own(s + 2)
+                    own_product(s + 2)
+                    own_fetch(s + 2, nc.scalar.copy)
             if s >= 1:
                 node_divide(s - 1)
                 node_sum(s - 1)

@@ -168,13 +168,14 @@ def tile_graphmodel_pa_kernel(
             part = slice(2 * g * P, (2 * g + 2) * P)
             quantise(grouped, own_codes[:, part], own_planes[:, part], 0, 2)
 
-        def spread(h):
-            nodes_of_half = slice(h * SLOTS * P, (h + 1) * SLOTS * P)
+        def spread(g, h):
+            slots = slice(2 * g * P, (2 * g + 2) * P)
+            sending = slice((h * SLOTS + 2 * g) * P, (h * SLOTS + 2 * g + 2) * P)
             for e in range(2):
                 for all_of, own, dtype in ((all_codes, own_codes, I32), (all_planes, own_planes, U8)):
                     nc.vector.tensor_copy(
-                        out=all_of[:, nodes_of_half].bitcast(dtype).rearrange("q (n e) -> q n e", e=2)[:, :, e],
-                        in_=own[:].bitcast(dtype).rearrange("q (n h) -> q n h", h=2)[:, :, h],
+                        out=all_of[:, sending].bitcast(dtype).rearrange("q (n e) -> q n e", e=2)[:, :, e],
+                        in_=own[:, slots].bitcast(dtype).rearrange("q (n h) -> q n h", h=2)[:, :, h],
                     )
 
         message_source = keep.tile([P, NODES, C], F32)
@@ -185,7 +186,7 @@ def tile_graphmodel_pa_kernel(
             pool, tag = (psum_sum, "turned%d" % (j // 3 % 2)) if j % 3 == 2 else (psum_acc, "acc")
             product = pool.tile([P, C], F32, name="message%d" % j, tag=tag)
             multiply(product[:], all_codes, all_planes, j, "V", True, True)
-            if j % 2 == 0:
+            if j < 9:
                 nc.scalar.mul(out=message_source[:, j, :], in_=product[:], mul=1.0 / NODES)
             else:
                 nc.vector.tensor_scalar(
@@ -428,13 +429,14 @@ def tile_graphmodel_pa_kernel(
 
         for g in range(SLOTS // 2):
             x_pair(g, nc.vector.tensor_copy if g == 1 else nc.scalar.copy)
+            spread(g, 0)
         for u in range(BATCH):
             flip(u, psum_sum, "turned%d" % u)
             regroup(u)
-        spread(0)
         quantise_batch(0)
-        spread(1)
         for j in range(NODES):
+            if j % 2 == 0 and j < SLOTS:
+                spread(j // 2, 1)
             message_product(j)
         for i in range(UNIT):
             aggregate(0, i)

from contextlib import ExitStack

import concourse.mybir as mybir
from concourse.masks import make_identity

F32 = mybir.dt.float32
BF16 = mybir.dt.bfloat16
U8 = mybir.dt.uint8
U32 = mybir.dt.uint32
I32 = mybir.dt.int32
FP8X4 = mybir.dt.float8_e4m3fn_x4
ALU = mybir.AluOpType
ACT = mybir.ActivationFunctionType
AXIS = mybir.AxisListType

GRAPHS, NODES, C = 64, 12, 512
P = 128
PACK = 4
SLOTS = NODES // 2
UNIT = 2
UNITS = SLOTS * NODES // UNIT
UNITS_PER_SLOT = NODES // UNIT
AHEAD = 2
CHUNKS = C // P
HALF_COUNT = C // 2
HALF_ROOT = 16.0
assert HALF_ROOT * HALF_ROOT == HALF_COUNT
BATCH = 2
BN_EPS = 1e-5
RV_MOD, RV_CNT, RV_FROM = 4, 0, 0
CHAIN = 2
LOADS_AHEAD = 5
WEIGHT_NAMES = ("A", "B", "E", "U", "V")

FLOPS = 2 * C * C * (GRAPHS * NODES * NODES + 4 * GRAPHS * NODES)


def tile_graphmodel_pa_kernel(
    tc, x, edge,
    WA_words, WA_scales, WB_words, WB_scales, WE_words, WE_scales, WU_words, WU_scales, WV_words, WV_scales,
    x_out, edge_out,
):
    nc = tc.nc
    given = {
        "A": (WA_words, WA_scales), "B": (WB_words, WB_scales), "E": (WE_words, WE_scales),
        "U": (WU_words, WU_scales), "V": (WV_words, WV_scales),
    }
    x_rows = x.rearrange("b (h s) c -> (b h) s c", h=2)
    x_out_rows = x_out.rearrange("b (h s) c -> (b h) s c", h=2)
    edge_rows = edge.rearrange("b (h r) c -> (b h) r c", h=2)
    edge_out_rows = edge_out.rearrange("b (h r) c -> (b h) r c", h=2)

    with ExitStack() as ctx:
        keep = ctx.enter_context(tc.tile_pool(name="keep", bufs=1))
        edges = ctx.enter_context(tc.tile_pool(name="edges", bufs=9))
        early = ctx.enter_context(tc.tile_pool(name="early", bufs=2))
        stage = ctx.enter_context(tc.tile_pool(name="stage", bufs=2))
        normed = ctx.enter_context(tc.tile_pool(name="normed", bufs=6))
        gates = ctx.enter_context(tc.tile_pool(name="gates", bufs=4))
        gated = ctx.enter_context(tc.tile_pool(name="gated", bufs=2))
        nodes = ctx.enter_context(tc.tile_pool(name="nodes", bufs=3))
        small = ctx.enter_context(tc.tile_pool(name="small", bufs=6))
        xouts = ctx.enter_context(tc.tile_pool(name="xouts", bufs=6))
        psum_flip = ctx.enter_context(tc.psum_pool(name="psum_flip", bufs=1))
        psum_acc = ctx.enter_context(tc.psum_pool(name="psum_acc", bufs=AHEAD * UNIT))
        psum_misc = ctx.enter_context(tc.psum_pool(name="psum_misc", bufs=1))
        psum_sum = ctx.enter_context(tc.psum_pool(name="psum_sum", bufs=1))
        ctx.enter_context(tc.manual_schedule())

        ident = keep.tile([P, P], F32)
        make_identity(nc, ident[:])

        x_own = [keep.tile([P, 2, C], BF16, name="x_own%d" % g) for g in range(SLOTS // 2)]

        def load_x(g, queue):
            queue.dma_start(out=x_own[g][:], in_=x_rows[:, 2 * g : 2 * g + 2, :])

        edge_in = {}
        WIDE = BATCH * UNIT

        def load_edges(b):
            edge_in[b] = edges.tile([P, WIDE, C], BF16, name="edge_in%d" % b, tag="edge_in")
            nc.sync.dma_start(out=edge_in[b][:], in_=edge_rows[:, b * WIDE : (b + 1) * WIDE, :])

        w_words = keep.tile([P, len(WEIGHT_NAMES), C], U32, align_bytes=64)
        w_planes = keep.tile([P, len(WEIGHT_NAMES), C], U8, align_bytes=64)
        nc.vector.memset(w_planes[:].bitcast(I32), 0)

        def load_weight(w):
            words, scales = given[w]
            k = WEIGHT_NAMES.index(w)
            for quadrant in range(4):
                plane_rows = w_planes[32 * quadrant : 32 * quadrant + 4, k, :]
                scale_rows = scales[0, 4 * quadrant : 4 * quadrant + 4, :]
                nc.sync.dma_start(out=plane_rows.bitcast(I32), in_=scale_rows.bitcast(I32))
            nc.sync.dma_start(
                out=w_words[:, k, :].bitcast(I32),
                in_=words[0].rearrange("p n t -> p (n t)").bitcast(I32),
            )

        load_x(0, nc.scalar)
        load_x(1, nc.sync)
        load_x(2, nc.scalar)
        load_edges(0)
        for w in ("V", "A", "B", "E"):
            load_weight(w)
        for b in range(1, LOADS_AHEAD):
            load_edges(b)
        load_weight("U")

        own_parity = keep.tile([P, 2], F32)
        nc.vector.tensor_reduce(
            out=own_parity[:], in_=ident[:].rearrange("p (a t) -> p t a", t=2), axis=AXIS.X, op=ALU.add
        )
        neg_parity = keep.tile([P, P // 2, 2], F32)
        nc.vector.tensor_scalar(
            out=neg_parity[:], in0=own_parity[:].unsqueeze(1).to_broadcast([P, P // 2, 2]),
            scalar1=-1.0 / (P * HALF_COUNT), scalar2=None, op0=ALU.mult,
        )
        minus_half = keep.tile([P, CHAIN * UNIT], F32)
        nc.vector.memset(minus_half[:], -0.5)
        warm = keep.tile([P, 1], F32)
        nc.vector.memset(warm[:], 0.0)
        nc.scalar.activation(out=warm[:], in_=warm[:], func=ACT.Tanh)

        def transpose_pair(rows, first, pool=psum_flip, tag="flipped"):
            flipped = pool.tile([P, 2, 2, P], F32, tag=tag)
            for i in range(2):
                words = rows[:, first + i, :].bitcast(F32)
                for u in range(2):
                    nc.tensor.transpose(flipped[:, i, u, :], words[:, u : C // 2 : 2], ident[:])
            return flipped

        def regroup_pair(flipped, grouped, first, engine_copy=nc.scalar.copy):
            engine_copy(
                out=grouped[:, first : first + 2, :, :].bitcast(F32),
                in_=flipped[:].rearrange("q i u r -> q i r u"),
            )

        def quantise(grouped, codes, planes, first, count):
            cols = slice(first * P, (first + count) * P)
            nc.vector.quantize_mx(
                out=codes[:, cols].bitcast(FP8X4), scales=planes[:, cols],
                in_=grouped[:, first : first + count, :, :].rearrange("q i r t -> q (i r t)"),
            )

        def multiply(out, codes, planes, index, w, start, stop, cols=slice(0, C)):
            k = WEIGHT_NAMES.index(w)
            nc.tensor.matmul_mx(
                out=out,
                lhsT=codes[:, index * P : (index + 1) * P].bitcast(FP8X4),
                lhsT_scale=planes[:, index * P : (index + 1) * P],
                rhs=w_words[:, k, cols].bitcast(FP8X4),
                rhs_scale=w_planes[:, k, cols],
                start=start,
                stop=stop,
            )

        own_codes = keep.tile([P, SLOTS * P], U32, align_bytes=64)
        own_planes = keep.tile([P, SLOTS * P], U8, align_bytes=64)
        all_codes = keep.tile([P, NODES * P], U32, align_bytes=64)
        all_planes = keep.tile([P, NODES * P], U8, align_bytes=64)

        def x_pair(g, engine_copy):
            grouped = early.tile([P, 2, P, PACK], BF16, align_bytes=64, name="grouped_x%d" % g, tag="grouped_x")
            flipped = transpose_pair(x_own[g], 0, pool=psum_acc, tag="acc")
            regroup_pair(flipped, grouped, 0, engine_copy=engine_copy)
            part = slice(2 * g * P, (2 * g + 2) * P)
            quantise(grouped, own_codes[:, part], own_planes[:, part], 0, 2)

        def spread(g, h):
            slots = slice(2 * g * P, (2 * g + 2) * P)
            sending = slice((h * SLOTS + 2 * g) * P, (h * SLOTS + 2 * g + 2) * P)
            for e in range(2):
                for all_of, own, dtype in ((all_codes, own_codes, I32), (all_planes, own_planes, U8)):
                    nc.vector.tensor_copy(
                        out=all_of[:, sending].bitcast(dtype).rearrange("q (n e) -> q n e", e=2)[:, :, e],
                        in_=own[:, slots].bitcast(dtype).rearrange("q (n h) -> q n h", h=2)[:, :, h],
                    )

        message_source = keep.tile([P, NODES, C], F32)
        own_turned = keep.tile([P, SLOTS, CHUNKS, P], F32)
        sums = keep.tile([P, SLOTS - 1, 2, CHUNKS, P], F32)

        def message_product(j):
            pool, tag = (psum_sum, "turned%d" % (j // 3 % 2)) if j % 3 == 2 else (psum_acc, "acc")
            product = pool.tile([P, C], F32, name="message%d" % j, tag=tag)
            multiply(product[:], all_codes, all_planes, j, "V", True, True)
            if j < 9:
                nc.scalar.mul(out=message_source[:, j, :], in_=product[:], mul=1.0 / NODES)
            else:
                nc.vector.tensor_scalar(
                    out=message_source[:, j, :], in0=product[:], scalar1=1.0 / NODES, scalar2=None, op0=ALU.mult
                )

        def own_product(s, pool=psum_misc, tag="misc"):
            k, rows = WEIGHT_NAMES.index("U"), slice(s * P, (s + 1) * P)
            product = pool.tile([P, CHUNKS, P], F32, name="own%d" % s, tag=tag)
            for q in range(CHUNKS):
                cols = slice(q * P, (q + 1) * P)
                nc.tensor.matmul_mx(
                    out=product[:, q, :], lhsT=w_words[:, k, cols].bitcast(FP8X4), lhsT_scale=w_planes[:, k, cols],
                    rhs=own_codes[:, rows].bitcast(FP8X4), rhs_scale=own_planes[:, rows], start=True, stop=True,
                )
            own_of[s] = product

        def own_fetch(s, engine_copy):
            engine_copy(out=own_turned[:, s, :, :], in_=own_of[s][:])

        own_of = {}

        def live(u):
            return 0 <= u < UNITS

        grouped_of, codes_of, planes_of, flipped_of = {}, {}, {}, {}
        acc_of, stats_of, factors_of, result_of, gate_of, weighted_of = {}, {}, {}, {}, {}, {}
        turned_of, x_new_of = {}, {}

        def regroup_on_vector(u):
            return u % RV_MOD < RV_CNT and u >= RV_FROM

        def flip(u, pool=psum_flip, tag="flipped"):
            flipped_of[u] = transpose_pair(edge_in[u // BATCH], UNIT * (u % BATCH), pool=pool, tag=tag)

        def regroup(u):
            b, k = u // BATCH, u % BATCH
            if k == 0:
                grouped_of[b] = stage.tile(
                    [P, BATCH * UNIT, P, PACK], BF16, align_bytes=64, name="grouped%d" % b, tag="grouped"
                )
            regroup_pair(flipped_of[u], grouped_of[b], UNIT * k, engine_copy=nc.vector.tensor_copy if regroup_on_vector(u) else nc.scalar.copy)

        def quantise_batch(b):
            codes_of[b] = stage.tile([P, BATCH * UNIT * P], U32, align_bytes=64, name="codes%d" % b, tag="codes")
            planes_of[b] = stage.tile([P, BATCH * UNIT * P], U8, align_bytes=64, name="planes%d" % b, tag="planes")
            quantise(grouped_of[b], codes_of[b], planes_of[b], 0, BATCH * UNIT)

        def stats_tile(m):
            if m not in stats_of:
                stats_of[m] = small.tile([P, UNIT + 1, 2, 3], F32, name="stats%d" % m, tag="stats")
            return stats_of[m]

        def aggregate(u, i):
            s, a = u // UNITS_PER_SLOT, u % UNITS_PER_SLOT
            if u < UNITS_PER_SLOT and u % 3 == 2:
                agg = psum_sum.tile([P, C], F32, name="agg%d_%d" % (u, i), tag="turned%d" % i)
            else:
                agg = psum_acc.tile([P, C], F32, name="agg%d_%d" % (u, i), tag="acc")
            multiply(agg[:], own_codes, own_planes, s, "A", True, False)
            multiply(agg[:], all_codes, all_planes, UNIT * a + i, "B", False, False)
            multiply(agg[:], codes_of[u // BATCH], planes_of[u // BATCH], UNIT * (u % BATCH) + i, "E", False, True)
            acc_of[(u, i)] = agg

        def statistics(u, i):
            nc.vector.bn_stats(out=stats_tile(u)[:, i, :, :].rearrange("p h k -> p (h k)"), in_=acc_of[(u, i)][:])

        joined_of, slope_of = {}, {}

        def has_chain(m):
            return live(m)

        def factors_square(m):
            nc.scalar.activation(
                out=stats_of[m][:, 0:UNIT, :, 0], in_=stats_of[m][:, 0:UNIT, :, 1], func=ACT.Square, scale=HALF_ROOT
            )

        def factors_mean(m):
            means = psum_misc.tile([P, UNIT, 2, 3], F32, tag="misc")
            nc.tensor.matmul(
                out=means[:].rearrange("p c h k -> p (c h k)"), lhsT=neg_parity[:].rearrange("p a t -> p (a t)"),
                rhs=stats_of[m][:, 0:UNIT, :, :].rearrange("p c h k -> p (c h k)"), start=True, stop=True,
            )
            factors_of[m] = {"means": means}

        def factors_join(m):
            g, k = m // CHAIN, m % CHAIN
            if k == 0:
                joined_of[g] = small.tile([P, CHAIN * UNIT, 3], F32, name="joined%d" % g, tag="joined")
            nc.vector.tensor_reduce(
                out=joined_of[g][:, k * UNIT : (k + 1) * UNIT, :], in_=factors_of[m]["means"][:].rearrange("p c h k -> p c k h"),
                axis=AXIS.X, op=ALU.add,
            )

        parts_of = {}

        def factors_parts(m):
            if m % CHAIN != CHAIN - 1:
                return
            joined = joined_of[m // CHAIN]
            parts = small.tile([P, 3, CHAIN * UNIT], F32, name="parts%d" % m, tag="parts")
            parts_of[m // CHAIN] = parts
            nc.vector.tensor_tensor(out=parts[:, 0, :], in0=joined[:, :, 1], in1=joined[:, :, 1], op=ALU.mult)
            nc.vector.scalar_tensor_tensor(
                out=parts[:, 1, :], in0=joined[:, :, 0], scalar=-BN_EPS, in1=joined[:, :, 2], op0=ALU.add, op1=ALU.add
            )

        def factors_slope(m):
            if m % CHAIN != CHAIN - 1:
                return
            g, n2 = m // CHAIN, float(HALF_COUNT * HALF_COUNT)
            parts = parts_of[g]
            nc.vector.scalar_tensor_tensor(
                out=parts[:, 2, :], in0=parts[:, 1, :], scalar=-1.0 / n2, in1=parts[:, 0, :], op0=ALU.mult, op1=ALU.subtract
            )
            slope_of[g] = small.tile([P, CHAIN * UNIT], F32, name="slope%d" % g, tag="slope")
            nc.gpsimd.tensor_tensor(out=slope_of[g][:], in0=parts[:, 2, :], in1=minus_half[:], op=ALU.pow)

        def normalise(u, i):
            if i == 0:
                result_of[u] = normed.tile([P, UNIT, C], F32, name="result%d" % u, tag="result")
            nc.scalar.activation(
                out=result_of[u][:, i, :], in_=acc_of[(u, i)][:], func=ACT.Relu,
                bias=joined_of[u // CHAIN][:, (u % CHAIN) * UNIT + i, 1:2], scale=1.0 / HALF_COUNT,
            )

        def residual(u, i):
            column = (u % CHAIN) * UNIT + i
            nc.vector.scalar_tensor_tensor(
                out=result_of[u][:, i, :], in0=result_of[u][:, i, :], scalar=slope_of[u // CHAIN][:, column : column + 1],
                in1=edge_in[u // BATCH][:, UNIT * (u % BATCH) + i, :], op0=ALU.mult, op1=ALU.add,
            )
            if i == UNIT - 1:
                nc.sync.dma_start(out=edge_out_rows[:, UNIT * u : UNIT * (u + 1), :], in_=result_of[u][:])

        def squash(u):
            gate_of[u] = gates.tile([P, UNIT, C], F32, name="gate%d" % u, tag="gate")
            nc.scalar.activation(out=gate_of[u][:], in_=result_of[u][:], func=ACT.Tanh, scale=0.5)

        def exponent(u):
            nc.scalar.activation(out=gate_of[u][:], in_=gate_of[u][:], func=ACT.Exp, scale=0.5)

        def weigh(u):
            a = u % UNITS_PER_SLOT
            weighted_of[u] = gated.tile([P, UNIT, C], F32, name="weighted%d" % u, tag="weighted")
            nc.vector.tensor_tensor(
                out=weighted_of[u][:], in0=gate_of[u][:], in1=message_source[:, UNIT * a : UNIT * (a + 1), :], op=ALU.mult
            )

        def add_up(u, k):
            s, a = u // UNITS_PER_SLOT, u % UNITS_PER_SLOT
            if a == 0:
                turned_of[(s, k)] = psum_sum.tile([P, CHUNKS, P], F32, name="turned%d_%d" % (s, k), tag="turned%d" % k)
            turned, rows = turned_of[(s, k)], (weighted_of if k else gate_of)[u]
            for i in range(UNIT):
                for q in range(CHUNKS):
                    nc.tensor.matmul(
                        out=turned[:, q, :], lhsT=rows[:, i, q * P : (q + 1) * P], rhs=ident[:], is_transpose=True,
                        start=(a == 0 and i == 0 and q == 0),
                        stop=(a == UNITS_PER_SLOT - 1 and i == UNIT - 1 and q == CHUNKS - 1),
                    )

        def node_fetch(s):
            nc.scalar.activation(out=sums[:, s, 0, :, :], in_=turned_of[(s, 0)][:], func=ACT.Square)
            nc.vector.tensor_copy(out=sums[:, s, 1, :, :], in_=turned_of[(s, 1)][:])

        share_of, last = {}, {}

        def node_invert(s):
            inverse = nodes.tile([P, CHUNKS, P], F32, name="inverse%d" % s, tag="inverse")
            if s < SLOTS - 1:
                nc.scalar.activation(out=inverse[:], in_=sums[:, s, 0, :, :], func=ACT.Abs_reciprocal_sqrt)
            else:
                nc.scalar.activation(out=inverse[:], in_=turned_of[(s, 0)][:], func=ACT.Square)
                nc.scalar.activation(out=inverse[:], in_=inverse[:], func=ACT.Abs_reciprocal_sqrt)
            share_of[s] = inverse

        def node_divide(s):
            message = sums[:, s, 1, :, :] if s < SLOTS - 1 else turned_of[(s, 1)][:]
            nc.vector.tensor_tensor(out=share_of[s][:], in0=message, in1=share_of[s][:], op=ALU.mult)

        def node_sum(s):
            pool, tag = (((psum_acc, "acc"),) * 4 + ((psum_flip, "flipped"), (psum_sum, "turned0")))[s]
            x_new_of[s] = pool.tile([P, CHUNKS, P], F32, name="x_new%d" % s, tag=tag)
            for k, rows in enumerate((share_of[s], own_turned[:, s, :, :])):
                for q in range(CHUNKS):
                    nc.tensor.matmul(
                        out=x_new_of[s][:, q, :], lhsT=rows[:, q, :], rhs=ident[:], is_transpose=True,
                        start=(k == 0 and q == 0), stop=(k == 1 and q == CHUNKS - 1),
                    )

        def node_statistics(s):
            nc.vector.bn_stats(
                out=last["stats"][:, s, :, :].rearrange("p h k -> p (h k)"), in_=x_new_of[s][:].rearrange("p q c -> p (q c)")
            )

        def node_means(lo, hi):
            stats = last["stats"]
            nc.scalar.activation(out=stats[:, lo:hi, :, 0], in_=stats[:, lo:hi, :, 1], func=ACT.Square, scale=HALF_ROOT)
            last["means"] = psum_misc.tile([P, hi - lo, 2, 3], F32, name="last_means%d" % lo, tag="misc")
            nc.tensor.matmul(
                out=last["means"][:].rearrange("p c h k -> p (c h k)"), lhsT=neg_parity[:].rearrange("p a t -> p (a t)"),
                rhs=stats[:, lo:hi, :, :].rearrange("p c h k -> p (c h k)"), start=True, stop=True,
            )

        def node_rstd(lo, hi):
            joined, work, n2 = last["joined"], last["work"], float(HALF_COUNT * HALF_COUNT)
            nc.vector.tensor_reduce(
                out=joined[:, lo:hi, :], in_=last["means"][:].rearrange("p c h k -> p c k h"), axis=AXIS.X, op=ALU.add
            )
            nc.vector.tensor_tensor(out=work[:, 0, lo:hi], in0=joined[:, lo:hi, 0], in1=joined[:, lo:hi, 2], op=ALU.add)
            nc.vector.tensor_tensor(out=work[:, 1, lo:hi], in0=joined[:, lo:hi, 1], in1=joined[:, lo:hi, 1], op=ALU.mult)
            nc.vector.tensor_scalar(
                out=work[:, 0, lo:hi], in0=work[:, 0, lo:hi], scalar1=-1.0 / n2, scalar2=BN_EPS / n2, op0=ALU.mult, op1=ALU.add
            )
            nc.vector.tensor_tensor(out=work[:, 0, lo:hi], in0=work[:, 0, lo:hi], in1=work[:, 1, lo:hi], op=ALU.subtract)
            nc.scalar.activation(out=work[:, 2, lo:hi], in_=work[:, 0, lo:hi], func=ACT.Abs_reciprocal_sqrt, scale=n2)

        def node_shift(lo, hi):
            joined, work = last["joined"], last["work"]
            nc.vector.scalar_tensor_tensor(
                out=work[:, 3, lo:hi], in0=joined[:, lo:hi, 1], scalar=float(HALF_COUNT), in1=work[:, 2, lo:hi],
                op0=ALU.mult, op1=ALU.mult,
            )
            last["rstd"], last["shift"] = work[:, 2, :], work[:, 3, :]

        def node_scale(s):
            last[s] = xouts.tile([P, C], F32, name="x_out%d" % s, tag="x_out")
            nc.vector.scalar_tensor_tensor(
                out=last[s][:], in0=x_new_of[s][:].rearrange("p q c -> p (q c)"), scalar=last["rstd"][:, s : s + 1],
                in1=x_own[s // 2][:, s % 2, :], op0=ALU.mult, op1=ALU.add,
            )

        def node_finish(s):
            nc.scalar.activation(out=last[s][:], in_=last[s][:], func=ACT.Relu, bias=last["shift"][:, s : s + 1], scale=1.0)
            nc.sync.dma_start(out=x_out_rows[:, s, :], in_=last[s][:])

        def slot_ending(u):
            return u // UNITS_PER_SLOT if live(u) and u % UNITS_PER_SLOT == UNITS_PER_SLOT - 1 else None

        for g in range(SLOTS // 2):
            x_pair(g, nc.vector.tensor_copy if g == 1 else nc.scalar.copy)
            spread(g, 0)
        for u in range(BATCH):
            flip(u, psum_sum, "turned%d" % u)
            regroup(u)
        quantise_batch(0)
        for j in range(NODES):
            if j % 2 == 0 and j < SLOTS:
                spread(j // 2, 1)
            message_product(j)
        for i in range(UNIT):
            aggregate(0, i)
            statistics(0, i)
        for u in range(BATCH, 2 * BATCH):
            flip(u, psum_sum, "turned%d" % (u % 2))
            regroup(u)
        quantise_batch(1)
        load_edges(LOADS_AHEAD)

        for n in range(1, UNITS + 8):
            if n % BATCH == 0 and n // BATCH + LOADS_AHEAD < UNITS // BATCH:
                load_edges(n // BATCH + LOADS_AHEAD)
            if live(n - 3):
                factors_slope(n - 3)
            if live(n - 2):
                factors_join(n - 2)
            if 1 < n and live(n - 1):
                statistics(n - 1, 0)
            if live(n - 2):
                normalise(n - 2, 0)
            if 1 < n and live(n - 1):
                statistics(n - 1, 1)
            if live(n - 7):
                weigh(n - 7)
            if live(n - 2):
                factors_parts(n - 2)
            if slot_ending(n - 8) is not None and slot_ending(n - 8) < SLOTS - 1:
                node_fetch(slot_ending(n - 8))
            if live(n + 3):
                flip(n + 3)
            if live(n - 4):
                residual(n - 4, 0)
            if live(n - 2):
                normalise(n - 2, 1)
            if live(n - 1):
                factors_square(n - 1)
            if live(n):
                aggregate(n, 0)
            if UNITS < n < UNITS + 4:
                own_product(n - UNITS - 1, psum_acc, "acc")
                own_fetch(n - UNITS - 1, nc.vector.tensor_copy)
            if live(n - 1):
                factors_mean(n - 1)
            if live(n - 4):
                residual(n - 4, 1)
            if live(n + 3):
                regroup(n + 3)
            if live(n):
                aggregate(n, 1)
            if live(n - 7):
                add_up(n - 7, 0)
            if live(n - 5):
                exponent(n - 5)
            if live(n - 4):
                squash(n - 4)
            if live(n + 3) and (n + 3) % BATCH == BATCH - 1:
                quantise_batch((n + 3) // BATCH)
            if live(n - 7):
                add_up(n - 7, 1)

        last["stats"] = keep.tile([P, SLOTS, 2, 3], F32, name="last_stats")
        last["joined"] = keep.tile([P, SLOTS, 3], F32, name="last_joined")
        last["work"] = keep.tile([P, 4, SLOTS], F32, name="last_work")
        FIRST = SLOTS // 2
        for s in range(FIRST + 2):
            node_invert(s)
            if s >= 1:
                if s + 2 < SLOTS:
                    own_product(s + 2)
                    own_fetch(s + 2, nc.scalar.copy)
            if s >= 1:
                node_divide(s - 1)
                node_sum(s - 1)
            if s >= 2:
                node_statistics(s - 2)
        node_means(0, FIRST)
        node_invert(5)
        node_divide(4)
        node_sum(4)
        node_statistics(3)
        node_rstd(0, FIRST)
        node_divide(5)
        node_sum(5)
        node_statistics(4)
        node_shift(0, FIRST)
        node_scale(0)
        node_statistics(5)
        node_means(FIRST, SLOTS)
        node_finish(0)
        node_scale(1)
        node_rstd(FIRST, SLOTS)
        node_finish(1)
        node_scale(2)
        node_shift(FIRST, SLOTS)
        node_finish(2)
        for s in range(FIRST, SLOTS + 1):
            if s < SLOTS:
                node_scale(s)
            if s > FIRST:
                node_finish(s - 1)
